import numpy as np
import ml_dtypes


def mxq(x, axis, fmt="e4m3"):
    dtype, down = {"e4m3": (ml_dtypes.float8_e4m3fn, 7), "e5m2": (ml_dtypes.float8_e5m2, 14)}[fmt]
    v = np.moveaxis(np.asarray(x, np.float32).astype(ml_dtypes.bfloat16).astype(np.float64), axis, -1)
    blocks = v.reshape(v.shape[:-1] + (-1, 32))
    amax = np.abs(blocks).max(-1, keepdims=True)
    byte = np.maximum(np.where(amax > 0, np.frexp(amax)[1] - 1 + 127, 0) - down, 1)
    scale = np.exp2(byte - 127.0)
    codes = (blocks / scale).astype(np.float32).astype(dtype).astype(np.float64)
    return np.moveaxis((codes * scale).reshape(v.shape), -1, axis)


WIDE = False


def mx_kscale(k):
    if not WIDE:
        return np.ones(k)
    levels = np.array([10, -10, 5, -5, 0])
    a = np.random.permutation(np.resize(levels, k // 512 * 4)).reshape(k // 512, 4)
    idx = np.arange(k)
    return np.exp2(a[idx // 512, idx % 128 // 32])


BF16 = ml_dtypes.bfloat16


def bf(x):
    return np.asarray(x, np.float32).astype(BF16)


def f64(x):
    return np.asarray(x).astype(np.float64)


B, C, H, W, KS, NCAPS, CCH = 1, 512, 32, 32, 3, 32, 16
STRIDE = 1
PAD = KS // 2
NIT = 3
NC = NCAPS * CCH


def gather_positions(y, k, stride, pad):
    yp = np.pad(y, ((0, 0), (0, 0), (0, 0), (pad, pad), (pad, pad), (0, 0)))
    hh, ww = yp.shape[3], yp.shape[4]
    oh = (hh - k) // stride + 1
    ow = (ww - k) // stride + 1
    tiles = [yp[i, j, :, i:i + stride * (oh - 1) + 1:stride, j:j + stride * (ow - 1) + 1:stride, :]
             for i in range(k) for j in range(k)]
    return np.stack(tiles, 3)


def setup_inputs():
    s = mx_kscale(C)
    g = np.exp2(np.linspace(-1.5, 1.5, KS * KS)).reshape(KS, KS, 1, 1)
    return {"input": bf(np.random.standard_normal((B, C, H, W)) * s[None, :, None, None]),
            "weight": bf(np.random.standard_normal((1, 1, 1, KS, KS, C, NC)) * g / np.sqrt(C) / s[:, None]),
            "bias": bf(np.random.standard_normal((1, 1, 1, KS, KS, 1, NC)) * 0.2)}


def reference(input, weight, bias):
    x = f64(input)
    nb, c, h, wd = x.shape
    n = weight.shape[-1]
    xq = mxq(x.transpose(0, 2, 3, 1).reshape(nb * h * wd, c), 1, "e4m3")
    wq = mxq(f64(weight).reshape(KS * KS, c, n), 1, "e4m3")
    b = f64(bias).reshape(KS * KS, n)
    prod = xq @ wq
    priors = gather_positions(prod.reshape(KS, KS, nb, h, wd, n), KS, STRIDE, PAD) + b
    oh, ow = priors.shape[1], priors.shape[2]
    priors = priors.reshape(nb, oh, ow, KS * KS, NCAPS, CCH)
    outputs = priors.mean(3, keepdims=True)
    for _ in range(NIT):
        d = outputs - priors
        cw = 1.0 / np.sqrt(np.sum(d * d, axis=-1, keepdims=True) + 1e-4)
        cw = cw / np.sum(cw, axis=3, keepdims=True)
        outputs = np.sum(priors * cw, axis=3, keepdims=True)
    out = outputs.reshape(nb, oh, ow, NCAPS * CCH)
    return np.transpose(out, (0, 3, 1, 2))

@@ -1,0 +1,312 @@
+from contextlib import ExitStack
+
+import concourse.mybir as mybir
+from concourse.masks import make_identity
+
+F32 = mybir.dt.float32
+BF16 = mybir.dt.bfloat16
+U32 = mybir.dt.uint32
+U8 = mybir.dt.uint8
+FP8X4 = mybir.dt.float8_e4m3fn_x4
+ALU = mybir.AluOpType
+ACT = mybir.ActivationFunctionType
+X_AXIS = mybir.AxisListType.X
+
+P = 128
+PACK = 4
+SIDE = 32
+PADDED_ROWS = SIDE + 2
+KERNEL = 3
+POSITIONS = KERNEL * KERNEL
+FEATURES = 512
+CAPSULE = 16
+ROUTING_STEPS = 3
+EPS = 1e-4
+
+PIXEL_TILES = SIDE * SIDE // P
+UNIT = 256
+UNIT_CAPSULES = UNIT // CAPSULE
+UNITS_PER_TILE = FEATURES // UNIT
+UNIT_BLOCKS = UNIT // P
+
+LANES = 4
+TILES_PER_GROUP = LANES // UNITS_PER_TILE
+JOBS_PER_GROUP = LANES * ROUTING_STEPS
+JOBS = PIXEL_TILES * UNITS_PER_TILE * ROUTING_STEPS
+PIECES_PER_TURN = 2
+
+FLOPS = 2 * POSITIONS * SIDE * SIDE * (P * PACK) * FEATURES
+
+
+def quantise_image(nc, stage, image, even_codes, even_scales, odd_codes, odd_scales):
+    raw_image = stage.tile([P, PACK, SIDE, SIDE], BF16)
+    nc.sync.dma_start(out=raw_image[:], in_=image[0].rearrange("(p j) h w -> p j h w", j=PACK))
+    row = SIDE * PACK
+    whole = SIDE * SIDE
+    rest = (PADDED_ROWS - SIDE) * SIDE
+    for kj in range(KERNEL):
+        shifted = stage.tile([P, PADDED_ROWS, SIDE, PACK], BF16, align_bytes=64)
+        nc.vector.memset(shifted[:, 0, :, :], 0.0)
+        nc.vector.memset(shifted[:, PADDED_ROWS - 1, :, :], 0.0)
+        first = max(0, 1 - kj)
+        last = min(SIDE, SIDE + 1 - kj)
+        if first > 0:
+            nc.vector.memset(shifted[:, 1 : SIDE + 1, 0, :], 0.0)
+        if last < SIDE:
+            nc.vector.memset(shifted[:, 1 : SIDE + 1, SIDE - 1, :], 0.0)
+        nc.vector.tensor_copy(
+            out=shifted[:, 1 : SIDE + 1, first:last, :],
+            in_=raw_image[:, :, :, first + kj - 1 : last + kj - 1].rearrange("p j h w -> p h w j"),
+        )
+        flat = shifted[:].rearrange("p r w j -> p (r w j)")
+        nc.vector.quantize_mx(
+            out=even_codes[:, kj, 0:whole].bitcast(FP8X4),
+            scales=even_scales[:, kj, 0:whole],
+            in_=flat[:, 0 : whole * PACK],
+        )
+        nc.vector.quantize_mx(
+            out=even_codes[:, kj, whole : whole + rest].bitcast(FP8X4),
+            scales=even_scales[:, kj, whole : whole + rest],
+            in_=flat[:, whole * PACK : (whole + rest) * PACK],
+        )
+        nc.vector.quantize_mx(
+            out=odd_codes[:, kj, :].bitcast(FP8X4),
+            scales=odd_scales[:, kj, :],
+            in_=flat[:, row : row + whole * PACK],
+        )
+
+
+def quantise_weight(nc, stage, weight, t, weight_codes, weight_scales):
+    raw_weight = stage.tile([P, PACK, FEATURES], BF16, bufs=3)
+    nc.sync.dma_start(
+        out=raw_weight[:],
+        in_=weight[0, 0, 0, t // KERNEL, t % KERNEL].rearrange("(p j) n -> p j n", j=PACK),
+    )
+    grouped = stage.tile([P, FEATURES, PACK], BF16, align_bytes=64)
+    nc.scalar.copy(out=grouped[:], in_=raw_weight[:].rearrange("p j n -> p n j"))
+    nc.vector.quantize_mx(
+        out=weight_codes[:, t, :].bitcast(FP8X4),
+        scales=weight_scales[:, t, :],
+        in_=grouped[:].rearrange("p n j -> p (n j)"),
+    )
+
+
+def job_parts(j):
+    group, rest = divmod(j, JOBS_PER_GROUP)
+    step, lane = divmod(rest, LANES)
+    return TILES_PER_GROUP * group + lane // UNITS_PER_TILE, lane % UNITS_PER_TILE, step
+
+
+def tile_capsulelayer_kernel(tc, image, weight, bias, out):
+    nc = tc.nc
+    out_rows = out[0].rearrange("f h w -> f (h w)")
+
+    with ExitStack() as stack:
+        stack.enter_context(tc.manual_schedule())
+        keep = stack.enter_context(tc.tile_pool(name="keep", bufs=1))
+        image_stage = stack.enter_context(tc.tile_pool(name="image_stage", bufs=1))
+        weight_stage = stack.enter_context(tc.tile_pool(name="weight_stage", bufs=2))
+        prior_pool = stack.enter_context(tc.tile_pool(name="prior_pool", bufs=2 * TILES_PER_GROUP))
+        work_pool = stack.enter_context(tc.tile_pool(name="work_pool", bufs=LANES))
+        small = stack.enter_context(tc.tile_pool(name="small", bufs=LANES))
+        product_banks = stack.enter_context(tc.psum_pool(name="product_banks", bufs=2))
+        total_banks = stack.enter_context(tc.psum_pool(name="total_banks", bufs=TILES_PER_GROUP))
+        flip_banks = stack.enter_context(tc.psum_pool(name="flip_banks", bufs=2))
+
+        weight_codes = keep.tile([P, POSITIONS, FEATURES], U32, align_bytes=64)
+        weight_scales = keep.tile([P, POSITIONS, FEATURES], U8, align_bytes=64)
+        even_codes = keep.tile([P, KERNEL, PADDED_ROWS * SIDE], U32, align_bytes=64)
+        even_scales = keep.tile([P, KERNEL, PADDED_ROWS * SIDE], U8, align_bytes=64)
+        odd_codes = keep.tile([P, KERNEL, SIDE * SIDE], U32, align_bytes=64)
+        odd_scales = keep.tile([P, KERNEL, SIDE * SIDE], U8, align_bytes=64)
+        bias_rows = keep.tile([P, POSITIONS, FEATURES], BF16)
+        bias_mean = keep.tile([P, FEATURES], F32)
+        identity = keep.tile([P, P], F32)
+        eps = keep.tile([P, 1], F32)
+
+        products, totals, priors_of, mean_of = {}, {}, {}, {}
+        work_of, pull_of, coupling_of, flipped_sum_of, upright_of = {}, {}, {}, {}, {}
+
+        def multiply(m, t):
+            ki, kj = divmod(t, KERNEL)
+            if ki == 1:
+                pixels = slice(P * m, P * m + P)
+                codes, scales = odd_codes[:, kj, pixels], odd_scales[:, kj, pixels]
+            else:
+                pixels = slice(P * m + SIDE * ki, P * m + SIDE * ki + P)
+                codes, scales = even_codes[:, kj, pixels], even_scales[:, kj, pixels]
+            product = product_banks.tile([P, FEATURES], F32)
+            products[(m, t)] = product
+            if t == 0:
+                total = total_banks.tile([P, FEATURES], F32)
+                totals[m] = total
+            nc.tensor.matmul_mx(
+                out=product[:],
+                lhsT=codes.bitcast(FP8X4),
+                lhsT_scale=scales,
+                rhs=weight_codes[:, t, :].bitcast(FP8X4),
+                rhs_scale=weight_scales[:, t, :],
+                start=True,
+                stop=True,
+            )
+            nc.tensor.matmul_mx(
+                out=totals[m][:],
+                lhsT=codes.bitcast(FP8X4),
+                lhsT_scale=scales,
+                rhs=weight_codes[:, t, :].bitcast(FP8X4),
+                rhs_scale=weight_scales[:, t, :],
+                start=(t == 0),
+                stop=(t == POSITIONS - 1),
+            )
+
+        def add_bias(m, t):
+            if t == 0:
+                priors = prior_pool.tile([P, POSITIONS, FEATURES], F32)
+                priors_of[m] = priors
+            nc.vector.tensor_tensor(
+                out=priors_of[m][:, t, :], in0=products[(m, t)][:], in1=bias_rows[:, t, :], op=ALU.add
+            )
+            if t == POSITIONS - 1:
+                mean = small.tile([P, FEATURES], F32)
+                mean_of[m] = mean
+                nc.vector.scalar_tensor_tensor(
+                    out=mean[:],
+                    in0=totals[m][:],
+                    scalar=1.0 / POSITIONS,
+                    in1=bias_mean[:],
+                    op0=ALU.mult,
+                    op1=ALU.add,
+                )
+
+        def unit_priors(j):
+            m, u, step = job_parts(j)
+            return priors_of[m][:, :, UNIT * u : UNIT * u + UNIT]
+
+        def subtract_and_square(j):
+            m, u, step = job_parts(j)
+            if step == 0:
+                centre = mean_of[m][:, UNIT * u : UNIT * u + UNIT]
+            else:
+                centre = upright_of[j - LANES][:]
+            work = work_pool.tile([P, POSITIONS, UNIT], F32)
+            work_of[j] = work
+            nc.vector.tensor_tensor(
+                out=work[:],
+                in0=unit_priors(j),
+                in1=centre.unsqueeze(1).to_broadcast([P, POSITIONS, UNIT]),
+                op=ALU.subtract,
+            )
+            nc.scalar.activation(out=work[:], in_=work[:], func=ACT.Square)
+
+        def sum_distances(j):
+            distance = small.tile([P, POSITIONS, UNIT_CAPSULES], F32)
+            nc.vector.tensor_reduce(
+                out=distance[:],
+                in_=work_of[j][:].rearrange("p t (c e) -> p t c e", e=CAPSULE),
+                axis=X_AXIS,
+                op=ALU.add,
+            )
+            pull = small.tile([P, POSITIONS, UNIT_CAPSULES], F32)
+            pull_of[j] = pull
+            nc.scalar.activation(
+                out=pull[:], in_=distance[:], func=ACT.Abs_reciprocal_sqrt, bias=eps[:, 0:1]
+            )
+
+        def normalise(j):
+            pull = pull_of[j]
+            pull_sum = small.tile([P, UNIT_CAPSULES], F32)
+            nc.vector.tensor_reduce(
+                out=pull_sum[:], in_=pull[:].rearrange("p t c -> p c t"), axis=X_AXIS, op=ALU.add
+            )
+            pull_scale = small.tile([P, UNIT_CAPSULES], F32)
+            nc.vector.reciprocal(out=pull_scale[:], in_=pull_sum[:])
+            coupling = small.tile([P, POSITIONS, UNIT_CAPSULES], F32)
+            coupling_of[j] = coupling
+            nc.vector.tensor_tensor(
+                out=coupling[:],
+                in0=pull[:],
+                in1=pull_scale[:].unsqueeze(1).to_broadcast([P, POSITIONS, UNIT_CAPSULES]),
+                op=ALU.mult,
+            )
+
+        def weigh(j):
+            nc.gpsimd.tensor_tensor(
+                out=work_of[j][:].rearrange("p t (c e) -> p t c e", e=CAPSULE),
+                in0=unit_priors(j).rearrange("p t (c e) -> p t c e", e=CAPSULE),
+                in1=coupling_of[j][:].unsqueeze(3).to_broadcast([P, POSITIONS, UNIT_CAPSULES, CAPSULE]),
+                op=ALU.mult,
+            )
+
+        def add_up(j):
+            flipped_sum = flip_banks.tile([P, UNIT_BLOCKS, P], F32)
+            flipped_sum_of[j] = flipped_sum
+            for b in range(UNIT_BLOCKS):
+                for t in range(POSITIONS):
+                    nc.tensor.matmul(
+                        out=flipped_sum[:, b, :],
+                        lhsT=work_of[j][:, t, P * b : P * b + P],
+                        rhs=identity[:],
+                        is_transpose=True,
+                        start=(t == 0),
+                        stop=(t == POSITIONS - 1),
+                    )
+
+        def collect(j):
+            m, u, step = job_parts(j)
+            flipped = small.tile([P, UNIT_BLOCKS, P], F32)
+            nc.scalar.copy(out=flipped[:], in_=flipped_sum_of[j][:])
+            if step == ROUTING_STEPS - 1:
+                nc.sync.dma_start(
+                    out=out_rows[UNIT * u : UNIT * u + UNIT, P * m : P * m + P].rearrange(
+                        "(b r) x -> r b x", r=P
+                    ),
+                    in_=flipped[:],
+                )
+            else:
+                upright = flip_banks.tile([P, UNIT], F32)
+                upright_of[j] = upright
+                for b in range(UNIT_BLOCKS):
+                    nc.tensor.transpose(
+                        out=upright[:, P * b : P * b + P], in_=flipped[:, b, :], identity=identity[:]
+                    )
+
+        nc.scalar.dma_start(
+            out=bias_rows[:].rearrange("p t n -> p (t n)"),
+            in_=bias[0, 0, 0].rearrange("i j o n -> (i j o n)").partition_broadcast(P),
+        )
+        make_identity(nc, identity[:])
+        nc.vector.memset(eps[:], EPS)
+        quantise_image(nc, image_stage, image, even_codes, even_scales, odd_codes, odd_scales)
+        nc.vector.tensor_reduce(
+            out=bias_mean[:], in_=bias_rows[:].rearrange("p t n -> p n t"), axis=X_AXIS, op=ALU.add
+        )
+        nc.vector.tensor_scalar_mul(out=bias_mean[:], in0=bias_mean[:], scalar1=1.0 / POSITIONS)
+        for t in range(POSITIONS):
+            quantise_weight(nc, weight_stage, weight, t, weight_codes, weight_scales)
+            for m in range(TILES_PER_GROUP):
+                multiply(m, t)
+                add_bias(m, t)
+
+        for k in range(JOBS + 3):
+            group, turn = divmod(k, JOBS_PER_GROUP)
+            pieces = []
+            for i in range(PIECES_PER_TURN):
+                piece = PIECES_PER_TURN * turn + i
+                m = TILES_PER_GROUP * (group + 1) + piece // POSITIONS
+                if piece < TILES_PER_GROUP * POSITIONS and m < PIXEL_TILES:
+                    pieces.append((m, piece % POSITIONS))
+            for m, t in pieces:
+                multiply(m, t)
+            if 0 <= k - 3 < JOBS:
+                collect(k - 3)
+            if k < JOBS:
+                subtract_and_square(k)
+            if 0 <= k - 1 < JOBS:
+                sum_distances(k - 1)
+            for m, t in pieces:
+                add_bias(m, t)
+            if 0 <= k - 1 < JOBS:
+                normalise(k - 1)
+                weigh(k - 1)
+            if 0 <= k - 2 < JOBS:
+                add_up(k - 2)

@@ -19,33 +19,56 @@ PADDED_ROWS = SIDE + 2
 KERNEL = 3
 POSITIONS = KERNEL * KERNEL
 FEATURES = 512
-CAPSULE = 16
-ROUTING_STEPS = 3
+CHANNELS = 16
+CAPSULES = FEATURES // CHANNELS
 EPS = 1e-4
 
-PIXEL_TILES = SIDE * SIDE // P
-UNIT = 256
-UNIT_CAPSULES = UNIT // CAPSULE
-UNITS_PER_TILE = FEATURES // UNIT
-UNIT_BLOCKS = UNIT // P
-
-LANES = 4
-TILES_PER_GROUP = LANES // UNITS_PER_TILE
-JOBS_PER_GROUP = LANES * ROUTING_STEPS
-JOBS = PIXEL_TILES * UNITS_PER_TILE * ROUTING_STEPS
-PIECES_PER_TURN = 2
+GROUPS = 2
+GROUP_TILES = 4
+LANES = GROUP_TILES * CAPSULES
+CHUNK = 2
+CHUNKS = CHANNELS // CHUNK
+PHASES = 4
+BANK_SLOTS = 4
+BANK = 2048
+GPSIMD_POSITIONS = (0, 6, 6, 5)
 
 FLOPS = 2 * POSITIONS * SIDE * SIDE * (P * PACK) * FEATURES
 
+PRIOR_BYTES = POSITIONS * CHANNELS * LANES * 4
+WORK_BYTES = POSITIONS * CHUNK * LANES * 4
+AT_PRIORS = 0
+AT_RAW_IMAGE = PRIOR_BYTES
+AT_SHIFTED = AT_RAW_IMAGE + PACK * SIDE * SIDE * 2
+AT_RAW_WEIGHT = AT_SHIFTED + 2 * PADDED_ROWS * SIDE * PACK * 2
+AT_GROUPED = AT_RAW_WEIGHT + 4 * PACK * FEATURES * 2
+AT_BIAS_ROWS = AT_GROUPED + 2 * PACK * FEATURES * 2
+AT_REST = 2 * PRIOR_BYTES
+AT_WEIGHT_CODES = AT_REST
+AT_WEIGHT_SCALES = AT_WEIGHT_CODES + POSITIONS * FEATURES * 4
+AT_EVEN_CODES = AT_WEIGHT_SCALES + POSITIONS * FEATURES
+AT_EVEN_SCALES = AT_EVEN_CODES + KERNEL * PADDED_ROWS * SIDE * 4
+AT_ODD_CODES = AT_EVEN_SCALES + KERNEL * PADDED_ROWS * SIDE
+AT_ODD_SCALES = AT_ODD_CODES + KERNEL * SIDE * SIDE * 4
+AT_BIAS = AT_ODD_SCALES + KERNEL * SIDE * SIDE
+AT_BIAS_MEAN = AT_BIAS + POSITIONS * FEATURES * 2
+AT_MEAN = AT_BIAS_MEAN + FEATURES * 4
+AT_WEIGHED = AT_REST
+AT_DIFFERENCE = AT_WEIGHED + 3 * WORK_BYTES
+AT_PULL_FLIPPED = AT_DIFFERENCE + 3 * WORK_BYTES
+AT_PULL = AT_PULL_FLIPPED + 2 * POSITIONS * LANES * 4
 
-def quantise_image(nc, stage, image, even_codes, even_scales, odd_codes, odd_scales):
-    raw_image = stage.tile([P, PACK, SIDE, SIDE], BF16)
+
+def quantise_image(nc, arena, image, even_codes, even_scales, odd_codes, odd_scales):
+    raw_image = arena.tile([P, PACK, SIDE, SIDE], BF16, offset=AT_RAW_IMAGE)
     nc.sync.dma_start(out=raw_image[:], in_=image[0].rearrange("(p j) h w -> p j h w", j=PACK))
     row = SIDE * PACK
     whole = SIDE * SIDE
     rest = (PADDED_ROWS - SIDE) * SIDE
     for kj in range(KERNEL):
-        shifted = stage.tile([P, PADDED_ROWS, SIDE, PACK], BF16, align_bytes=64)
+        shifted = arena.tile(
+            [P, PADDED_ROWS, SIDE, PACK], BF16, align_bytes=64, bufs=2, offset=AT_SHIFTED
+        )
         nc.vector.memset(shifted[:, 0, :, :], 0.0)
         nc.vector.memset(shifted[:, PADDED_ROWS - 1, :, :], 0.0)
         first = max(0, 1 - kj)
@@ -76,56 +99,62 @@ def quantise_image(nc, stage, image, even_codes, even_scales, odd_codes, odd_sca
         )
 
 
-def quantise_weight(nc, stage, weight, t, weight_codes, weight_scales):
-    raw_weight = stage.tile([P, PACK, FEATURES], BF16, bufs=3)
+def quantise_weight(nc, arena, weight, t, weight_codes, weight_scales):
+    raw_weight = arena.tile([P, PACK, FEATURES], BF16, bufs=4, offset=AT_RAW_WEIGHT)
     nc.sync.dma_start(
         out=raw_weight[:],
         in_=weight[0, 0, 0, t // KERNEL, t % KERNEL].rearrange("(p j) n -> p j n", j=PACK),
     )
-    grouped = stage.tile([P, FEATURES, PACK], BF16, align_bytes=64)
-    nc.scalar.copy(out=grouped[:], in_=raw_weight[:].rearrange("p j n -> p n j"))
+    grouped = arena.tile(
+        [P, CHANNELS, CAPSULES, PACK], BF16, align_bytes=64, bufs=2, offset=AT_GROUPED
+    )
+    nc.scalar.copy(
+        out=grouped[:], in_=raw_weight[:].rearrange("p j (c e) -> p e c j", e=CHANNELS)
+    )
     nc.vector.quantize_mx(
         out=weight_codes[:, t, :].bitcast(FP8X4),
         scales=weight_scales[:, t, :],
-        in_=grouped[:].rearrange("p n j -> p (n j)"),
+        in_=grouped[:].rearrange("p e c j -> p (e c j)"),
     )
-
-
-def job_parts(j):
-    group, rest = divmod(j, JOBS_PER_GROUP)
-    step, lane = divmod(rest, LANES)
-    return TILES_PER_GROUP * group + lane // UNITS_PER_TILE, lane % UNITS_PER_TILE, step
 
 
 def tile_capsulelayer_kernel(tc, image, weight, bias, out):
     nc = tc.nc
-    out_rows = out[0].rearrange("f h w -> f (h w)")
+    out_view = out[0].rearrange("(c e) h w -> c e (h w)", e=CHANNELS)
 
     with ExitStack() as stack:
         stack.enter_context(tc.manual_schedule())
-        keep = stack.enter_context(tc.tile_pool(name="keep", bufs=1))
-        image_stage = stack.enter_context(tc.tile_pool(name="image_stage", bufs=1))
-        weight_stage = stack.enter_context(tc.tile_pool(name="weight_stage", bufs=2))
-        prior_pool = stack.enter_context(tc.tile_pool(name="prior_pool", bufs=2 * TILES_PER_GROUP))
-        work_pool = stack.enter_context(tc.tile_pool(name="work_pool", bufs=LANES))
-        small = stack.enter_context(tc.tile_pool(name="small", bufs=LANES))
-        product_banks = stack.enter_context(tc.psum_pool(name="product_banks", bufs=2))
-        total_banks = stack.enter_context(tc.psum_pool(name="total_banks", bufs=TILES_PER_GROUP))
-        flip_banks = stack.enter_context(tc.psum_pool(name="flip_banks", bufs=2))
+        arena = stack.enter_context(tc.tile_pool(name="arena", bufs=1))
+        small = stack.enter_context(tc.tile_pool(name="small", bufs=2))
+        banks = stack.enter_context(tc.psum_pool(name="banks", bufs=1))
 
-        weight_codes = keep.tile([P, POSITIONS, FEATURES], U32, align_bytes=64)
-        weight_scales = keep.tile([P, POSITIONS, FEATURES], U8, align_bytes=64)
-        even_codes = keep.tile([P, KERNEL, PADDED_ROWS * SIDE], U32, align_bytes=64)
-        even_scales = keep.tile([P, KERNEL, PADDED_ROWS * SIDE], U8, align_bytes=64)
-        odd_codes = keep.tile([P, KERNEL, SIDE * SIDE], U32, align_bytes=64)
-        odd_scales = keep.tile([P, KERNEL, SIDE * SIDE], U8, align_bytes=64)
-        bias_rows = keep.tile([P, POSITIONS, FEATURES], BF16)
-        bias_mean = keep.tile([P, FEATURES], F32)
-        identity = keep.tile([P, P], F32)
-        eps = keep.tile([P, 1], F32)
+        priors_0 = arena.tile([P, POSITIONS, CHANNELS, LANES], F32, offset=AT_PRIORS)
+        priors_1 = arena.tile([P, POSITIONS, CHANNELS, LANES], F32, offset=AT_PRIORS + PRIOR_BYTES)
+        priors_of = (priors_0, priors_1)
+        mean_0 = arena.tile([P, CHANNELS, LANES], F32, offset=AT_MEAN)
+        mean_1 = arena.tile([P, CHANNELS, LANES], F32, offset=AT_MEAN + CHANNELS * LANES * 4)
+        mean_of = (mean_0, mean_1)
+        weight_codes = arena.tile(
+            [P, POSITIONS, FEATURES], U32, align_bytes=64, offset=AT_WEIGHT_CODES
+        )
+        weight_scales = arena.tile(
+            [P, POSITIONS, FEATURES], U8, align_bytes=64, offset=AT_WEIGHT_SCALES
+        )
+        even_codes = arena.tile(
+            [P, KERNEL, PADDED_ROWS * SIDE], U32, align_bytes=64, offset=AT_EVEN_CODES
+        )
+        even_scales = arena.tile(
+            [P, KERNEL, PADDED_ROWS * SIDE], U8, align_bytes=64, offset=AT_EVEN_SCALES
+        )
+        odd_codes = arena.tile([P, KERNEL, SIDE * SIDE], U32, align_bytes=64, offset=AT_ODD_CODES)
+        odd_scales = arena.tile([P, KERNEL, SIDE * SIDE], U8, align_bytes=64, offset=AT_ODD_SCALES)
+        bias_rows = arena.tile([P, POSITIONS, CAPSULES, CHANNELS], BF16, offset=AT_BIAS_ROWS)
+        bias_tile = arena.tile([P, POSITIONS, CHANNELS, CAPSULES], BF16, offset=AT_BIAS)
+        bias_mean = arena.tile([P, CHANNELS, CAPSULES], F32, offset=AT_BIAS_MEAN)
+        identity = small.tile([P, P], F32, bufs=1)
+        eps = small.tile([P, 1], F32, bufs=1)
 
-        products, totals, priors_of, mean_of = {}, {}, {}, {}
-        work_of, pull_of, coupling_of, flipped_sum_of, upright_of = {}, {}, {}, {}, {}
+        products, totals = {}, {}
 
         def multiply(m, t):
             ki, kj = divmod(t, KERNEL)
@@ -135,13 +164,13 @@ def tile_capsulelayer_kernel(tc, image, weight, bias, out):
             else:
                 pixels = slice(P * m + SIDE * ki, P * m + SIDE * ki + P)
                 codes, scales = even_codes[:, kj, pixels], even_scales[:, kj, pixels]
-            product = product_banks.tile([P, FEATURES], F32)
+            product = banks.tile([P, CHANNELS, CAPSULES], F32, bufs=3, offset=0)
             products[(m, t)] = product
             if t == 0:
-                total = total_banks.tile([P, FEATURES], F32)
-                totals[m] = total
+                product_sum = banks.tile([P, CHANNELS, CAPSULES], F32, bufs=4, offset=3 * BANK)
+                totals[m] = product_sum
             nc.tensor.matmul_mx(
-                out=product[:],
+                out=product[:].rearrange("p e c -> p (e c)"),
                 lhsT=codes.bitcast(FP8X4),
                 lhsT_scale=scales,
                 rhs=weight_codes[:, t, :].bitcast(FP8X4),
@@ -150,7 +179,7 @@ def tile_capsulelayer_kernel(tc, image, weight, bias, out):
                 stop=True,
             )
             nc.tensor.matmul_mx(
-                out=totals[m][:],
+                out=totals[m][:].rearrange("p e c -> p (e c)"),
                 lhsT=codes.bitcast(FP8X4),
                 lhsT_scale=scales,
                 rhs=weight_codes[:, t, :].bitcast(FP8X4),
@@ -160,17 +189,17 @@ def tile_capsulelayer_kernel(tc, image, weight, bias, out):
             )
 
         def add_bias(m, t):
-            if t == 0:
-                priors = prior_pool.tile([P, POSITIONS, FEATURES], F32)
-                priors_of[m] = priors
+            g, lane = divmod(m, GROUP_TILES)
+            lanes = slice(CAPSULES * lane, CAPSULES * lane + CAPSULES)
             nc.vector.tensor_tensor(
-                out=priors_of[m][:, t, :], in0=products[(m, t)][:], in1=bias_rows[:, t, :], op=ALU.add
+                out=priors_of[g][:, t, :, lanes],
+                in0=products[(m, t)][:],
+                in1=bias_tile[:, t, :, :],
+                op=ALU.add,
             )
             if t == POSITIONS - 1:
-                mean = small.tile([P, FEATURES], F32)
-                mean_of[m] = mean
                 nc.vector.scalar_tensor_tensor(
-                    out=mean[:],
+                    out=mean_of[g][:, :, lanes],
                     in0=totals[m][:],
                     scalar=1.0 / POSITIONS,
                     in1=bias_mean[:],
@@ -178,135 +207,218 @@ def tile_capsulelayer_kernel(tc, image, weight, bias, out):
                     op1=ALU.add,
                 )
 
-        def unit_priors(j):
-            m, u, step = job_parts(j)
-            return priors_of[m][:, :, UNIT * u : UNIT * u + UNIT]
+        nc.scalar.dma_start(
+            out=bias_rows[:].rearrange("p t c e -> p (t c e)"),
+            in_=bias[0, 0, 0].rearrange("i j o n -> (i j o n)").partition_broadcast(P),
+        )
+        make_identity(nc, identity[:])
+        nc.vector.memset(eps[:], EPS)
+        nc.gpsimd.tensor_copy(out=bias_tile[:], in_=bias_rows[:].rearrange("p t c e -> p t e c"))
+        quantise_image(nc, arena, image, even_codes, even_scales, odd_codes, odd_scales)
+        nc.vector.tensor_reduce(
+            out=bias_mean[:], in_=bias_tile[:].rearrange("p t e c -> p e c t"), axis=X_AXIS, op=ALU.add
+        )
+        nc.vector.tensor_scalar_mul(out=bias_mean[:], in0=bias_mean[:], scalar1=1.0 / POSITIONS)
+        for t in range(POSITIONS):
+            quantise_weight(nc, arena, weight, t, weight_codes, weight_scales)
+            for m in range(GROUP_TILES):
+                multiply(m, t)
+                add_bias(m, t)
+        for t in range(POSITIONS):
+            for m in range(GROUP_TILES, 2 * GROUP_TILES):
+                multiply(m, t)
+                add_bias(m, t)
 
-        def subtract_and_square(j):
-            m, u, step = job_parts(j)
-            if step == 0:
-                centre = mean_of[m][:, UNIT * u : UNIT * u + UNIT]
-            else:
-                centre = upright_of[j - LANES][:]
-            work = work_pool.tile([P, POSITIONS, UNIT], F32)
-            work_of[j] = work
-            nc.vector.tensor_tensor(
-                out=work[:],
-                in0=unit_priors(j),
-                in1=centre.unsqueeze(1).to_broadcast([P, POSITIONS, UNIT]),
-                op=ALU.subtract,
-            )
-            nc.scalar.activation(out=work[:], in_=work[:], func=ACT.Square)
+        items = [(s, g, k) for s in range(PHASES) for g in range(GROUPS) for k in range(CHUNKS)]
+        weighed_of, total_of, centre_flipped_of, centre_of, difference_of = {}, {}, {}, {}, {}
+        distance_banks = {}
+        pull_flipped_of, pull_scale_of, pull_sbuf_of, pull_psum_of = {}, {}, {}, {}
 
-        def sum_distances(j):
-            distance = small.tile([P, POSITIONS, UNIT_CAPSULES], F32)
-            nc.vector.tensor_reduce(
-                out=distance[:],
-                in_=work_of[j][:].rearrange("p t (c e) -> p t c e", e=CAPSULE),
-                axis=X_AXIS,
-                op=ALU.add,
-            )
-            pull = small.tile([P, POSITIONS, UNIT_CAPSULES], F32)
-            pull_of[j] = pull
-            nc.scalar.activation(
-                out=pull[:], in_=distance[:], func=ACT.Abs_reciprocal_sqrt, bias=eps[:, 0:1]
-            )
+        def chunk_priors(i):
+            s, g, k = items[i]
+            return priors_of[g][:, :, CHUNK * k : CHUNK * k + CHUNK, :]
 
-        def normalise(j):
-            pull = pull_of[j]
-            pull_sum = small.tile([P, UNIT_CAPSULES], F32)
-            nc.vector.tensor_reduce(
-                out=pull_sum[:], in_=pull[:].rearrange("p t c -> p c t"), axis=X_AXIS, op=ALU.add
-            )
-            pull_scale = small.tile([P, UNIT_CAPSULES], F32)
-            nc.vector.reciprocal(out=pull_scale[:], in_=pull_sum[:])
-            coupling = small.tile([P, POSITIONS, UNIT_CAPSULES], F32)
-            coupling_of[j] = coupling
-            nc.vector.tensor_tensor(
-                out=coupling[:],
-                in0=pull[:],
-                in1=pull_scale[:].unsqueeze(1).to_broadcast([P, POSITIONS, UNIT_CAPSULES]),
-                op=ALU.mult,
-            )
-
-        def weigh(j):
+        def weigh_gpsimd(i):
+            s, g, k = items[i]
+            n = GPSIMD_POSITIONS[s]
+            weighed = arena.tile([P, POSITIONS, CHUNK, LANES], F32, bufs=3, offset=AT_WEIGHED)
+            weighed_of[i] = weighed
             nc.gpsimd.tensor_tensor(
-                out=work_of[j][:].rearrange("p t (c e) -> p t c e", e=CAPSULE),
-                in0=unit_priors(j).rearrange("p t (c e) -> p t c e", e=CAPSULE),
-                in1=coupling_of[j][:].unsqueeze(3).to_broadcast([P, POSITIONS, UNIT_CAPSULES, CAPSULE]),
+                out=weighed[:, 0:n, :, :],
+                in0=chunk_priors(i)[:, 0:n, :, :],
+                in1=pull_sbuf_of[(s, g)][:, 0:n, :].unsqueeze(2).to_broadcast([P, n, CHUNK, LANES]),
                 op=ALU.mult,
             )
 
-        def add_up(j):
-            flipped_sum = flip_banks.tile([P, UNIT_BLOCKS, P], F32)
-            flipped_sum_of[j] = flipped_sum
-            for b in range(UNIT_BLOCKS):
+        def weigh_vector(i):
+            s, g, k = items[i]
+            n = GPSIMD_POSITIONS[s]
+            nc.vector.tensor_tensor(
+                out=weighed_of[i][:, n:POSITIONS, :, :],
+                in0=chunk_priors(i)[:, n:POSITIONS, :, :],
+                in1=pull_psum_of[(s, g)][:, 0 : POSITIONS - n, :]
+                .unsqueeze(2)
+                .to_broadcast([P, POSITIONS - n, CHUNK, LANES]),
+                op=ALU.mult,
+            )
+
+        def sum_positions(i):
+            weighted_sum = banks.tile([P, BANK_SLOTS, P], F32, offset=6 * BANK)
+            total_of[i] = weighted_sum
+            for c in range(CHUNK):
                 for t in range(POSITIONS):
                     nc.tensor.matmul(
-                        out=flipped_sum[:, b, :],
-                        lhsT=work_of[j][:, t, P * b : P * b + P],
+                        out=weighted_sum[:, c, :],
+                        lhsT=weighed_of[i][:, t, c, :],
                         rhs=identity[:],
                         is_transpose=True,
                         start=(t == 0),
                         stop=(t == POSITIONS - 1),
                     )
 
-        def collect(j):
-            m, u, step = job_parts(j)
-            flipped = small.tile([P, UNIT_BLOCKS, P], F32)
-            nc.scalar.copy(out=flipped[:], in_=flipped_sum_of[j][:])
-            if step == ROUTING_STEPS - 1:
-                nc.sync.dma_start(
-                    out=out_rows[UNIT * u : UNIT * u + UNIT, P * m : P * m + P].rearrange(
-                        "(b r) x -> r b x", r=P
-                    ),
-                    in_=flipped[:],
-                )
+        def normalise(i):
+            s, g, k = items[i]
+            if s == PHASES - 1:
+                centre_flipped = small.tile([P, CHUNK, P], F32, bufs=4, tag="result")
             else:
-                upright = flip_banks.tile([P, UNIT], F32)
-                upright_of[j] = upright
-                for b in range(UNIT_BLOCKS):
-                    nc.tensor.transpose(
-                        out=upright[:, P * b : P * b + P], in_=flipped[:, b, :], identity=identity[:]
+                centre_flipped = small.tile([P, CHUNK, P], F32, bufs=3, tag="centre_flipped")
+            centre_flipped_of[i] = centre_flipped
+            nc.vector.tensor_tensor(
+                out=centre_flipped[:],
+                in0=total_of[i][:, 0:CHUNK, :],
+                in1=pull_scale_of[(s, g)][:].unsqueeze(1).to_broadcast([P, CHUNK, P]),
+                op=ALU.mult,
+            )
+
+        def store(i):
+            s, g, k = items[i]
+            for lane in range(GROUP_TILES):
+                m = GROUP_TILES * g + lane
+                nc.sync.dma_start(
+                    out=out_view[:, CHUNK * k : CHUNK * k + CHUNK, P * m : P * m + P],
+                    in_=centre_flipped_of[i][CAPSULES * lane : CAPSULES * lane + CAPSULES, :, :],
+                )
+
+        def flip_centre(i):
+            centre = banks.tile([P, BANK_SLOTS, LANES], F32, offset=7 * BANK)
+            centre_of[i] = centre
+            for c in range(CHUNK):
+                nc.tensor.transpose(
+                    out=centre[:, c, :], in_=centre_flipped_of[i][:, c, :], identity=identity[:]
+                )
+
+        def subtract_and_square(i):
+            s, g, k = items[i]
+            if s == 0:
+                centre = mean_of[g][:, CHUNK * k : CHUNK * k + CHUNK, :]
+            else:
+                centre = centre_of[i][:, 0:CHUNK, :]
+            difference = arena.tile([P, POSITIONS, CHUNK, LANES], F32, bufs=3, offset=AT_DIFFERENCE)
+            difference_of[i] = difference
+            nc.vector.tensor_tensor(
+                out=difference[:],
+                in0=chunk_priors(i),
+                in1=centre.unsqueeze(1).to_broadcast([P, POSITIONS, CHUNK, LANES]),
+                op=ALU.subtract,
+            )
+            nc.scalar.activation(out=difference[:], in_=difference[:], func=ACT.Square)
+
+        def sum_channels(i):
+            s, g, k = items[i]
+            if k == 0:
+                distance_0 = banks.tile([P, BANK_SLOTS, P], F32, offset=0)
+                distance_1 = banks.tile([P, BANK_SLOTS, P], F32, offset=BANK)
+                distance_2 = banks.tile([P, BANK_SLOTS, P], F32, offset=2 * BANK)
+                distance_banks[(s, g)] = (distance_0, distance_1, distance_2)
+            for t in range(POSITIONS):
+                b, slot = divmod(t, BANK_SLOTS)
+                last_slot = slot == BANK_SLOTS - 1 or t == POSITIONS - 1
+                for c in range(CHUNK):
+                    nc.tensor.matmul(
+                        out=distance_banks[(s, g)][b][:, slot, :],
+                        lhsT=difference_of[i][:, t, c, :],
+                        rhs=identity[:],
+                        is_transpose=True,
+                        start=(k == 0 and slot == 0 and c == 0),
+                        stop=(k == CHUNKS - 1 and last_slot and c == CHUNK - 1),
                     )
 
-        nc.scalar.dma_start(
-            out=bias_rows[:].rearrange("p t n -> p (t n)"),
-            in_=bias[0, 0, 0].rearrange("i j o n -> (i j o n)").partition_broadcast(P),
-        )
-        make_identity(nc, identity[:])
-        nc.vector.memset(eps[:], EPS)
-        quantise_image(nc, image_stage, image, even_codes, even_scales, odd_codes, odd_scales)
-        nc.vector.tensor_reduce(
-            out=bias_mean[:], in_=bias_rows[:].rearrange("p t n -> p n t"), axis=X_AXIS, op=ALU.add
-        )
-        nc.vector.tensor_scalar_mul(out=bias_mean[:], in0=bias_mean[:], scalar1=1.0 / POSITIONS)
-        for t in range(POSITIONS):
-            quantise_weight(nc, weight_stage, weight, t, weight_codes, weight_scales)
-            for m in range(TILES_PER_GROUP):
-                multiply(m, t)
-                add_bias(m, t)
+        def pulls(s, g):
+            pull_flipped = arena.tile([P, POSITIONS, P], F32, bufs=2, offset=AT_PULL_FLIPPED)
+            pull_flipped_of[(s + 1, g)] = pull_flipped
+            for b in range(3):
+                n = min(BANK_SLOTS, POSITIONS - BANK_SLOTS * b)
+                nc.scalar.activation(
+                    out=pull_flipped[:, BANK_SLOTS * b : BANK_SLOTS * b + n, :],
+                    in_=distance_banks[(s, g)][b][:, 0:n, :],
+                    func=ACT.Abs_reciprocal_sqrt,
+                    bias=eps[:, 0:1],
+                )
 
-        for k in range(JOBS + 3):
-            group, turn = divmod(k, JOBS_PER_GROUP)
-            pieces = []
-            for i in range(PIECES_PER_TURN):
-                piece = PIECES_PER_TURN * turn + i
-                m = TILES_PER_GROUP * (group + 1) + piece // POSITIONS
-                if piece < TILES_PER_GROUP * POSITIONS and m < PIXEL_TILES:
-                    pieces.append((m, piece % POSITIONS))
-            for m, t in pieces:
-                multiply(m, t)
-            if 0 <= k - 3 < JOBS:
-                collect(k - 3)
-            if k < JOBS:
-                subtract_and_square(k)
-            if 0 <= k - 1 < JOBS:
-                sum_distances(k - 1)
-            for m, t in pieces:
-                add_bias(m, t)
-            if 0 <= k - 1 < JOBS:
-                normalise(k - 1)
-                weigh(k - 1)
-            if 0 <= k - 2 < JOBS:
-                add_up(k - 2)
+        def flip_pulls(s, g, first, last, psum_tile):
+            for t in range(first, last):
+                nc.tensor.transpose(
+                    out=psum_tile[:, t - first, :],
+                    in_=pull_flipped_of[(s, g)][:, t, :],
+                    identity=identity[:],
+                )
+
+        def pulls_first_part(s, g):
+            pull_sum = small.tile([P, P], F32)
+            nc.vector.tensor_reduce(
+                out=pull_sum[:],
+                in_=pull_flipped_of[(s, g)][:].rearrange("p t x -> p x t"),
+                axis=X_AXIS,
+                op=ALU.add,
+            )
+            pull_scale = small.tile([P, P], F32)
+            pull_scale_of[(s, g)] = pull_scale
+            nc.vector.reciprocal(out=pull_scale[:], in_=pull_sum[:])
+            pull_sbuf = arena.tile([P, 6, LANES], F32, bufs=2, offset=AT_PULL)
+            pull_sbuf_of[(s, g)] = pull_sbuf
+            passing = banks.tile([P, BANK_SLOTS, LANES], F32, offset=3 * BANK)
+            flip_pulls(s, g, 0, BANK_SLOTS, passing)
+            nc.scalar.copy(out=pull_sbuf[:, 0:BANK_SLOTS, :], in_=passing[:])
+
+        def pulls_second_part(s, g):
+            n = GPSIMD_POSITIONS[s]
+            passing = banks.tile([P, BANK_SLOTS, LANES], F32, offset=3 * BANK)
+            flip_pulls(s, g, BANK_SLOTS, n, passing)
+            nc.scalar.copy(
+                out=pull_sbuf_of[(s, g)][:, BANK_SLOTS:n, :], in_=passing[:, 0 : n - BANK_SLOTS, :]
+            )
+            pull_psum = banks.tile([P, BANK_SLOTS, LANES], F32, bufs=2, offset=4 * BANK)
+            pull_psum_of[(s, g)] = pull_psum
+            flip_pulls(s, g, n, POSITIONS, pull_psum)
+
+        count = len(items)
+
+        def at(i):
+            return items[i] if 0 <= i < count else (-1, -1, -1)
+
+        for turn in range(count + 6):
+            if at(turn)[0] >= 1:
+                weigh_gpsimd(turn)
+            if at(turn - 1)[0] >= 1:
+                sum_positions(turn - 1)
+            if 0 <= at(turn - 2)[0] < PHASES - 1:
+                subtract_and_square(turn - 2)
+            s, g, k = at(turn - 3)
+            if 0 <= s < PHASES - 1:
+                sum_channels(turn - 3)
+                if k == CHUNKS - 1:
+                    pulls(s, g)
+            if at(turn - 1)[0] >= 1:
+                normalise(turn - 1)
+                if at(turn - 1)[0] == PHASES - 1:
+                    store(turn - 1)
+                else:
+                    flip_centre(turn - 1)
+            s, g, k = at(turn - 4)
+            if 0 <= s < PHASES - 1 and k == CHUNKS - 1:
+                pulls_first_part(s + 1, g)
+            s, g, k = at(turn - 5)
+            if 0 <= s < PHASES - 1 and k == CHUNKS - 1:
+                pulls_second_part(s + 1, g)
+            if at(turn)[0] >= 1:
+                weigh_vector(turn)

@@ -32,6 +32,9 @@ PHASES = 4
 BANK_SLOTS = 4
 BANK = 2048
 GPSIMD_POSITIONS = (0, 6, 6, 5)
+TURN_PASSES = (31, 46, 46, 35)
+WARM_EVERY = 4
+WARM_WORTH = 13
 
 FLOPS = 2 * POSITIONS * SIDE * SIDE * (P * PACK) * FEATURES
 
@@ -376,36 +379,58 @@ def tile_capsulelayer_kernel(tc, image, weight, bias, out):
             nc.vector.reciprocal(out=pull_scale[:], in_=pull_sum[:])
             pull_sbuf = arena.tile([P, 6, LANES], F32, bufs=2, offset=AT_PULL)
             pull_sbuf_of[(s, g)] = pull_sbuf
-            passing = banks.tile([P, BANK_SLOTS, LANES], F32, offset=3 * BANK)
+            passing = banks.tile([P, BANK_SLOTS, LANES], F32, tag="pulls%d" % g, offset=(4 + g) * BANK)
             flip_pulls(s, g, 0, BANK_SLOTS, passing)
             nc.scalar.copy(out=pull_sbuf[:, 0:BANK_SLOTS, :], in_=passing[:])
 
         def pulls_second_part(s, g):
             n = GPSIMD_POSITIONS[s]
-            passing = banks.tile([P, BANK_SLOTS, LANES], F32, offset=3 * BANK)
+            passing = banks.tile([P, BANK_SLOTS, LANES], F32, tag="pulls%d" % g, offset=(4 + g) * BANK)
             flip_pulls(s, g, BANK_SLOTS, n, passing)
             nc.scalar.copy(
                 out=pull_sbuf_of[(s, g)][:, BANK_SLOTS:n, :], in_=passing[:, 0 : n - BANK_SLOTS, :]
             )
-            pull_psum = banks.tile([P, BANK_SLOTS, LANES], F32, bufs=2, offset=4 * BANK)
+
+        def pulls_third_part(s, g):
+            n = GPSIMD_POSITIONS[s]
+            pull_psum = banks.tile([P, BANK_SLOTS, LANES], F32, tag="pulls%d" % g, offset=(4 + g) * BANK)
             pull_psum_of[(s, g)] = pull_psum
             flip_pulls(s, g, n, POSITIONS, pull_psum)
 
         count = len(items)
+        scratch = banks.tile([P, BANK_SLOTS, P], F32, offset=3 * BANK)
+
+        def fill(n):
+            for j in range(n):
+                nc.tensor.transpose(
+                    out=scratch[:, j % BANK_SLOTS, :], in_=identity[:], identity=identity[:]
+                )
+
+        def warm():
+            nc.tensor.matmul(
+                out=scratch[:].rearrange("p s x -> p (s x)"),
+                lhsT=identity[:],
+                rhs=priors_0[:, 0, 0:BANK_SLOTS, :].rearrange("p e x -> p (e x)"),
+                start=True,
+                stop=True,
+            )
 
         def at(i):
             return items[i] if 0 <= i < count else (-1, -1, -1)
 
-        for turn in range(count + 6):
+        for turn in range(count + 7):
+            passes = 0
             if at(turn)[0] >= 1:
                 weigh_gpsimd(turn)
             if at(turn - 1)[0] >= 1:
                 sum_positions(turn - 1)
+                passes += CHUNK * POSITIONS
             if 0 <= at(turn - 2)[0] < PHASES - 1:
                 subtract_and_square(turn - 2)
             s, g, k = at(turn - 3)
             if 0 <= s < PHASES - 1:
                 sum_channels(turn - 3)
+                passes += CHUNK * POSITIONS
                 if k == CHUNKS - 1:
                     pulls(s, g)
             if at(turn - 1)[0] >= 1:
@@ -414,11 +439,23 @@ def tile_capsulelayer_kernel(tc, image, weight, bias, out):
                     store(turn - 1)
                 else:
                     flip_centre(turn - 1)
+                    passes += CHUNK
             s, g, k = at(turn - 4)
             if 0 <= s < PHASES - 1 and k == CHUNKS - 1:
                 pulls_first_part(s + 1, g)
+                passes += BANK_SLOTS
             s, g, k = at(turn - 5)
             if 0 <= s < PHASES - 1 and k == CHUNKS - 1:
                 pulls_second_part(s + 1, g)
+                passes += GPSIMD_POSITIONS[s + 1] - BANK_SLOTS
+            s, g, k = at(turn - 6)
+            if 0 <= s < PHASES - 1 and k == CHUNKS - 1:
+                pulls_third_part(s + 1, g)
+                passes += POSITIONS - GPSIMD_POSITIONS[s + 1]
+            if turn < count:
+                if turn % WARM_EVERY == 0:
+                    warm()
+                    passes += WARM_WORTH
+                fill(max(0, TURN_PASSES[at(turn)[0]] - passes))
             if at(turn)[0] >= 1:
                 weigh_vector(turn)

@@ -32,9 +32,6 @@ PHASES = 4
 BANK_SLOTS = 4
 BANK = 2048
 GPSIMD_POSITIONS = (0, 6, 6, 5)
-TURN_PASSES = (31, 46, 46, 35)
-WARM_EVERY = 4
-WARM_WORTH = 13
 
 FLOPS = 2 * POSITIONS * SIDE * SIDE * (P * PACK) * FEATURES
 
@@ -266,7 +263,7 @@ def tile_capsulelayer_kernel(tc, image, weight, bias, out):
             )
 
         def sum_positions(i):
-            weighted_sum = banks.tile([P, BANK_SLOTS, P], F32, offset=6 * BANK)
+            weighted_sum = banks.tile([P, BANK_SLOTS, P], F32, offset=3 * BANK)
             total_of[i] = weighted_sum
             for c in range(CHUNK):
                 for t in range(POSITIONS):
@@ -303,7 +300,7 @@ def tile_capsulelayer_kernel(tc, image, weight, bias, out):
                 )
 
         def flip_centre(i):
-            centre = banks.tile([P, BANK_SLOTS, LANES], F32, offset=7 * BANK)
+            centre = banks.tile([P, BANK_SLOTS, LANES], F32, bufs=2, offset=6 * BANK)
             centre_of[i] = centre
             for c in range(CHUNK):
                 nc.tensor.transpose(
@@ -348,12 +345,12 @@ def tile_capsulelayer_kernel(tc, image, weight, bias, out):
 
         def pulls(s, g):
             pull_flipped = arena.tile([P, POSITIONS, P], F32, bufs=2, offset=AT_PULL_FLIPPED)
-            pull_flipped_of[(s + 1, g)] = pull_flipped
+            pull_flipped_of[(s, g)] = pull_flipped
             for b in range(3):
                 n = min(BANK_SLOTS, POSITIONS - BANK_SLOTS * b)
                 nc.scalar.activation(
                     out=pull_flipped[:, BANK_SLOTS * b : BANK_SLOTS * b + n, :],
-                    in_=distance_banks[(s, g)][b][:, 0:n, :],
+                    in_=distance_banks[(s - 1, g)][b][:, 0:n, :],
                     func=ACT.Abs_reciprocal_sqrt,
                     bias=eps[:, 0:1],
                 )
@@ -366,7 +363,7 @@ def tile_capsulelayer_kernel(tc, image, weight, bias, out):
                     identity=identity[:],
                 )
 
-        def pulls_first_part(s, g):
+        def scale_of_pulls(s, g):
             pull_sum = small.tile([P, P], F32)
             nc.vector.tensor_reduce(
                 out=pull_sum[:],
@@ -377,85 +374,74 @@ def tile_capsulelayer_kernel(tc, image, weight, bias, out):
             pull_scale = small.tile([P, P], F32)
             pull_scale_of[(s, g)] = pull_scale
             nc.vector.reciprocal(out=pull_scale[:], in_=pull_sum[:])
+
+        passing_of = {}
+
+        def flip_first_pulls(s, g):
+            passing = banks.tile([P, BANK_SLOTS, LANES], F32, tag="pulls%d" % g, offset=(4 + g) * BANK)
+            passing_of[(s, g)] = passing
+            flip_pulls(s, g, 0, BANK_SLOTS, passing)
+
+        def copy_first_pulls(s, g):
             pull_sbuf = arena.tile([P, 6, LANES], F32, bufs=2, offset=AT_PULL)
             pull_sbuf_of[(s, g)] = pull_sbuf
-            passing = banks.tile([P, BANK_SLOTS, LANES], F32, tag="pulls%d" % g, offset=(4 + g) * BANK)
-            flip_pulls(s, g, 0, BANK_SLOTS, passing)
-            nc.scalar.copy(out=pull_sbuf[:, 0:BANK_SLOTS, :], in_=passing[:])
+            nc.scalar.copy(out=pull_sbuf[:, 0:BANK_SLOTS, :], in_=passing_of[(s, g)][:])
 
-        def pulls_second_part(s, g):
-            n = GPSIMD_POSITIONS[s]
+        def flip_second_pulls(s, g):
             passing = banks.tile([P, BANK_SLOTS, LANES], F32, tag="pulls%d" % g, offset=(4 + g) * BANK)
-            flip_pulls(s, g, BANK_SLOTS, n, passing)
+            passing_of[(s, g)] = passing
+            flip_pulls(s, g, BANK_SLOTS, GPSIMD_POSITIONS[s], passing)
+
+        def copy_second_pulls(s, g):
+            n = GPSIMD_POSITIONS[s]
             nc.scalar.copy(
-                out=pull_sbuf_of[(s, g)][:, BANK_SLOTS:n, :], in_=passing[:, 0 : n - BANK_SLOTS, :]
+                out=pull_sbuf_of[(s, g)][:, BANK_SLOTS:n, :],
+                in_=passing_of[(s, g)][:, 0 : n - BANK_SLOTS, :],
             )
 
-        def pulls_third_part(s, g):
-            n = GPSIMD_POSITIONS[s]
+        def flip_third_pulls(s, g):
             pull_psum = banks.tile([P, BANK_SLOTS, LANES], F32, tag="pulls%d" % g, offset=(4 + g) * BANK)
             pull_psum_of[(s, g)] = pull_psum
-            flip_pulls(s, g, n, POSITIONS, pull_psum)
+            flip_pulls(s, g, GPSIMD_POSITIONS[s], POSITIONS, pull_psum)
 
         count = len(items)
-        scratch = banks.tile([P, BANK_SLOTS, P], F32, offset=3 * BANK)
-
-        def fill(n):
-            for j in range(n):
-                nc.tensor.transpose(
-                    out=scratch[:, j % BANK_SLOTS, :], in_=identity[:], identity=identity[:]
-                )
-
-        def warm():
-            nc.tensor.matmul(
-                out=scratch[:].rearrange("p s x -> p (s x)"),
-                lhsT=identity[:],
-                rhs=priors_0[:, 0, 0:BANK_SLOTS, :].rearrange("p e x -> p (e x)"),
-                start=True,
-                stop=True,
-            )
 
         def at(i):
             return items[i] if 0 <= i < count else (-1, -1, -1)
 
-        for turn in range(count + 7):
-            passes = 0
+        def phase_end(turn, lag):
+            s, g, k = at(turn - lag)
+            if 0 <= s < PHASES - 1 and k == CHUNKS - 1:
+                return (s + 1, g)
+            return None
+
+        for turn in range(count + 9):
             if at(turn)[0] >= 1:
                 weigh_gpsimd(turn)
+            if 1 <= at(turn - 2)[0] < PHASES - 1:
+                flip_centre(turn - 2)
             if at(turn - 1)[0] >= 1:
                 sum_positions(turn - 1)
-                passes += CHUNK * POSITIONS
-            if 0 <= at(turn - 2)[0] < PHASES - 1:
-                subtract_and_square(turn - 2)
-            s, g, k = at(turn - 3)
-            if 0 <= s < PHASES - 1:
-                sum_channels(turn - 3)
-                passes += CHUNK * POSITIONS
-                if k == CHUNKS - 1:
-                    pulls(s, g)
+            if phase_end(turn, 5):
+                pulls(*phase_end(turn, 5))
+            if phase_end(turn, 6):
+                copy_first_pulls(*phase_end(turn, 6))
+            if phase_end(turn, 7):
+                copy_second_pulls(*phase_end(turn, 7))
+            if 0 <= at(turn - 3)[0] < PHASES - 1:
+                subtract_and_square(turn - 3)
+            if 0 <= at(turn - 4)[0] < PHASES - 1:
+                sum_channels(turn - 4)
+            if phase_end(turn, 5):
+                flip_first_pulls(*phase_end(turn, 5))
+            if phase_end(turn, 6):
+                flip_second_pulls(*phase_end(turn, 6))
+                scale_of_pulls(*phase_end(turn, 6))
+            if phase_end(turn, 7):
+                flip_third_pulls(*phase_end(turn, 7))
+            if at(turn)[0] >= 1:
+                weigh_vector(turn)
             if at(turn - 1)[0] >= 1:
                 normalise(turn - 1)
                 if at(turn - 1)[0] == PHASES - 1:
                     store(turn - 1)
-                else:
-                    flip_centre(turn - 1)
-                    passes += CHUNK
-            s, g, k = at(turn - 4)
-            if 0 <= s < PHASES - 1 and k == CHUNKS - 1:
-                pulls_first_part(s + 1, g)
-                passes += BANK_SLOTS
-            s, g, k = at(turn - 5)
-            if 0 <= s < PHASES - 1 and k == CHUNKS - 1:
-                pulls_second_part(s + 1, g)
-                passes += GPSIMD_POSITIONS[s + 1] - BANK_SLOTS
-            s, g, k = at(turn - 6)
-            if 0 <= s < PHASES - 1 and k == CHUNKS - 1:
-                pulls_third_part(s + 1, g)
-                passes += POSITIONS - GPSIMD_POSITIONS[s + 1]
-            if turn < count:
-                if turn % WARM_EVERY == 0:
-                    warm()
-                    passes += WARM_WORTH
-                fill(max(0, TURN_PASSES[at(turn)[0]] - passes))
-            if at(turn)[0] >= 1:
-                weigh_vector(turn)

@@ -7,6 +7,7 @@ F32 = mybir.dt.float32
 BF16 = mybir.dt.bfloat16
 U32 = mybir.dt.uint32
 U8 = mybir.dt.uint8
+I32 = mybir.dt.int32
 FP8X4 = mybir.dt.float8_e4m3fn_x4
 ALU = mybir.AluOpType
 ACT = mybir.ActivationFunctionType
@@ -32,6 +33,7 @@ PHASES = 4
 BANK_SLOTS = 4
 BANK = 2048
 GPSIMD_POSITIONS = (0, 6, 6, 5)
+POSITION_ORDER = (1, 7, 4, 0, 6, 3, 2, 8, 5)
 
 FLOPS = 2 * POSITIONS * SIDE * SIDE * (P * PACK) * FEATURES
 
@@ -39,10 +41,11 @@ PRIOR_BYTES = POSITIONS * CHANNELS * LANES * 4
 WORK_BYTES = POSITIONS * CHUNK * LANES * 4
 AT_PRIORS = 0
 AT_RAW_IMAGE = PRIOR_BYTES
-AT_SHIFTED = AT_RAW_IMAGE + PACK * SIDE * SIDE * 2
-AT_RAW_WEIGHT = AT_SHIFTED + 2 * PADDED_ROWS * SIDE * PACK * 2
+AT_PADDED = AT_RAW_IMAGE + PACK * SIDE * SIDE * 2
+AT_RAW_WEIGHT = AT_PADDED + PADDED_ROWS * SIDE * PACK * 2
 AT_GROUPED = AT_RAW_WEIGHT + 4 * PACK * FEATURES * 2
-AT_BIAS_ROWS = AT_GROUPED + 2 * PACK * FEATURES * 2
+AT_BIAS_TABLE = AT_GROUPED + 2 * PACK * FEATURES * 2
+AT_ONES = AT_BIAS_TABLE + FEATURES * 2
 AT_REST = 2 * PRIOR_BYTES
 AT_WEIGHT_CODES = AT_REST
 AT_WEIGHT_SCALES = AT_WEIGHT_CODES + POSITIONS * FEATURES * 4
@@ -59,44 +62,48 @@ AT_PULL_FLIPPED = AT_DIFFERENCE + 3 * WORK_BYTES
 AT_PULL = AT_PULL_FLIPPED + 2 * POSITIONS * LANES * 4
 
 
-def quantise_image(nc, arena, image, even_codes, even_scales, odd_codes, odd_scales):
+def quantise_image(nc, arena, image, even_codes, even_scales):
     raw_image = arena.tile([P, PACK, SIDE, SIDE], BF16, offset=AT_RAW_IMAGE)
     nc.sync.dma_start(out=raw_image[:], in_=image[0].rearrange("(p j) h w -> p j h w", j=PACK))
-    row = SIDE * PACK
+    padded = arena.tile([P, PADDED_ROWS, SIDE, PACK], BF16, align_bytes=64, offset=AT_PADDED)
+    nc.vector.memset(padded[:, 0, :, :], 0.0)
+    nc.vector.memset(padded[:, PADDED_ROWS - 1, :, :], 0.0)
+    nc.vector.memset(even_scales[:].rearrange("p k x -> p (k x)").bitcast(I32), 0)
+    nc.vector.tensor_copy(
+        out=padded[:, 1 : SIDE + 1, :, :], in_=raw_image[:].rearrange("p j h w -> p h w j")
+    )
+    flat = padded[:].rearrange("p r w j -> p (r w j)")
     whole = SIDE * SIDE
     rest = (PADDED_ROWS - SIDE) * SIDE
-    for kj in range(KERNEL):
-        shifted = arena.tile(
-            [P, PADDED_ROWS, SIDE, PACK], BF16, align_bytes=64, bufs=2, offset=AT_SHIFTED
-        )
-        nc.vector.memset(shifted[:, 0, :, :], 0.0)
-        nc.vector.memset(shifted[:, PADDED_ROWS - 1, :, :], 0.0)
-        first = max(0, 1 - kj)
-        last = min(SIDE, SIDE + 1 - kj)
-        if first > 0:
-            nc.vector.memset(shifted[:, 1 : SIDE + 1, 0, :], 0.0)
-        if last < SIDE:
-            nc.vector.memset(shifted[:, 1 : SIDE + 1, SIDE - 1, :], 0.0)
-        nc.vector.tensor_copy(
-            out=shifted[:, 1 : SIDE + 1, first:last, :],
-            in_=raw_image[:, :, :, first + kj - 1 : last + kj - 1].rearrange("p j h w -> p h w j"),
-        )
-        flat = shifted[:].rearrange("p r w j -> p (r w j)")
-        nc.vector.quantize_mx(
-            out=even_codes[:, kj, 0:whole].bitcast(FP8X4),
-            scales=even_scales[:, kj, 0:whole],
-            in_=flat[:, 0 : whole * PACK],
-        )
-        nc.vector.quantize_mx(
-            out=even_codes[:, kj, whole : whole + rest].bitcast(FP8X4),
-            scales=even_scales[:, kj, whole : whole + rest],
-            in_=flat[:, whole * PACK : (whole + rest) * PACK],
-        )
-        nc.vector.quantize_mx(
-            out=odd_codes[:, kj, :].bitcast(FP8X4),
-            scales=odd_scales[:, kj, :],
-            in_=flat[:, row : row + whole * PACK],
-        )
+    nc.vector.quantize_mx(
+        out=even_codes[:, 1, 0:whole].bitcast(FP8X4),
+        scales=even_scales[:, 1, 0:whole],
+        in_=flat[:, 0 : whole * PACK],
+    )
+    nc.vector.quantize_mx(
+        out=even_codes[:, 1, whole : whole + rest].bitcast(FP8X4),
+        scales=even_scales[:, 1, whole : whole + rest],
+        in_=flat[:, whole * PACK : (whole + rest) * PACK],
+    )
+
+
+def shift_columns(nc, kj, even_codes, even_scales):
+    pixels = PADDED_ROWS * SIDE
+    to, source = (slice(1, pixels), slice(0, pixels - 1)) if kj == 0 else (slice(0, pixels - 1), slice(1, pixels))
+    empty = 0 if kj == 0 else SIDE - 1
+    nc.vector.tensor_copy(
+        out=even_codes[:, kj, to].bitcast(I32), in_=even_codes[:, 1, source].bitcast(I32)
+    )
+    nc.vector.memset(
+        even_codes[:, kj, :].bitcast(I32).rearrange("p (r w) -> p r w", w=SIDE)[:, :, empty : empty + 1], 0
+    )
+    nc.vector.tensor_copy(out=even_scales[:, kj, to], in_=even_scales[:, 1, source])
+
+
+def shift_rows(nc, kj, even_codes, even_scales, odd_codes, odd_scales):
+    rows = slice(SIDE, SIDE + SIDE * SIDE)
+    nc.vector.tensor_copy(out=odd_codes[:, kj, :].bitcast(I32), in_=even_codes[:, kj, rows].bitcast(I32))
+    nc.vector.tensor_copy(out=odd_scales[:, kj, :].bitcast(I32), in_=even_scales[:, kj, rows].bitcast(I32))
 
 
 def quantise_weight(nc, arena, weight, t, weight_codes, weight_scales):
@@ -105,16 +112,12 @@ def quantise_weight(nc, arena, weight, t, weight_codes, weight_scales):
         out=raw_weight[:],
         in_=weight[0, 0, 0, t // KERNEL, t % KERNEL].rearrange("(p j) n -> p j n", j=PACK),
     )
-    grouped = arena.tile(
-        [P, CHANNELS, CAPSULES, PACK], BF16, align_bytes=64, bufs=2, offset=AT_GROUPED
-    )
-    nc.scalar.copy(
-        out=grouped[:], in_=raw_weight[:].rearrange("p j (c e) -> p e c j", e=CHANNELS)
-    )
+    grouped = arena.tile([P, FEATURES, PACK], BF16, align_bytes=64, bufs=2, offset=AT_GROUPED)
+    nc.scalar.copy(out=grouped[:], in_=raw_weight[:].rearrange("p j n -> p n j"))
     nc.vector.quantize_mx(
         out=weight_codes[:, t, :].bitcast(FP8X4),
         scales=weight_scales[:, t, :],
-        in_=grouped[:].rearrange("p e c j -> p (e c j)"),
+        in_=grouped[:].rearrange("p n j -> p (n j)"),
     )
 
 
@@ -148,9 +151,10 @@ def tile_capsulelayer_kernel(tc, image, weight, bias, out):
         )
         odd_codes = arena.tile([P, KERNEL, SIDE * SIDE], U32, align_bytes=64, offset=AT_ODD_CODES)
         odd_scales = arena.tile([P, KERNEL, SIDE * SIDE], U8, align_bytes=64, offset=AT_ODD_SCALES)
-        bias_rows = arena.tile([P, POSITIONS, CAPSULES, CHANNELS], BF16, offset=AT_BIAS_ROWS)
-        bias_tile = arena.tile([P, POSITIONS, CHANNELS, CAPSULES], BF16, offset=AT_BIAS)
-        bias_mean = arena.tile([P, CHANNELS, CAPSULES], F32, offset=AT_BIAS_MEAN)
+        bias_rows = arena.tile([P, POSITIONS, CAPSULES, CHANNELS], BF16, offset=AT_BIAS)
+        bias_mean = arena.tile([P, CAPSULES, CHANNELS], F32, offset=AT_BIAS_MEAN)
+        bias_table = arena.tile([P, FEATURES], BF16, offset=AT_BIAS_TABLE)
+        ones = arena.tile([P, P], BF16, offset=AT_ONES)
         identity = small.tile([P, P], F32, bufs=1)
         eps = small.tile([P, 1], F32, bufs=1)
 
@@ -164,13 +168,13 @@ def tile_capsulelayer_kernel(tc, image, weight, bias, out):
             else:
                 pixels = slice(P * m + SIDE * ki, P * m + SIDE * ki + P)
                 codes, scales = even_codes[:, kj, pixels], even_scales[:, kj, pixels]
-            product = banks.tile([P, CHANNELS, CAPSULES], F32, bufs=3, offset=0)
+            product = banks.tile([P, CAPSULES, CHANNELS], F32, bufs=3, offset=0)
             products[(m, t)] = product
-            if t == 0:
-                product_sum = banks.tile([P, CHANNELS, CAPSULES], F32, bufs=4, offset=3 * BANK)
+            if t == POSITION_ORDER[0]:
+                product_sum = banks.tile([P, CAPSULES, CHANNELS], F32, bufs=4, offset=3 * BANK)
                 totals[m] = product_sum
             nc.tensor.matmul_mx(
-                out=product[:].rearrange("p e c -> p (e c)"),
+                out=product[:].rearrange("p c e -> p (c e)"),
                 lhsT=codes.bitcast(FP8X4),
                 lhsT_scale=scales,
                 rhs=weight_codes[:, t, :].bitcast(FP8X4),
@@ -179,13 +183,13 @@ def tile_capsulelayer_kernel(tc, image, weight, bias, out):
                 stop=True,
             )
             nc.tensor.matmul_mx(
-                out=totals[m][:].rearrange("p e c -> p (e c)"),
+                out=totals[m][:].rearrange("p c e -> p (c e)"),
                 lhsT=codes.bitcast(FP8X4),
                 lhsT_scale=scales,
                 rhs=weight_codes[:, t, :].bitcast(FP8X4),
                 rhs_scale=weight_scales[:, t, :],
-                start=(t == 0),
-                stop=(t == POSITIONS - 1),
+                start=(t == POSITION_ORDER[0]),
+                stop=(t == POSITION_ORDER[-1]),
             )
 
         def add_bias(m, t):
@@ -193,16 +197,16 @@ def tile_capsulelayer_kernel(tc, image, weight, bias, out):
             lanes = slice(CAPSULES * lane, CAPSULES * lane + CAPSULES)
             nc.vector.tensor_tensor(
                 out=priors_of[g][:, t, :, lanes],
-                in0=products[(m, t)][:],
-                in1=bias_tile[:, t, :, :],
+                in0=products[(m, t)][:].rearrange("p c e -> p e c"),
+                in1=bias_rows[:, t, :, :].rearrange("p c e -> p e c"),
                 op=ALU.add,
             )
-            if t == POSITIONS - 1:
+            if t == POSITION_ORDER[-1]:
                 nc.vector.scalar_tensor_tensor(
                     out=mean_of[g][:, :, lanes],
-                    in0=totals[m][:],
+                    in0=totals[m][:].rearrange("p c e -> p e c"),
                     scalar=1.0 / POSITIONS,
-                    in1=bias_mean[:],
+                    in1=bias_mean[:].rearrange("p c e -> p e c"),
                     op0=ALU.mult,
                     op1=ALU.add,
                 )
@@ -211,20 +215,34 @@ def tile_capsulelayer_kernel(tc, image, weight, bias, out):
             out=bias_rows[:].rearrange("p t c e -> p (t c e)"),
             in_=bias[0, 0, 0].rearrange("i j o n -> (i j o n)").partition_broadcast(P),
         )
+        nc.gpsimd.memset(bias_table[:], 0.0)
+        nc.gpsimd.memset(ones[:], 1.0)
+        nc.scalar.dma_start(
+            out=bias_table[0:POSITIONS, :], in_=bias[0, 0, 0].rearrange("i j o n -> (i j o) n")
+        )
         make_identity(nc, identity[:])
         nc.vector.memset(eps[:], EPS)
-        nc.gpsimd.tensor_copy(out=bias_tile[:], in_=bias_rows[:].rearrange("p t c e -> p t e c"))
-        quantise_image(nc, arena, image, even_codes, even_scales, odd_codes, odd_scales)
-        nc.vector.tensor_reduce(
-            out=bias_mean[:], in_=bias_tile[:].rearrange("p t e c -> p e c t"), axis=X_AXIS, op=ALU.add
+        quantise_image(nc, arena, image, even_codes, even_scales)
+        bias_sum = banks.tile([P, CAPSULES, CHANNELS], F32, offset=7 * BANK)
+        nc.tensor.matmul(
+            out=bias_sum[:].rearrange("p c e -> p (c e)"),
+            lhsT=ones[:],
+            rhs=bias_table[:],
+            start=True,
+            stop=True,
         )
-        nc.vector.tensor_scalar_mul(out=bias_mean[:], in0=bias_mean[:], scalar1=1.0 / POSITIONS)
-        for t in range(POSITIONS):
+        nc.scalar.activation(out=bias_mean[:], in_=bias_sum[:], func=ACT.Copy, scale=1.0 / POSITIONS)
+        for t in POSITION_ORDER:
+            ki, kj = divmod(t, KERNEL)
+            if ki == 0 and kj != 1:
+                shift_columns(nc, kj, even_codes, even_scales)
+            if ki == 1:
+                shift_rows(nc, kj, even_codes, even_scales, odd_codes, odd_scales)
             quantise_weight(nc, arena, weight, t, weight_codes, weight_scales)
             for m in range(GROUP_TILES):
                 multiply(m, t)
                 add_bias(m, t)
-        for t in range(POSITIONS):
+        for t in POSITION_ORDER:
             for m in range(GROUP_TILES, 2 * GROUP_TILES):
                 multiply(m, t)
                 add_bias(m, t)

@@ -34,6 +34,7 @@ BANK_SLOTS = 4
 BANK = 2048
 GPSIMD_POSITIONS = (0, 6, 6, 5)
 POSITION_ORDER = (1, 7, 4, 0, 6, 3, 2, 8, 5)
+SCALAR_BIASES = 5
 
 FLOPS = 2 * POSITIONS * SIDE * SIDE * (P * PACK) * FEATURES
 
@@ -62,13 +63,7 @@ AT_PULL_FLIPPED = AT_DIFFERENCE + 3 * WORK_BYTES
 AT_PULL = AT_PULL_FLIPPED + 2 * POSITIONS * LANES * 4
 
 
-def quantise_image(nc, arena, image, even_codes, even_scales):
-    raw_image = arena.tile([P, PACK, SIDE, SIDE], BF16, offset=AT_RAW_IMAGE)
-    nc.sync.dma_start(out=raw_image[:], in_=image[0].rearrange("(p j) h w -> p j h w", j=PACK))
-    padded = arena.tile([P, PADDED_ROWS, SIDE, PACK], BF16, align_bytes=64, offset=AT_PADDED)
-    nc.vector.memset(padded[:, 0, :, :], 0.0)
-    nc.vector.memset(padded[:, PADDED_ROWS - 1, :, :], 0.0)
-    nc.vector.memset(even_scales[:].rearrange("p k x -> p (k x)").bitcast(I32), 0)
+def quantise_image(nc, raw_image, padded, even_codes, even_scales):
     nc.vector.tensor_copy(
         out=padded[:, 1 : SIDE + 1, :, :], in_=raw_image[:].rearrange("p j h w -> p h w j")
     )
@@ -151,8 +146,9 @@ def tile_capsulelayer_kernel(tc, image, weight, bias, out):
         )
         odd_codes = arena.tile([P, KERNEL, SIDE * SIDE], U32, align_bytes=64, offset=AT_ODD_CODES)
         odd_scales = arena.tile([P, KERNEL, SIDE * SIDE], U8, align_bytes=64, offset=AT_ODD_SCALES)
-        bias_rows = arena.tile([P, POSITIONS, CAPSULES, CHANNELS], BF16, offset=AT_BIAS)
-        bias_mean = arena.tile([P, CAPSULES, CHANNELS], F32, offset=AT_BIAS_MEAN)
+        bias_tile = arena.tile([P, POSITIONS, CHANNELS, CAPSULES], BF16, offset=AT_BIAS)
+        bias_mean = arena.tile([P, CHANNELS, CAPSULES], F32, offset=AT_BIAS_MEAN)
+        selector = arena.tile([P, P], BF16, offset=AT_ONES + P * 2)
         bias_table = arena.tile([P, FEATURES], BF16, offset=AT_BIAS_TABLE)
         ones = arena.tile([P, P], BF16, offset=AT_ONES)
         identity = small.tile([P, P], F32, bufs=1)
@@ -198,7 +194,7 @@ def tile_capsulelayer_kernel(tc, image, weight, bias, out):
             nc.vector.tensor_tensor(
                 out=priors_of[g][:, t, :, lanes],
                 in0=products[(m, t)][:].rearrange("p c e -> p e c"),
-                in1=bias_rows[:, t, :, :].rearrange("p c e -> p e c"),
+                in1=bias_tile[:, t, :, :],
                 op=ALU.add,
             )
             if t == POSITION_ORDER[-1]:
@@ -206,23 +202,42 @@ def tile_capsulelayer_kernel(tc, image, weight, bias, out):
                     out=mean_of[g][:, :, lanes],
                     in0=totals[m][:].rearrange("p c e -> p e c"),
                     scalar=1.0 / POSITIONS,
-                    in1=bias_mean[:].rearrange("p c e -> p e c"),
+                    in1=bias_mean[:],
                     op0=ALU.mult,
                     op1=ALU.add,
                 )
 
-        nc.scalar.dma_start(
-            out=bias_rows[:].rearrange("p t c e -> p (t c e)"),
-            in_=bias[0, 0, 0].rearrange("i j o n -> (i j o n)").partition_broadcast(P),
-        )
-        nc.gpsimd.memset(bias_table[:], 0.0)
-        nc.gpsimd.memset(ones[:], 1.0)
-        nc.scalar.dma_start(
+        nc.vector.memset(bias_table[:], 0.0)
+        nc.sync.dma_start(
             out=bias_table[0:POSITIONS, :], in_=bias[0, 0, 0].rearrange("i j o n -> (i j o) n")
         )
+        raw_image = arena.tile([P, PACK, SIDE, SIDE], BF16, offset=AT_RAW_IMAGE)
+        nc.sync.dma_start(out=raw_image[:], in_=image[0].rearrange("(p j) h w -> p j h w", j=PACK))
+        make_identity(nc, selector[:])
+        nc.gpsimd.memset(ones[:], 1.0)
         make_identity(nc, identity[:])
         nc.vector.memset(eps[:], EPS)
-        quantise_image(nc, arena, image, even_codes, even_scales)
+        padded = arena.tile([P, PADDED_ROWS, SIDE, PACK], BF16, align_bytes=64, offset=AT_PADDED)
+        nc.vector.memset(padded[:, 0, :, :], 0.0)
+        nc.vector.memset(padded[:, PADDED_ROWS - 1, :, :], 0.0)
+        nc.vector.memset(even_scales[:].rearrange("p k x -> p (k x)").bitcast(I32), 0)
+
+        def spread_bias(t, engine_copy):
+            product = banks.tile([P, CAPSULES, CHANNELS], F32, bufs=3, offset=0)
+            nc.tensor.matmul(
+                out=product[:].rearrange("p c e -> p (c e)"),
+                lhsT=selector[:, t : t + 1].to_broadcast([P, P]),
+                rhs=bias_table[:],
+                start=True,
+                stop=True,
+            )
+            engine_copy(out=bias_tile[:, t, :, :], in_=product[:].rearrange("p c e -> p e c"))
+
+        for t in POSITION_ORDER[0:SCALAR_BIASES]:
+            spread_bias(t, nc.scalar.copy)
+        quantise_image(nc, raw_image, padded, even_codes, even_scales)
+        for t in POSITION_ORDER[SCALAR_BIASES:]:
+            spread_bias(t, nc.vector.tensor_copy)
         bias_sum = banks.tile([P, CAPSULES, CHANNELS], F32, offset=7 * BANK)
         nc.tensor.matmul(
             out=bias_sum[:].rearrange("p c e -> p (c e)"),
@@ -231,7 +246,12 @@ def tile_capsulelayer_kernel(tc, image, weight, bias, out):
             start=True,
             stop=True,
         )
-        nc.scalar.activation(out=bias_mean[:], in_=bias_sum[:], func=ACT.Copy, scale=1.0 / POSITIONS)
+        nc.scalar.activation(
+            out=bias_mean[:],
+            in_=bias_sum[:].rearrange("p c e -> p e c"),
+            func=ACT.Copy,
+            scale=1.0 / POSITIONS,
+        )
         for t in POSITION_ORDER:
             ki, kj = divmod(t, KERNEL)
             if ki == 0 and kj != 1:

@@ -61,6 +61,11 @@ AT_WEIGHED = AT_REST
 AT_DIFFERENCE = AT_WEIGHED + 3 * WORK_BYTES
 AT_PULL_FLIPPED = AT_DIFFERENCE + 3 * WORK_BYTES
 AT_PULL = AT_PULL_FLIPPED + 2 * POSITIONS * LANES * 4
+AT_SMALL = AT_MEAN + 2 * CHANNELS * LANES * 4
+AT_RESULT = AT_SMALL
+AT_CENTRE_FLIPPED = AT_RESULT + 4 * CHUNK * P * 4
+AT_PULL_SUM = AT_CENTRE_FLIPPED + 3 * CHUNK * P * 4
+AT_PULL_SCALE = AT_PULL_SUM + 2 * P * 4
 
 
 def quantise_image(nc, raw_image, padded, even_codes, even_scales):
@@ -129,9 +134,12 @@ def tile_capsulelayer_kernel(tc, image, weight, bias, out):
         priors_0 = arena.tile([P, POSITIONS, CHANNELS, LANES], F32, offset=AT_PRIORS)
         priors_1 = arena.tile([P, POSITIONS, CHANNELS, LANES], F32, offset=AT_PRIORS + PRIOR_BYTES)
         priors_of = (priors_0, priors_1)
-        mean_0 = arena.tile([P, CHANNELS, LANES], F32, offset=AT_MEAN)
-        mean_1 = arena.tile([P, CHANNELS, LANES], F32, offset=AT_MEAN + CHANNELS * LANES * 4)
+        mean_0 = arena.tile([P, CHANNELS, LANES], F32, offset=AT_SMALL)
+        mean_1 = arena.tile([P, CHANNELS, LANES], F32, offset=AT_WEIGHED)
         mean_of = (mean_0, mean_1)
+        mean_flipped_0 = arena.tile([P, CHANNELS, P], F32, offset=AT_MEAN)
+        mean_flipped_1 = arena.tile([P, CHANNELS, P], F32, offset=AT_MEAN + CHANNELS * P * 4)
+        mean_flipped_of = (mean_flipped_0, mean_flipped_1)
         weight_codes = arena.tile(
             [P, POSITIONS, FEATURES], U32, align_bytes=64, offset=AT_WEIGHT_CODES
         )
@@ -207,6 +215,22 @@ def tile_capsulelayer_kernel(tc, image, weight, bias, out):
                     op1=ALU.add,
                 )
 
+        def flip_mean(g, q):
+            if g == 0:
+                flipped_mean = banks.tile([P, BANK_SLOTS, P], F32, tag="product", bufs=3, offset=0)
+            else:
+                flipped_mean = banks.tile([P, BANK_SLOTS, P], F32, tag="weighted_sum", offset=3 * BANK)
+            for c in range(BANK_SLOTS):
+                nc.tensor.transpose(
+                    out=flipped_mean[:, c, :],
+                    in_=mean_of[g][:, BANK_SLOTS * q + c, :],
+                    identity=identity[:],
+                )
+            nc.scalar.copy(
+                out=mean_flipped_of[g][:, BANK_SLOTS * q : BANK_SLOTS * q + BANK_SLOTS, :],
+                in_=flipped_mean[:],
+            )
+
         nc.vector.memset(bias_table[:], 0.0)
         nc.sync.dma_start(
             out=bias_table[0:POSITIONS, :], in_=bias[0, 0, 0].rearrange("i j o n -> (i j o) n")
@@ -266,6 +290,8 @@ def tile_capsulelayer_kernel(tc, image, weight, bias, out):
             for m in range(GROUP_TILES, 2 * GROUP_TILES):
                 multiply(m, t)
                 add_bias(m, t)
+                if t == POSITION_ORDER[0]:
+                    flip_mean(0, m - GROUP_TILES)
 
         items = [(s, g, k) for s in range(PHASES) for g in range(GROUPS) for k in range(CHUNKS)]
         weighed_of, total_of, centre_flipped_of, centre_of, difference_of = {}, {}, {}, {}, {}
@@ -317,9 +343,11 @@ def tile_capsulelayer_kernel(tc, image, weight, bias, out):
         def normalise(i):
             s, g, k = items[i]
             if s == PHASES - 1:
-                centre_flipped = small.tile([P, CHUNK, P], F32, bufs=4, tag="result")
+                centre_flipped = arena.tile([P, CHUNK, P], F32, bufs=4, tag="result", offset=AT_RESULT)
             else:
-                centre_flipped = small.tile([P, CHUNK, P], F32, bufs=3, tag="centre_flipped")
+                centre_flipped = arena.tile(
+                    [P, CHUNK, P], F32, bufs=3, tag="centre_flipped", offset=AT_CENTRE_FLIPPED
+                )
             centre_flipped_of[i] = centre_flipped
             nc.vector.tensor_tensor(
                 out=centre_flipped[:],
@@ -338,19 +366,19 @@ def tile_capsulelayer_kernel(tc, image, weight, bias, out):
                 )
 
         def flip_centre(i):
+            s, g, k = items[i]
             centre = banks.tile([P, BANK_SLOTS, LANES], F32, bufs=2, offset=6 * BANK)
             centre_of[i] = centre
             for c in range(CHUNK):
-                nc.tensor.transpose(
-                    out=centre[:, c, :], in_=centre_flipped_of[i][:, c, :], identity=identity[:]
-                )
+                if s == 0:
+                    flipped = mean_flipped_of[g][:, CHUNK * k + c, :]
+                else:
+                    flipped = centre_flipped_of[i][:, c, :]
+                nc.tensor.transpose(out=centre[:, c, :], in_=flipped, identity=identity[:])
 
         def subtract_and_square(i):
             s, g, k = items[i]
-            if s == 0:
-                centre = mean_of[g][:, CHUNK * k : CHUNK * k + CHUNK, :]
-            else:
-                centre = centre_of[i][:, 0:CHUNK, :]
+            centre = centre_of[i][:, 0:CHUNK, :]
             difference = arena.tile([P, POSITIONS, CHUNK, LANES], F32, bufs=3, offset=AT_DIFFERENCE)
             difference_of[i] = difference
             nc.vector.tensor_tensor(
@@ -402,14 +430,14 @@ def tile_capsulelayer_kernel(tc, image, weight, bias, out):
                 )
 
         def scale_of_pulls(s, g):
-            pull_sum = small.tile([P, P], F32)
+            pull_sum = arena.tile([P, P], F32, bufs=2, offset=AT_PULL_SUM)
             nc.vector.tensor_reduce(
                 out=pull_sum[:],
                 in_=pull_flipped_of[(s, g)][:].rearrange("p t x -> p x t"),
                 axis=X_AXIS,
                 op=ALU.add,
             )
-            pull_scale = small.tile([P, P], F32)
+            pull_scale = arena.tile([P, P], F32, bufs=2, offset=AT_PULL_SCALE)
             pull_scale_of[(s, g)] = pull_scale
             nc.vector.reciprocal(out=pull_scale[:], in_=pull_sum[:])
 
@@ -456,7 +484,9 @@ def tile_capsulelayer_kernel(tc, image, weight, bias, out):
         for turn in range(count + 9):
             if at(turn)[0] >= 1:
                 weigh_gpsimd(turn)
-            if 1 <= at(turn - 2)[0] < PHASES - 1:
+            if 2 <= turn < 2 + CHANNELS // BANK_SLOTS:
+                flip_mean(1, turn - 2)
+            if 0 <= at(turn - 2)[0] < PHASES - 1:
                 flip_centre(turn - 2)
             if at(turn - 1)[0] >= 1:
                 sum_positions(turn - 1)

@@ -32,7 +32,10 @@ CHUNKS = CHANNELS // CHUNK
 PHASES = 4
 BANK_SLOTS = 4
 BANK = 2048
-GPSIMD_POSITIONS = (0, 6, 6, 5)
+FIRST_IN_PSUM = (9, 6, 6, 5)
+IN_SBUF = (0, 7, 7, 5)
+LAST_SHARE = 3
+LATE_FROM = 5
 POSITION_ORDER = (1, 7, 4, 0, 6, 3, 2, 8, 5)
 SCALAR_BIASES = 5
 
@@ -134,9 +137,6 @@ def tile_capsulelayer_kernel(tc, image, weight, bias, out):
         priors_0 = arena.tile([P, POSITIONS, CHANNELS, LANES], F32, offset=AT_PRIORS)
         priors_1 = arena.tile([P, POSITIONS, CHANNELS, LANES], F32, offset=AT_PRIORS + PRIOR_BYTES)
         priors_of = (priors_0, priors_1)
-        mean_0 = arena.tile([P, CHANNELS, LANES], F32, offset=AT_SMALL)
-        mean_1 = arena.tile([P, CHANNELS, LANES], F32, offset=AT_WEIGHED)
-        mean_of = (mean_0, mean_1)
         mean_flipped_0 = arena.tile([P, CHANNELS, P], F32, offset=AT_MEAN)
         mean_flipped_1 = arena.tile([P, CHANNELS, P], F32, offset=AT_MEAN + CHANNELS * P * 4)
         mean_flipped_of = (mean_flipped_0, mean_flipped_1)
@@ -155,14 +155,12 @@ def tile_capsulelayer_kernel(tc, image, weight, bias, out):
         odd_codes = arena.tile([P, KERNEL, SIDE * SIDE], U32, align_bytes=64, offset=AT_ODD_CODES)
         odd_scales = arena.tile([P, KERNEL, SIDE * SIDE], U8, align_bytes=64, offset=AT_ODD_SCALES)
         bias_tile = arena.tile([P, POSITIONS, CHANNELS, CAPSULES], BF16, offset=AT_BIAS)
-        bias_mean = arena.tile([P, CHANNELS, CAPSULES], F32, offset=AT_BIAS_MEAN)
         selector = arena.tile([P, P], BF16, offset=AT_ONES + P * 2)
         bias_table = arena.tile([P, FEATURES], BF16, offset=AT_BIAS_TABLE)
-        ones = arena.tile([P, P], BF16, offset=AT_ONES)
         identity = small.tile([P, P], F32, bufs=1)
         eps = small.tile([P, 1], F32, bufs=1)
 
-        products, totals = {}, {}
+        products, prior_sums = {}, {}
 
         def multiply(m, t):
             ki, kj = divmod(t, KERNEL)
@@ -172,11 +170,8 @@ def tile_capsulelayer_kernel(tc, image, weight, bias, out):
             else:
                 pixels = slice(P * m + SIDE * ki, P * m + SIDE * ki + P)
                 codes, scales = even_codes[:, kj, pixels], even_scales[:, kj, pixels]
-            product = banks.tile([P, CAPSULES, CHANNELS], F32, bufs=3, offset=0)
+            product = banks.tile([P, CAPSULES, CHANNELS], F32, bufs=4, offset=4 * BANK)
             products[(m, t)] = product
-            if t == POSITION_ORDER[0]:
-                product_sum = banks.tile([P, CAPSULES, CHANNELS], F32, bufs=4, offset=3 * BANK)
-                totals[m] = product_sum
             nc.tensor.matmul_mx(
                 out=product[:].rearrange("p c e -> p (c e)"),
                 lhsT=codes.bitcast(FP8X4),
@@ -185,15 +180,6 @@ def tile_capsulelayer_kernel(tc, image, weight, bias, out):
                 rhs_scale=weight_scales[:, t, :],
                 start=True,
                 stop=True,
-            )
-            nc.tensor.matmul_mx(
-                out=totals[m][:].rearrange("p c e -> p (c e)"),
-                lhsT=codes.bitcast(FP8X4),
-                lhsT_scale=scales,
-                rhs=weight_codes[:, t, :].bitcast(FP8X4),
-                rhs_scale=weight_scales[:, t, :],
-                start=(t == POSITION_ORDER[0]),
-                stop=(t == POSITION_ORDER[-1]),
             )
 
         def add_bias(m, t):
@@ -205,31 +191,33 @@ def tile_capsulelayer_kernel(tc, image, weight, bias, out):
                 in1=bias_tile[:, t, :, :],
                 op=ALU.add,
             )
-            if t == POSITION_ORDER[-1]:
-                nc.vector.scalar_tensor_tensor(
-                    out=mean_of[g][:, :, lanes],
-                    in0=totals[m][:].rearrange("p c e -> p e c"),
-                    scalar=1.0 / POSITIONS,
-                    in1=bias_mean[:],
-                    op0=ALU.mult,
-                    op1=ALU.add,
+
+        def add_to_sum(g, t):
+            if t == POSITION_ORDER[0]:
+                prior_sum_0 = banks.tile([P, BANK_SLOTS, P], F32, offset=0)
+                prior_sum_1 = banks.tile([P, BANK_SLOTS, P], F32, offset=BANK)
+                prior_sum_2 = banks.tile([P, BANK_SLOTS, P], F32, offset=2 * BANK)
+                prior_sum_3 = banks.tile([P, BANK_SLOTS, P], F32, offset=3 * BANK)
+                prior_sums[g] = (prior_sum_0, prior_sum_1, prior_sum_2, prior_sum_3)
+            for e in range(CHANNELS):
+                q, slot = divmod(e, BANK_SLOTS)
+                nc.tensor.matmul(
+                    out=prior_sums[g][q][:, slot, :],
+                    lhsT=priors_of[g][:, t, e, :],
+                    rhs=identity[:],
+                    is_transpose=True,
+                    start=(t == POSITION_ORDER[0] and slot == 0),
+                    stop=(t == POSITION_ORDER[-1] and slot == BANK_SLOTS - 1),
                 )
 
-        def flip_mean(g, q):
-            if g == 0:
-                flipped_mean = banks.tile([P, BANK_SLOTS, P], F32, tag="product", bufs=3, offset=0)
-            else:
-                flipped_mean = banks.tile([P, BANK_SLOTS, P], F32, tag="weighted_sum", offset=3 * BANK)
-            for c in range(BANK_SLOTS):
-                nc.tensor.transpose(
-                    out=flipped_mean[:, c, :],
-                    in_=mean_of[g][:, BANK_SLOTS * q + c, :],
-                    identity=identity[:],
+        def mean_prior(g):
+            for q in range(CHANNELS // BANK_SLOTS):
+                nc.scalar.activation(
+                    out=mean_flipped_of[g][:, BANK_SLOTS * q : BANK_SLOTS * q + BANK_SLOTS, :],
+                    in_=prior_sums[g][q][:],
+                    func=ACT.Copy,
+                    scale=1.0 / POSITIONS,
                 )
-            nc.scalar.copy(
-                out=mean_flipped_of[g][:, BANK_SLOTS * q : BANK_SLOTS * q + BANK_SLOTS, :],
-                in_=flipped_mean[:],
-            )
 
         nc.vector.memset(bias_table[:], 0.0)
         nc.sync.dma_start(
@@ -238,7 +226,6 @@ def tile_capsulelayer_kernel(tc, image, weight, bias, out):
         raw_image = arena.tile([P, PACK, SIDE, SIDE], BF16, offset=AT_RAW_IMAGE)
         nc.sync.dma_start(out=raw_image[:], in_=image[0].rearrange("(p j) h w -> p j h w", j=PACK))
         make_identity(nc, selector[:])
-        nc.gpsimd.memset(ones[:], 1.0)
         make_identity(nc, identity[:])
         nc.vector.memset(eps[:], EPS)
         padded = arena.tile([P, PADDED_ROWS, SIDE, PACK], BF16, align_bytes=64, offset=AT_PADDED)
@@ -247,7 +234,7 @@ def tile_capsulelayer_kernel(tc, image, weight, bias, out):
         nc.vector.memset(even_scales[:].rearrange("p k x -> p (k x)").bitcast(I32), 0)
 
         def spread_bias(t, engine_copy):
-            product = banks.tile([P, CAPSULES, CHANNELS], F32, bufs=3, offset=0)
+            product = banks.tile([P, CAPSULES, CHANNELS], F32, bufs=4, offset=4 * BANK)
             nc.tensor.matmul(
                 out=product[:].rearrange("p c e -> p (c e)"),
                 lhsT=selector[:, t : t + 1].to_broadcast([P, P]),
@@ -262,49 +249,46 @@ def tile_capsulelayer_kernel(tc, image, weight, bias, out):
         quantise_image(nc, raw_image, padded, even_codes, even_scales)
         for t in POSITION_ORDER[SCALAR_BIASES:]:
             spread_bias(t, nc.vector.tensor_copy)
-        bias_sum = banks.tile([P, CAPSULES, CHANNELS], F32, offset=7 * BANK)
-        nc.tensor.matmul(
-            out=bias_sum[:].rearrange("p c e -> p (c e)"),
-            lhsT=ones[:],
-            rhs=bias_table[:],
-            start=True,
-            stop=True,
-        )
-        nc.scalar.activation(
-            out=bias_mean[:],
-            in_=bias_sum[:].rearrange("p c e -> p e c"),
-            func=ACT.Copy,
-            scale=1.0 / POSITIONS,
-        )
-        for t in POSITION_ORDER:
+        def add_and_close(g, t):
+            add_to_sum(g, t)
+            if t == POSITION_ORDER[-1]:
+                mean_prior(g)
+
+        steps = [(g, t) for g in range(GROUPS) for t in POSITION_ORDER]
+        for i, (g, t) in enumerate(steps):
             ki, kj = divmod(t, KERNEL)
-            if ki == 0 and kj != 1:
-                shift_columns(nc, kj, even_codes, even_scales)
-            if ki == 1:
-                shift_rows(nc, kj, even_codes, even_scales, odd_codes, odd_scales)
-            quantise_weight(nc, arena, weight, t, weight_codes, weight_scales)
-            for m in range(GROUP_TILES):
+            if g == 0:
+                if ki == 0 and kj != 1:
+                    shift_columns(nc, kj, even_codes, even_scales)
+                if ki == 1:
+                    shift_rows(nc, kj, even_codes, even_scales, odd_codes, odd_scales)
+                quantise_weight(nc, arena, weight, t, weight_codes, weight_scales)
+            for m in range(GROUP_TILES * g, GROUP_TILES * g + GROUP_TILES):
                 multiply(m, t)
                 add_bias(m, t)
-        for t in POSITION_ORDER:
-            for m in range(GROUP_TILES, 2 * GROUP_TILES):
-                multiply(m, t)
-                add_bias(m, t)
-                if t == POSITION_ORDER[0]:
-                    flip_mean(0, m - GROUP_TILES)
+            if i > 0:
+                add_and_close(*steps[i - 1])
 
         items = [(s, g, k) for s in range(PHASES) for g in range(GROUPS) for k in range(CHUNKS)]
         weighed_of, total_of, centre_flipped_of, centre_of, difference_of = {}, {}, {}, {}, {}
         distance_banks = {}
-        pull_flipped_of, pull_scale_of, pull_sbuf_of, pull_psum_of = {}, {}, {}, {}
+        pull_flipped_of, pull_scale_of, pull_sbuf_of, pull_psum_of, late_pulls_of = {}, {}, {}, {}, {}
 
         def chunk_priors(i):
             s, g, k = items[i]
             return priors_of[g][:, :, CHUNK * k : CHUNK * k + CHUNK, :]
 
+        def gpsimd_share(i):
+            s, g, k = items[i]
+            if s == PHASES - 1 and (g == 1 or k >= LATE_FROM):
+                return LAST_SHARE
+            if s < PHASES - 1:
+                return FIRST_IN_PSUM[s] + k % 2
+            return FIRST_IN_PSUM[s]
+
         def weigh_gpsimd(i):
             s, g, k = items[i]
-            n = GPSIMD_POSITIONS[s]
+            n = gpsimd_share(i)
             weighed = arena.tile([P, POSITIONS, CHUNK, LANES], F32, bufs=3, offset=AT_WEIGHED)
             weighed_of[i] = weighed
             nc.gpsimd.tensor_tensor(
@@ -316,18 +300,27 @@ def tile_capsulelayer_kernel(tc, image, weight, bias, out):
 
         def weigh_vector(i):
             s, g, k = items[i]
-            n = GPSIMD_POSITIONS[s]
-            nc.vector.tensor_tensor(
-                out=weighed_of[i][:, n:POSITIONS, :, :],
-                in0=chunk_priors(i)[:, n:POSITIONS, :, :],
-                in1=pull_psum_of[(s, g)][:, 0 : POSITIONS - n, :]
-                .unsqueeze(2)
-                .to_broadcast([P, POSITIONS - n, CHUNK, LANES]),
-                op=ALU.mult,
-            )
+            n = gpsimd_share(i)
+            f = FIRST_IN_PSUM[s]
+            for first, last, base, pulls_in_psum in (
+                (n, f, n, late_pulls_of),
+                (max(n, f), POSITIONS, f, pull_psum_of),
+            ):
+                if first < last:
+                    nc.vector.tensor_tensor(
+                        out=weighed_of[i][:, first:last, :, :],
+                        in0=chunk_priors(i)[:, first:last, :, :],
+                        in1=pulls_in_psum[(s, g)][:, first - base : last - base, :]
+                        .unsqueeze(2)
+                        .to_broadcast([P, last - first, CHUNK, LANES]),
+                        op=ALU.mult,
+                    )
 
         def sum_positions(i):
-            weighted_sum = banks.tile([P, BANK_SLOTS, P], F32, offset=3 * BANK)
+            if items[i][0] == PHASES - 1 and i % 2 == 1:
+                weighted_sum = banks.tile([P, BANK_SLOTS, P], F32, tag="centre", bufs=2, offset=6 * BANK)
+            else:
+                weighted_sum = banks.tile([P, BANK_SLOTS, P], F32, offset=3 * BANK)
             total_of[i] = weighted_sum
             for c in range(CHUNK):
                 for t in range(POSITIONS):
@@ -449,17 +442,17 @@ def tile_capsulelayer_kernel(tc, image, weight, bias, out):
             flip_pulls(s, g, 0, BANK_SLOTS, passing)
 
         def copy_first_pulls(s, g):
-            pull_sbuf = arena.tile([P, 6, LANES], F32, bufs=2, offset=AT_PULL)
+            pull_sbuf = arena.tile([P, 7, LANES], F32, bufs=2, offset=AT_PULL)
             pull_sbuf_of[(s, g)] = pull_sbuf
             nc.scalar.copy(out=pull_sbuf[:, 0:BANK_SLOTS, :], in_=passing_of[(s, g)][:])
 
         def flip_second_pulls(s, g):
             passing = banks.tile([P, BANK_SLOTS, LANES], F32, tag="pulls%d" % g, offset=(4 + g) * BANK)
             passing_of[(s, g)] = passing
-            flip_pulls(s, g, BANK_SLOTS, GPSIMD_POSITIONS[s], passing)
+            flip_pulls(s, g, BANK_SLOTS, IN_SBUF[s], passing)
 
         def copy_second_pulls(s, g):
-            n = GPSIMD_POSITIONS[s]
+            n = IN_SBUF[s]
             nc.scalar.copy(
                 out=pull_sbuf_of[(s, g)][:, BANK_SLOTS:n, :],
                 in_=passing_of[(s, g)][:, 0 : n - BANK_SLOTS, :],
@@ -468,7 +461,12 @@ def tile_capsulelayer_kernel(tc, image, weight, bias, out):
         def flip_third_pulls(s, g):
             pull_psum = banks.tile([P, BANK_SLOTS, LANES], F32, tag="pulls%d" % g, offset=(4 + g) * BANK)
             pull_psum_of[(s, g)] = pull_psum
-            flip_pulls(s, g, GPSIMD_POSITIONS[s], POSITIONS, pull_psum)
+            flip_pulls(s, g, FIRST_IN_PSUM[s], POSITIONS, pull_psum)
+
+        def flip_late_pulls(s, g):
+            late_pulls = banks.tile([P, BANK_SLOTS, LANES], F32, tag="late_pulls%d" % g, offset=g * BANK)
+            late_pulls_of[(s, g)] = late_pulls
+            flip_pulls(s, g, LAST_SHARE, FIRST_IN_PSUM[s], late_pulls)
 
         count = len(items)
 
@@ -484,10 +482,10 @@ def tile_capsulelayer_kernel(tc, image, weight, bias, out):
         for turn in range(count + 9):
             if at(turn)[0] >= 1:
                 weigh_gpsimd(turn)
-            if 2 <= turn < 2 + CHANNELS // BANK_SLOTS:
-                flip_mean(1, turn - 2)
             if 0 <= at(turn - 2)[0] < PHASES - 1:
                 flip_centre(turn - 2)
+            if turn == 2:
+                add_and_close(*steps[-1])
             if at(turn - 1)[0] >= 1:
                 sum_positions(turn - 1)
             if phase_end(turn, 5):
@@ -507,6 +505,10 @@ def tile_capsulelayer_kernel(tc, image, weight, bias, out):
                 scale_of_pulls(*phase_end(turn, 6))
             if phase_end(turn, 7):
                 flip_third_pulls(*phase_end(turn, 7))
+            if phase_end(turn, 5) == (PHASES - 1, 1):
+                flip_late_pulls(PHASES - 1, 0)
+            if phase_end(turn, 6) == (PHASES - 1, 1):
+                flip_late_pulls(PHASES - 1, 1)
             if at(turn)[0] >= 1:
                 weigh_vector(turn)
             if at(turn - 1)[0] >= 1:

@@ -47,7 +47,7 @@ AT_PRIORS = 0
 AT_RAW_IMAGE = PRIOR_BYTES
 AT_PADDED = AT_RAW_IMAGE + PACK * SIDE * SIDE * 2
 AT_RAW_WEIGHT = AT_PADDED + PADDED_ROWS * SIDE * PACK * 2
-AT_GROUPED = AT_RAW_WEIGHT + 4 * PACK * FEATURES * 2
+AT_GROUPED = AT_RAW_WEIGHT + POSITIONS * PACK * FEATURES * 2
 AT_BIAS_TABLE = AT_GROUPED + 2 * PACK * FEATURES * 2
 AT_ONES = AT_BIAS_TABLE + FEATURES * 2
 AT_REST = 2 * PRIOR_BYTES
@@ -90,31 +90,45 @@ def quantise_image(nc, raw_image, padded, even_codes, even_scales):
     )
 
 
-def shift_columns(nc, kj, even_codes, even_scales):
+def move_codes(nc, even_codes, even_scales, odd_codes, odd_scales):
+    pixels = PADDED_ROWS * SIDE
+    whole = SIDE * SIDE
+    middle = even_codes[:, 1, :].bitcast(I32)
+    nc.sync.dma_start(out=odd_codes[:, 1, :].bitcast(I32), in_=middle[:, SIDE : SIDE + whole])
+    nc.sync.dma_start(
+        out=odd_scales[:, 1, :].bitcast(I32), in_=even_scales[:, 1, SIDE : SIDE + whole].bitcast(I32)
+    )
+    nc.sync.dma_start(out=even_codes[:, 0, 1:pixels].bitcast(I32), in_=middle[:, 0 : pixels - 1])
+    nc.sync.dma_start(out=odd_codes[:, 0, :].bitcast(I32), in_=middle[:, SIDE - 1 : SIDE - 1 + whole])
+    nc.sync.dma_start(out=even_codes[:, 2, 0 : pixels - 1].bitcast(I32), in_=middle[:, 1:pixels])
+    nc.sync.dma_start(out=odd_codes[:, 2, :].bitcast(I32), in_=middle[:, SIDE + 1 : SIDE + 1 + whole])
+
+
+def finish_shift(nc, kj, even_codes, even_scales, odd_codes, odd_scales):
     pixels = PADDED_ROWS * SIDE
     to, source = (slice(1, pixels), slice(0, pixels - 1)) if kj == 0 else (slice(0, pixels - 1), slice(1, pixels))
     empty = 0 if kj == 0 else SIDE - 1
-    nc.vector.tensor_copy(
-        out=even_codes[:, kj, to].bitcast(I32), in_=even_codes[:, 1, source].bitcast(I32)
-    )
-    nc.vector.memset(
-        even_codes[:, kj, :].bitcast(I32).rearrange("p (r w) -> p r w", w=SIDE)[:, :, empty : empty + 1], 0
-    )
+    for codes in (even_codes, odd_codes):
+        nc.vector.memset(
+            codes[:, kj, :].bitcast(I32).rearrange("p (r w) -> p r w", w=SIDE)[:, :, empty : empty + 1], 0
+        )
     nc.vector.tensor_copy(out=even_scales[:, kj, to], in_=even_scales[:, 1, source])
+    nc.sync.dma_start(
+        out=odd_scales[:, kj, :].bitcast(I32),
+        in_=even_scales[:, kj, SIDE : SIDE + SIDE * SIDE].bitcast(I32),
+    )
 
 
-def shift_rows(nc, kj, even_codes, even_scales, odd_codes, odd_scales):
-    rows = slice(SIDE, SIDE + SIDE * SIDE)
-    nc.vector.tensor_copy(out=odd_codes[:, kj, :].bitcast(I32), in_=even_codes[:, kj, rows].bitcast(I32))
-    nc.vector.tensor_copy(out=odd_scales[:, kj, :].bitcast(I32), in_=even_scales[:, kj, rows].bitcast(I32))
-
-
-def quantise_weight(nc, arena, weight, t, weight_codes, weight_scales):
-    raw_weight = arena.tile([P, PACK, FEATURES], BF16, bufs=4, offset=AT_RAW_WEIGHT)
+def load_weight(nc, arena, weight, t):
+    raw_weight = arena.tile([P, PACK, FEATURES], BF16, bufs=POSITIONS, offset=AT_RAW_WEIGHT)
     nc.sync.dma_start(
         out=raw_weight[:],
         in_=weight[0, 0, 0, t // KERNEL, t % KERNEL].rearrange("(p j) n -> p j n", j=PACK),
     )
+    return raw_weight
+
+
+def quantise_weight(nc, arena, raw_weight, t, weight_codes, weight_scales):
     grouped = arena.tile([P, FEATURES, PACK], BF16, align_bytes=64, bufs=2, offset=AT_GROUPED)
     nc.scalar.copy(out=grouped[:], in_=raw_weight[:].rearrange("p j n -> p n j"))
     nc.vector.quantize_mx(
@@ -225,6 +239,9 @@ def tile_capsulelayer_kernel(tc, image, weight, bias, out):
         )
         raw_image = arena.tile([P, PACK, SIDE, SIDE], BF16, offset=AT_RAW_IMAGE)
         nc.sync.dma_start(out=raw_image[:], in_=image[0].rearrange("(p j) h w -> p j h w", j=PACK))
+        raw_weight_of = {}
+        for t in POSITION_ORDER:
+            raw_weight_of[t] = load_weight(nc, arena, weight, t)
         make_identity(nc, selector[:])
         make_identity(nc, identity[:])
         nc.vector.memset(eps[:], EPS)
@@ -247,6 +264,7 @@ def tile_capsulelayer_kernel(tc, image, weight, bias, out):
         for t in POSITION_ORDER[0:SCALAR_BIASES]:
             spread_bias(t, nc.scalar.copy)
         quantise_image(nc, raw_image, padded, even_codes, even_scales)
+        move_codes(nc, even_codes, even_scales, odd_codes, odd_scales)
         for t in POSITION_ORDER[SCALAR_BIASES:]:
             spread_bias(t, nc.vector.tensor_copy)
         def add_and_close(g, t):
@@ -259,10 +277,8 @@ def tile_capsulelayer_kernel(tc, image, weight, bias, out):
             ki, kj = divmod(t, KERNEL)
             if g == 0:
                 if ki == 0 and kj != 1:
-                    shift_columns(nc, kj, even_codes, even_scales)
-                if ki == 1:
-                    shift_rows(nc, kj, even_codes, even_scales, odd_codes, odd_scales)
-                quantise_weight(nc, arena, weight, t, weight_codes, weight_scales)
+                    finish_shift(nc, kj, even_codes, even_scales, odd_codes, odd_scales)
+                quantise_weight(nc, arena, raw_weight_of[t], t, weight_codes, weight_scales)
             for m in range(GROUP_TILES * g, GROUP_TILES * g + GROUP_TILES):
                 multiply(m, t)
                 add_bias(m, t)
@@ -283,7 +299,7 @@ def tile_capsulelayer_kernel(tc, image, weight, bias, out):
             if s == PHASES - 1 and (g == 1 or k >= LATE_FROM):
                 return LAST_SHARE
             if s < PHASES - 1:
-                return FIRST_IN_PSUM[s] + k % 2
+                return FIRST_IN_PSUM[s] + (1 if k % 4 == 3 else 0)
             return FIRST_IN_PSUM[s]
 
         def weigh_gpsimd(i):
@@ -434,7 +450,7 @@ def tile_capsulelayer_kernel(tc, image, weight, bias, out):
             pull_scale_of[(s, g)] = pull_scale
             nc.vector.reciprocal(out=pull_scale[:], in_=pull_sum[:])
 
-        passing_of = {}
+        passing_of, root_of = {}, {}
 
         def flip_first_pulls(s, g):
             passing = banks.tile([P, BANK_SLOTS, LANES], F32, tag="pulls%d" % g, offset=(4 + g) * BANK)
@@ -450,6 +466,16 @@ def tile_capsulelayer_kernel(tc, image, weight, bias, out):
             passing = banks.tile([P, BANK_SLOTS, LANES], F32, tag="pulls%d" % g, offset=(4 + g) * BANK)
             passing_of[(s, g)] = passing
             flip_pulls(s, g, BANK_SLOTS, IN_SBUF[s], passing)
+            if s < PHASES - 1:
+                for t in range(POSITIONS):
+                    nc.tensor.matmul(
+                        out=passing[:, BANK_SLOTS - 1, :],
+                        lhsT=pull_flipped_of[(s, g)][:, t, :],
+                        rhs=identity[:],
+                        is_transpose=True,
+                        start=(t == 0),
+                        stop=(t == POSITIONS - 1),
+                    )
 
         def copy_second_pulls(s, g):
             n = IN_SBUF[s]
@@ -457,11 +483,27 @@ def tile_capsulelayer_kernel(tc, image, weight, bias, out):
                 out=pull_sbuf_of[(s, g)][:, BANK_SLOTS:n, :],
                 in_=passing_of[(s, g)][:, 0 : n - BANK_SLOTS, :],
             )
+            if s < PHASES - 1:
+                root = arena.tile([P, LANES], F32, bufs=2, offset=AT_PULL_SUM)
+                nc.scalar.activation(
+                    out=root[:], in_=passing_of[(s, g)][:, BANK_SLOTS - 1, :], func=ACT.Abs_reciprocal_sqrt
+                )
+                nc.scalar.activation(out=root[:], in_=root[:], func=ACT.Square)
+                root_of[(s, g)] = root
 
         def flip_third_pulls(s, g):
             pull_psum = banks.tile([P, BANK_SLOTS, LANES], F32, tag="pulls%d" % g, offset=(4 + g) * BANK)
             pull_psum_of[(s, g)] = pull_psum
             flip_pulls(s, g, FIRST_IN_PSUM[s], POSITIONS, pull_psum)
+            if s < PHASES - 1:
+                nc.tensor.transpose(
+                    out=pull_psum[:, BANK_SLOTS - 1, :], in_=root_of[(s, g)][:], identity=identity[:]
+                )
+
+        def copy_scale(s, g):
+            pull_scale = arena.tile([P, P], F32, bufs=2, offset=AT_PULL_SCALE)
+            pull_scale_of[(s, g)] = pull_scale
+            nc.scalar.copy(out=pull_scale[:], in_=pull_psum_of[(s, g)][:, BANK_SLOTS - 1, :])
 
         def flip_late_pulls(s, g):
             late_pulls = banks.tile([P, BANK_SLOTS, LANES], F32, tag="late_pulls%d" % g, offset=g * BANK)
@@ -494,6 +536,8 @@ def tile_capsulelayer_kernel(tc, image, weight, bias, out):
                 copy_first_pulls(*phase_end(turn, 6))
             if phase_end(turn, 7):
                 copy_second_pulls(*phase_end(turn, 7))
+            if phase_end(turn, 8) and phase_end(turn, 8)[0] < PHASES - 1:
+                copy_scale(*phase_end(turn, 8))
             if 0 <= at(turn - 3)[0] < PHASES - 1:
                 subtract_and_square(turn - 3)
             if 0 <= at(turn - 4)[0] < PHASES - 1:
@@ -502,7 +546,8 @@ def tile_capsulelayer_kernel(tc, image, weight, bias, out):
                 flip_first_pulls(*phase_end(turn, 5))
             if phase_end(turn, 6):
                 flip_second_pulls(*phase_end(turn, 6))
-                scale_of_pulls(*phase_end(turn, 6))
+                if phase_end(turn, 6)[0] == PHASES - 1:
+                    scale_of_pulls(*phase_end(turn, 6))
             if phase_end(turn, 7):
                 flip_third_pulls(*phase_end(turn, 7))
             if phase_end(turn, 5) == (PHASES - 1, 1):

@@ -32,12 +32,12 @@ CHUNKS = CHANNELS // CHUNK
 PHASES = 4
 BANK_SLOTS = 4
 BANK = 2048
-FIRST_IN_PSUM = (9, 6, 6, 5)
-IN_SBUF = (0, 7, 7, 5)
+FIRST_IN_PSUM = (9, 6, 6, 6)
+IN_SBUF = (0, 7, 7, 6)
 LAST_SHARE = 3
 LATE_FROM = 5
 POSITION_ORDER = (1, 7, 4, 0, 6, 3, 2, 8, 5)
-SCALAR_BIASES = 5
+EARLY_BIASES = 7
 
 FLOPS = 2 * POSITIONS * SIDE * SIDE * (P * PACK) * FEATURES
 
@@ -261,11 +261,11 @@ def tile_capsulelayer_kernel(tc, image, weight, bias, out):
             )
             engine_copy(out=bias_tile[:, t, :, :], in_=product[:].rearrange("p c e -> p e c"))
 
-        for t in POSITION_ORDER[0:SCALAR_BIASES]:
-            spread_bias(t, nc.scalar.copy)
+        for i, t in enumerate(POSITION_ORDER[0:EARLY_BIASES]):
+            spread_bias(t, nc.vector.tensor_copy if i in (0, 2) else nc.scalar.copy)
         quantise_image(nc, raw_image, padded, even_codes, even_scales)
         move_codes(nc, even_codes, even_scales, odd_codes, odd_scales)
-        for t in POSITION_ORDER[SCALAR_BIASES:]:
+        for t in POSITION_ORDER[EARLY_BIASES:]:
             spread_bias(t, nc.vector.tensor_copy)
         def add_and_close(g, t):
             add_to_sum(g, t)
@@ -298,8 +298,6 @@ def tile_capsulelayer_kernel(tc, image, weight, bias, out):
             s, g, k = items[i]
             if s == PHASES - 1 and (g == 1 or k >= LATE_FROM):
                 return LAST_SHARE
-            if s < PHASES - 1:
-                return FIRST_IN_PSUM[s] + (1 if k % 4 == 3 else 0)
             return FIRST_IN_PSUM[s]
 
         def weigh_gpsimd(i):
@@ -438,18 +436,6 @@ def tile_capsulelayer_kernel(tc, image, weight, bias, out):
                     identity=identity[:],
                 )
 
-        def scale_of_pulls(s, g):
-            pull_sum = arena.tile([P, P], F32, bufs=2, offset=AT_PULL_SUM)
-            nc.vector.tensor_reduce(
-                out=pull_sum[:],
-                in_=pull_flipped_of[(s, g)][:].rearrange("p t x -> p x t"),
-                axis=X_AXIS,
-                op=ALU.add,
-            )
-            pull_scale = arena.tile([P, P], F32, bufs=2, offset=AT_PULL_SCALE)
-            pull_scale_of[(s, g)] = pull_scale
-            nc.vector.reciprocal(out=pull_scale[:], in_=pull_sum[:])
-
         passing_of, root_of = {}, {}
 
         def flip_first_pulls(s, g):
@@ -466,16 +452,15 @@ def tile_capsulelayer_kernel(tc, image, weight, bias, out):
             passing = banks.tile([P, BANK_SLOTS, LANES], F32, tag="pulls%d" % g, offset=(4 + g) * BANK)
             passing_of[(s, g)] = passing
             flip_pulls(s, g, BANK_SLOTS, IN_SBUF[s], passing)
-            if s < PHASES - 1:
-                for t in range(POSITIONS):
-                    nc.tensor.matmul(
-                        out=passing[:, BANK_SLOTS - 1, :],
-                        lhsT=pull_flipped_of[(s, g)][:, t, :],
-                        rhs=identity[:],
-                        is_transpose=True,
-                        start=(t == 0),
-                        stop=(t == POSITIONS - 1),
-                    )
+            for t in range(POSITIONS):
+                nc.tensor.matmul(
+                    out=passing[:, BANK_SLOTS - 1, :],
+                    lhsT=pull_flipped_of[(s, g)][:, t, :],
+                    rhs=identity[:],
+                    is_transpose=True,
+                    start=(t == 0),
+                    stop=(t == POSITIONS - 1),
+                )
 
         def copy_second_pulls(s, g):
             n = IN_SBUF[s]
@@ -483,22 +468,20 @@ def tile_capsulelayer_kernel(tc, image, weight, bias, out):
                 out=pull_sbuf_of[(s, g)][:, BANK_SLOTS:n, :],
                 in_=passing_of[(s, g)][:, 0 : n - BANK_SLOTS, :],
             )
-            if s < PHASES - 1:
-                root = arena.tile([P, LANES], F32, bufs=2, offset=AT_PULL_SUM)
-                nc.scalar.activation(
-                    out=root[:], in_=passing_of[(s, g)][:, BANK_SLOTS - 1, :], func=ACT.Abs_reciprocal_sqrt
-                )
-                nc.scalar.activation(out=root[:], in_=root[:], func=ACT.Square)
-                root_of[(s, g)] = root
+            root = arena.tile([P, LANES], F32, bufs=2, offset=AT_PULL_SUM)
+            nc.scalar.activation(
+                out=root[:], in_=passing_of[(s, g)][:, BANK_SLOTS - 1, :], func=ACT.Abs_reciprocal_sqrt
+            )
+            nc.scalar.activation(out=root[:], in_=root[:], func=ACT.Square)
+            root_of[(s, g)] = root
 
         def flip_third_pulls(s, g):
             pull_psum = banks.tile([P, BANK_SLOTS, LANES], F32, tag="pulls%d" % g, offset=(4 + g) * BANK)
             pull_psum_of[(s, g)] = pull_psum
             flip_pulls(s, g, FIRST_IN_PSUM[s], POSITIONS, pull_psum)
-            if s < PHASES - 1:
-                nc.tensor.transpose(
-                    out=pull_psum[:, BANK_SLOTS - 1, :], in_=root_of[(s, g)][:], identity=identity[:]
-                )
+            nc.tensor.transpose(
+                out=pull_psum[:, BANK_SLOTS - 1, :], in_=root_of[(s, g)][:], identity=identity[:]
+            )
 
         def copy_scale(s, g):
             pull_scale = arena.tile([P, P], F32, bufs=2, offset=AT_PULL_SCALE)
@@ -536,7 +519,7 @@ def tile_capsulelayer_kernel(tc, image, weight, bias, out):
                 copy_first_pulls(*phase_end(turn, 6))
             if phase_end(turn, 7):
                 copy_second_pulls(*phase_end(turn, 7))
-            if phase_end(turn, 8) and phase_end(turn, 8)[0] < PHASES - 1:
+            if phase_end(turn, 8):
                 copy_scale(*phase_end(turn, 8))
             if 0 <= at(turn - 3)[0] < PHASES - 1:
                 subtract_and_square(turn - 3)
@@ -546,8 +529,6 @@ def tile_capsulelayer_kernel(tc, image, weight, bias, out):
                 flip_first_pulls(*phase_end(turn, 5))
             if phase_end(turn, 6):
                 flip_second_pulls(*phase_end(turn, 6))
-                if phase_end(turn, 6)[0] == PHASES - 1:
-                    scale_of_pulls(*phase_end(turn, 6))
             if phase_end(turn, 7):
                 flip_third_pulls(*phase_end(turn, 7))
             if phase_end(turn, 5) == (PHASES - 1, 1):

@@ -32,8 +32,8 @@ CHUNKS = CHANNELS // CHUNK
 PHASES = 4
 BANK_SLOTS = 4
 BANK = 2048
-FIRST_IN_PSUM = (9, 6, 6, 6)
-IN_SBUF = (0, 7, 7, 6)
+FIRST_IN_PSUM = (9, 5, 5, 5)
+IN_SBUF = (0, 6, 6, 5)
 LAST_SHARE = 3
 LATE_FROM = 5
 POSITION_ORDER = (1, 7, 4, 0, 6, 3, 2, 8, 5)
@@ -245,6 +245,8 @@ def tile_capsulelayer_kernel(tc, image, weight, bias, out):
         make_identity(nc, selector[:])
         make_identity(nc, identity[:])
         nc.vector.memset(eps[:], EPS)
+        warm = small.tile([P, 1], F32, bufs=1)
+        nc.scalar.activation(out=warm[:], in_=eps[:], func=ACT.Abs_reciprocal_sqrt)
         padded = arena.tile([P, PADDED_ROWS, SIDE, PACK], BF16, align_bytes=64, offset=AT_PADDED)
         nc.vector.memset(padded[:, 0, :, :], 0.0)
         nc.vector.memset(padded[:, PADDED_ROWS - 1, :, :], 0.0)
@@ -298,6 +300,8 @@ def tile_capsulelayer_kernel(tc, image, weight, bias, out):
             s, g, k = items[i]
             if s == PHASES - 1 and (g == 1 or k >= LATE_FROM):
                 return LAST_SHARE
+            if s < PHASES - 1:
+                return 6
             return FIRST_IN_PSUM[s]
 
         def weigh_gpsimd(i):
@@ -444,7 +448,7 @@ def tile_capsulelayer_kernel(tc, image, weight, bias, out):
             flip_pulls(s, g, 0, BANK_SLOTS, passing)
 
         def copy_first_pulls(s, g):
-            pull_sbuf = arena.tile([P, 7, LANES], F32, bufs=2, offset=AT_PULL)
+            pull_sbuf = arena.tile([P, 6, LANES], F32, bufs=2, offset=AT_PULL)
             pull_sbuf_of[(s, g)] = pull_sbuf
             nc.scalar.copy(out=pull_sbuf[:, 0:BANK_SLOTS, :], in_=passing_of[(s, g)][:])
 
@@ -478,15 +482,25 @@ def tile_capsulelayer_kernel(tc, image, weight, bias, out):
         def flip_third_pulls(s, g):
             pull_psum = banks.tile([P, BANK_SLOTS, LANES], F32, tag="pulls%d" % g, offset=(4 + g) * BANK)
             pull_psum_of[(s, g)] = pull_psum
-            flip_pulls(s, g, FIRST_IN_PSUM[s], POSITIONS, pull_psum)
-            nc.tensor.transpose(
-                out=pull_psum[:, BANK_SLOTS - 1, :], in_=root_of[(s, g)][:], identity=identity[:]
-            )
+            for t in range(FIRST_IN_PSUM[s] + 1, POSITIONS):
+                nc.tensor.transpose(
+                    out=pull_psum[:, t - FIRST_IN_PSUM[s], :],
+                    in_=pull_flipped_of[(s, g)][:, t, :],
+                    identity=identity[:],
+                )
+            nc.tensor.transpose(out=pull_psum[:, 0, :], in_=root_of[(s, g)][:], identity=identity[:])
 
         def copy_scale(s, g):
             pull_scale = arena.tile([P, P], F32, bufs=2, offset=AT_PULL_SCALE)
             pull_scale_of[(s, g)] = pull_scale
-            nc.scalar.copy(out=pull_scale[:], in_=pull_psum_of[(s, g)][:, BANK_SLOTS - 1, :])
+            nc.scalar.copy(out=pull_scale[:], in_=pull_psum_of[(s, g)][:, 0, :])
+
+        def flip_fourth_pull(s, g):
+            nc.tensor.transpose(
+                out=pull_psum_of[(s, g)][:, 0, :],
+                in_=pull_flipped_of[(s, g)][:, FIRST_IN_PSUM[s], :],
+                identity=identity[:],
+            )
 
         def flip_late_pulls(s, g):
             late_pulls = banks.tile([P, BANK_SLOTS, LANES], F32, tag="late_pulls%d" % g, offset=g * BANK)
@@ -531,6 +545,8 @@ def tile_capsulelayer_kernel(tc, image, weight, bias, out):
                 flip_second_pulls(*phase_end(turn, 6))
             if phase_end(turn, 7):
                 flip_third_pulls(*phase_end(turn, 7))
+            if phase_end(turn, 8):
+                flip_fourth_pull(*phase_end(turn, 8))
             if phase_end(turn, 5) == (PHASES - 1, 1):
                 flip_late_pulls(PHASES - 1, 0)
             if phase_end(turn, 6) == (PHASES - 1, 1):

@@ -32,10 +32,15 @@ CHUNKS = CHANNELS // CHUNK
 PHASES = 4
 BANK_SLOTS = 4
 BANK = 2048
-FIRST_IN_PSUM = (9, 5, 5, 5)
-IN_SBUF = (0, 6, 6, 5)
+WEIGHED = POSITIONS - 1
+FIRST_IN_PSUM = 4
+MIDDLE_SHARES = (5, 6)
+IN_SBUF = 6
 LAST_SHARE = 3
-LATE_FROM = 5
+LATE_FROM = 6
+STILL_SUBTRACTING = 3
+GPSIMD_SUBTRACTS = 2
+GPSIMD_SQUARES = 2
 POSITION_ORDER = (1, 7, 4, 0, 6, 3, 2, 8, 5)
 EARLY_BIASES = 7
 
@@ -55,20 +60,17 @@ AT_WEIGHT_CODES = AT_REST
 AT_WEIGHT_SCALES = AT_WEIGHT_CODES + POSITIONS * FEATURES * 4
 AT_EVEN_CODES = AT_WEIGHT_SCALES + POSITIONS * FEATURES
 AT_EVEN_SCALES = AT_EVEN_CODES + KERNEL * PADDED_ROWS * SIDE * 4
-AT_ODD_CODES = AT_EVEN_SCALES + KERNEL * PADDED_ROWS * SIDE
-AT_ODD_SCALES = AT_ODD_CODES + KERNEL * SIDE * SIDE * 4
+AT_ODD_SCALES = AT_EVEN_SCALES + KERNEL * PADDED_ROWS * SIDE
 AT_BIAS = AT_ODD_SCALES + KERNEL * SIDE * SIDE
-AT_BIAS_MEAN = AT_BIAS + POSITIONS * FEATURES * 2
-AT_MEAN = AT_BIAS_MEAN + FEATURES * 4
 AT_WEIGHED = AT_REST
 AT_DIFFERENCE = AT_WEIGHED + 3 * WORK_BYTES
-AT_PULL_FLIPPED = AT_DIFFERENCE + 3 * WORK_BYTES
-AT_PULL = AT_PULL_FLIPPED + 2 * POSITIONS * LANES * 4
-AT_SMALL = AT_MEAN + 2 * CHANNELS * LANES * 4
-AT_RESULT = AT_SMALL
-AT_CENTRE_FLIPPED = AT_RESULT + 4 * CHUNK * P * 4
-AT_PULL_SUM = AT_CENTRE_FLIPPED + 3 * CHUNK * P * 4
-AT_PULL_SCALE = AT_PULL_SUM + 2 * P * 4
+AT_MEAN_FLIPPED = AT_DIFFERENCE + 3 * WORK_BYTES
+AT_PULL_FLIPPED = AT_MEAN_FLIPPED
+AT_CENTRE_FLIPPED = AT_PULL_FLIPPED + 2 * POSITIONS * LANES * 4
+AT_RESULT = AT_CENTRE_FLIPPED + 3 * CHUNK * P * 4
+AT_MEAN = AT_MEAN_FLIPPED + 2 * CHANNELS * P * 4
+AT_PULL = AT_MEAN + 2 * CHANNELS * LANES * 4
+AT_PULL_SUM = AT_PULL + 2 * IN_SBUF * LANES * 4
 
 
 def quantise_image(nc, raw_image, padded, even_codes, even_scales):
@@ -90,28 +92,24 @@ def quantise_image(nc, raw_image, padded, even_codes, even_scales):
     )
 
 
-def move_codes(nc, even_codes, even_scales, odd_codes, odd_scales):
+def move_codes(nc, codes, even_scales, odd_scales):
     pixels = PADDED_ROWS * SIDE
     whole = SIDE * SIDE
-    middle = even_codes[:, 1, :].bitcast(I32)
-    nc.sync.dma_start(out=odd_codes[:, 1, :].bitcast(I32), in_=middle[:, SIDE : SIDE + whole])
+    middle = codes[:, 1, :].bitcast(I32)
     nc.sync.dma_start(
         out=odd_scales[:, 1, :].bitcast(I32), in_=even_scales[:, 1, SIDE : SIDE + whole].bitcast(I32)
     )
-    nc.sync.dma_start(out=even_codes[:, 0, 1:pixels].bitcast(I32), in_=middle[:, 0 : pixels - 1])
-    nc.sync.dma_start(out=odd_codes[:, 0, :].bitcast(I32), in_=middle[:, SIDE - 1 : SIDE - 1 + whole])
-    nc.sync.dma_start(out=even_codes[:, 2, 0 : pixels - 1].bitcast(I32), in_=middle[:, 1:pixels])
-    nc.sync.dma_start(out=odd_codes[:, 2, :].bitcast(I32), in_=middle[:, SIDE + 1 : SIDE + 1 + whole])
+    nc.sync.dma_start(out=codes[:, 0, 1:pixels].bitcast(I32), in_=middle[:, 0 : pixels - 1])
+    nc.sync.dma_start(out=codes[:, 2, 0 : pixels - 1].bitcast(I32), in_=middle[:, 1:pixels])
 
 
-def finish_shift(nc, kj, even_codes, even_scales, odd_codes, odd_scales):
+def finish_shift(nc, kj, codes, even_scales, odd_scales):
     pixels = PADDED_ROWS * SIDE
     to, source = (slice(1, pixels), slice(0, pixels - 1)) if kj == 0 else (slice(0, pixels - 1), slice(1, pixels))
     empty = 0 if kj == 0 else SIDE - 1
-    for codes in (even_codes, odd_codes):
-        nc.vector.memset(
-            codes[:, kj, :].bitcast(I32).rearrange("p (r w) -> p r w", w=SIDE)[:, :, empty : empty + 1], 0
-        )
+    nc.vector.memset(
+        codes[:, kj, :].bitcast(I32).rearrange("p (r w) -> p r w", w=SIDE)[:, :, empty : empty + 1], 0
+    )
     nc.vector.tensor_copy(out=even_scales[:, kj, to], in_=even_scales[:, 1, source])
     nc.sync.dma_start(
         out=odd_scales[:, kj, :].bitcast(I32),
@@ -151,9 +149,12 @@ def tile_capsulelayer_kernel(tc, image, weight, bias, out):
         priors_0 = arena.tile([P, POSITIONS, CHANNELS, LANES], F32, offset=AT_PRIORS)
         priors_1 = arena.tile([P, POSITIONS, CHANNELS, LANES], F32, offset=AT_PRIORS + PRIOR_BYTES)
         priors_of = (priors_0, priors_1)
-        mean_flipped_0 = arena.tile([P, CHANNELS, P], F32, offset=AT_MEAN)
-        mean_flipped_1 = arena.tile([P, CHANNELS, P], F32, offset=AT_MEAN + CHANNELS * P * 4)
+        mean_flipped_0 = arena.tile([P, CHANNELS, P], F32, offset=AT_MEAN_FLIPPED)
+        mean_flipped_1 = arena.tile([P, CHANNELS, P], F32, offset=AT_MEAN_FLIPPED + CHANNELS * P * 4)
         mean_flipped_of = (mean_flipped_0, mean_flipped_1)
+        mean_0 = arena.tile([P, CHANNELS, LANES], F32, offset=AT_MEAN)
+        mean_1 = arena.tile([P, CHANNELS, LANES], F32, offset=AT_MEAN + CHANNELS * LANES * 4)
+        mean_of = (mean_0, mean_1)
         weight_codes = arena.tile(
             [P, POSITIONS, FEATURES], U32, align_bytes=64, offset=AT_WEIGHT_CODES
         )
@@ -166,7 +167,6 @@ def tile_capsulelayer_kernel(tc, image, weight, bias, out):
         even_scales = arena.tile(
             [P, KERNEL, PADDED_ROWS * SIDE], U8, align_bytes=64, offset=AT_EVEN_SCALES
         )
-        odd_codes = arena.tile([P, KERNEL, SIDE * SIDE], U32, align_bytes=64, offset=AT_ODD_CODES)
         odd_scales = arena.tile([P, KERNEL, SIDE * SIDE], U8, align_bytes=64, offset=AT_ODD_SCALES)
         bias_tile = arena.tile([P, POSITIONS, CHANNELS, CAPSULES], BF16, offset=AT_BIAS)
         selector = arena.tile([P, P], BF16, offset=AT_ONES + P * 2)
@@ -178,12 +178,12 @@ def tile_capsulelayer_kernel(tc, image, weight, bias, out):
 
         def multiply(m, t):
             ki, kj = divmod(t, KERNEL)
+            pixels = slice(P * m + SIDE * ki, P * m + SIDE * ki + P)
+            codes = even_codes[:, kj, pixels]
             if ki == 1:
-                pixels = slice(P * m, P * m + P)
-                codes, scales = odd_codes[:, kj, pixels], odd_scales[:, kj, pixels]
+                scales = odd_scales[:, kj, P * m : P * m + P]
             else:
-                pixels = slice(P * m + SIDE * ki, P * m + SIDE * ki + P)
-                codes, scales = even_codes[:, kj, pixels], even_scales[:, kj, pixels]
+                scales = even_scales[:, kj, pixels]
             product = banks.tile([P, CAPSULES, CHANNELS], F32, bufs=4, offset=4 * BANK)
             products[(m, t)] = product
             nc.tensor.matmul_mx(
@@ -266,7 +266,7 @@ def tile_capsulelayer_kernel(tc, image, weight, bias, out):
         for i, t in enumerate(POSITION_ORDER[0:EARLY_BIASES]):
             spread_bias(t, nc.vector.tensor_copy if i in (0, 2) else nc.scalar.copy)
         quantise_image(nc, raw_image, padded, even_codes, even_scales)
-        move_codes(nc, even_codes, even_scales, odd_codes, odd_scales)
+        move_codes(nc, even_codes, even_scales, odd_scales)
         for t in POSITION_ORDER[EARLY_BIASES:]:
             spread_bias(t, nc.vector.tensor_copy)
         def add_and_close(g, t):
@@ -274,23 +274,34 @@ def tile_capsulelayer_kernel(tc, image, weight, bias, out):
             if t == POSITION_ORDER[-1]:
                 mean_prior(g)
 
+        def prepare(i):
+            if i < POSITIONS:
+                t = POSITION_ORDER[i]
+                ki, kj = divmod(t, KERNEL)
+                if ki == 0 and kj != 1:
+                    finish_shift(nc, kj, even_codes, even_scales, odd_scales)
+                quantise_weight(nc, arena, raw_weight_of[t], t, weight_codes, weight_scales)
+
+        prepare(0)
         steps = [(g, t) for g in range(GROUPS) for t in POSITION_ORDER]
         for i, (g, t) in enumerate(steps):
-            ki, kj = divmod(t, KERNEL)
-            if g == 0:
-                if ki == 0 and kj != 1:
-                    finish_shift(nc, kj, even_codes, even_scales, odd_codes, odd_scales)
-                quantise_weight(nc, arena, raw_weight_of[t], t, weight_codes, weight_scales)
-            for m in range(GROUP_TILES * g, GROUP_TILES * g + GROUP_TILES):
-                multiply(m, t)
-                add_bias(m, t)
+            for lane in range(GROUP_TILES):
+                if i < POSITIONS and lane == 2:
+                    prepare(i + 1)
+                multiply(GROUP_TILES * g + lane, t)
+                add_bias(GROUP_TILES * g + lane, t)
             if i > 0:
                 add_and_close(*steps[i - 1])
 
         items = [(s, g, k) for s in range(PHASES) for g in range(GROUPS) for k in range(CHUNKS)]
+        count = len(items)
+        first_weighed = GROUPS * CHUNKS
         weighed_of, total_of, centre_flipped_of, centre_of, difference_of = {}, {}, {}, {}, {}
         distance_banks = {}
-        pull_flipped_of, pull_scale_of, pull_sbuf_of, pull_psum_of, late_pulls_of = {}, {}, {}, {}, {}
+        pull_flipped_of, root_of, pull_bank_of, pull_sbuf_of, pull_psum_of, late_pull_of = {}, {}, {}, {}, {}, {}
+
+        def at(i):
+            return items[i] if 0 <= i < count else (-1, -1, -1)
 
         def chunk_priors(i):
             s, g, k = items[i]
@@ -298,16 +309,16 @@ def tile_capsulelayer_kernel(tc, image, weight, bias, out):
 
         def gpsimd_share(i):
             s, g, k = items[i]
-            if s == PHASES - 1 and (g == 1 or k >= LATE_FROM):
-                return LAST_SHARE
             if s < PHASES - 1:
-                return 6
-            return FIRST_IN_PSUM[s]
+                return MIDDLE_SHARES[k % len(MIDDLE_SHARES)]
+            if g == 0 and k < STILL_SUBTRACTING:
+                return MIDDLE_SHARES[0]
+            return LAST_SHARE if g == 1 or k >= LATE_FROM else FIRST_IN_PSUM
 
         def weigh_gpsimd(i):
             s, g, k = items[i]
             n = gpsimd_share(i)
-            weighed = arena.tile([P, POSITIONS, CHUNK, LANES], F32, bufs=3, offset=AT_WEIGHED)
+            weighed = arena.tile([P, WEIGHED, CHUNK, LANES], F32, bufs=3, offset=AT_WEIGHED)
             weighed_of[i] = weighed
             nc.gpsimd.tensor_tensor(
                 out=weighed[:, 0:n, :, :],
@@ -319,10 +330,10 @@ def tile_capsulelayer_kernel(tc, image, weight, bias, out):
         def weigh_vector(i):
             s, g, k = items[i]
             n = gpsimd_share(i)
-            f = FIRST_IN_PSUM[s]
+            f = FIRST_IN_PSUM
             for first, last, base, pulls_in_psum in (
-                (n, f, n, late_pulls_of),
-                (max(n, f), POSITIONS, f, pull_psum_of),
+                (n, f, n, late_pull_of),
+                (max(n, f), WEIGHED, f, pull_psum_of),
             ):
                 if first < last:
                     nc.vector.tensor_tensor(
@@ -335,37 +346,38 @@ def tile_capsulelayer_kernel(tc, image, weight, bias, out):
                     )
 
         def sum_positions(i):
-            if items[i][0] == PHASES - 1 and i % 2 == 1:
+            s, g, k = items[i]
+            if s == PHASES - 1 and i % 2 == 1:
                 weighted_sum = banks.tile([P, BANK_SLOTS, P], F32, tag="centre", bufs=2, offset=6 * BANK)
             else:
                 weighted_sum = banks.tile([P, BANK_SLOTS, P], F32, offset=3 * BANK)
             total_of[i] = weighted_sum
             for c in range(CHUNK):
-                for t in range(POSITIONS):
-                    nc.tensor.matmul(
-                        out=weighted_sum[:, c, :],
-                        lhsT=weighed_of[i][:, t, c, :],
-                        rhs=identity[:],
-                        is_transpose=True,
-                        start=(t == 0),
-                        stop=(t == POSITIONS - 1),
-                    )
+                blocks = [weighed_of[i][:, t, c, :] for t in range(WEIGHED)]
+                if s == PHASES - 1:
+                    blocks = [mean_of[g][:, CHUNK * k + c, :]] + blocks
+                add_flipped(weighted_sum[:, c, :], blocks)
 
-        def normalise(i):
-            s, g, k = items[i]
-            if s == PHASES - 1:
+        def add_flipped(out_block, blocks):
+            for j, block in enumerate(blocks):
+                nc.tensor.matmul(
+                    out=out_block,
+                    lhsT=block,
+                    rhs=identity[:],
+                    is_transpose=True,
+                    start=(j == 0),
+                    stop=(j == len(blocks) - 1),
+                )
+
+        def empty_sum(i):
+            if items[i][0] == PHASES - 1:
                 centre_flipped = arena.tile([P, CHUNK, P], F32, bufs=4, tag="result", offset=AT_RESULT)
             else:
                 centre_flipped = arena.tile(
                     [P, CHUNK, P], F32, bufs=3, tag="centre_flipped", offset=AT_CENTRE_FLIPPED
                 )
             centre_flipped_of[i] = centre_flipped
-            nc.vector.tensor_tensor(
-                out=centre_flipped[:],
-                in0=total_of[i][:, 0:CHUNK, :],
-                in1=pull_scale_of[(s, g)][:].unsqueeze(1).to_broadcast([P, CHUNK, P]),
-                op=ALU.mult,
-            )
+            nc.scalar.copy(out=centre_flipped[:], in_=total_of[i][:, 0:CHUNK, :])
 
         def store(i):
             s, g, k = items[i]
@@ -387,18 +399,48 @@ def tile_capsulelayer_kernel(tc, image, weight, bias, out):
                     flipped = centre_flipped_of[i][:, c, :]
                 nc.tensor.transpose(out=centre[:, c, :], in_=flipped, identity=identity[:])
 
-        def subtract_and_square(i):
+        def keep_mean(i):
             s, g, k = items[i]
-            centre = centre_of[i][:, 0:CHUNK, :]
+            nc.scalar.copy(
+                out=mean_of[g][:, CHUNK * k : CHUNK * k + CHUNK, :], in_=centre_of[i][:, 0:CHUNK, :]
+            )
+
+        def subtract(i):
+            s, g, k = items[i]
             difference = arena.tile([P, POSITIONS, CHUNK, LANES], F32, bufs=3, offset=AT_DIFFERENCE)
             difference_of[i] = difference
+            target = chunk_priors(i) if s == 0 else difference
+            n = POSITIONS - GPSIMD_SUBTRACTS if i + 3 < first_weighed else POSITIONS
             nc.vector.tensor_tensor(
-                out=difference[:],
-                in0=chunk_priors(i),
-                in1=centre.unsqueeze(1).to_broadcast([P, POSITIONS, CHUNK, LANES]),
+                out=target[:, 0:n, :, :],
+                in0=chunk_priors(i)[:, 0:n, :, :],
+                in1=centre_of[i][:, 0:CHUNK, :].unsqueeze(1).to_broadcast([P, n, CHUNK, LANES]),
                 op=ALU.subtract,
             )
-            nc.scalar.activation(out=difference[:], in_=difference[:], func=ACT.Square)
+            if n < POSITIONS:
+                nc.gpsimd.tensor_tensor(
+                    out=target[:, n:POSITIONS, :, :],
+                    in0=chunk_priors(i)[:, n:POSITIONS, :, :],
+                    in1=mean_of[g][:, CHUNK * k : CHUNK * k + CHUNK, :]
+                    .unsqueeze(1)
+                    .to_broadcast([P, POSITIONS - n, CHUNK, LANES]),
+                    op=ALU.subtract,
+                )
+
+        def square(i):
+            s, g, k = items[i]
+            source = chunk_priors(i) if s == 0 else difference_of[i]
+            n = POSITIONS - GPSIMD_SQUARES if i + 3 < first_weighed else POSITIONS
+            nc.scalar.activation(
+                out=difference_of[i][:, 0:n, :, :], in_=source[:, 0:n, :, :], func=ACT.Square
+            )
+            if n < POSITIONS:
+                nc.gpsimd.tensor_tensor(
+                    out=difference_of[i][:, n:POSITIONS, :, :],
+                    in0=source[:, n:POSITIONS, :, :],
+                    in1=source[:, n:POSITIONS, :, :],
+                    op=ALU.mult,
+                )
 
         def sum_channels(i):
             s, g, k = items[i]
@@ -420,6 +462,11 @@ def tile_capsulelayer_kernel(tc, image, weight, bias, out):
                         stop=(k == CHUNKS - 1 and last_slot and c == CHUNK - 1),
                     )
 
+        def take_pull_bank(s, g):
+            pull_bank = banks.tile([P, BANK_SLOTS, LANES], F32, tag="pulls%d" % g, offset=(4 + g) * BANK)
+            pull_bank_of[(s, g)] = pull_bank
+            return pull_bank
+
         def pulls(s, g):
             pull_flipped = arena.tile([P, POSITIONS, P], F32, bufs=2, offset=AT_PULL_FLIPPED)
             pull_flipped_of[(s, g)] = pull_flipped
@@ -432,85 +479,64 @@ def tile_capsulelayer_kernel(tc, image, weight, bias, out):
                     bias=eps[:, 0:1],
                 )
 
-        def flip_pulls(s, g, first, last, psum_tile):
-            for t in range(first, last):
-                nc.tensor.transpose(
-                    out=psum_tile[:, t - first, :],
-                    in_=pull_flipped_of[(s, g)][:, t, :],
-                    identity=identity[:],
-                )
+        def sum_pulls(s, g):
+            add_flipped(take_pull_bank(s, g)[:, 0, :], [pull_flipped_of[(s, g)][:, t, :] for t in range(POSITIONS)])
 
-        passing_of, root_of = {}, {}
+        def invert_sum(s, g):
+            root = arena.tile([P, LANES], F32, bufs=2, offset=AT_PULL_SUM)
+            root_of[(s, g)] = root
+            nc.scalar.activation(out=root[:], in_=pull_bank_of[(s, g)][:, 0, :], func=ACT.Abs_reciprocal_sqrt)
+            nc.scalar.activation(out=root[:], in_=root[:], func=ACT.Square)
+
+        def flip_scale(s, g):
+            nc.tensor.transpose(out=take_pull_bank(s, g)[:, 0, :], in_=root_of[(s, g)][:], identity=identity[:])
+
+        def normalise_pulls(s, g):
+            pull_flipped = pull_flipped_of[(s, g)]
+            scale = pull_bank_of[(s, g)]
+            nc.vector.tensor_tensor(
+                out=pull_flipped[:, 0:WEIGHED, :],
+                in0=pull_flipped[:, 0:WEIGHED, :],
+                in1=scale[:, 0:1, :].to_broadcast([P, WEIGHED, P]),
+                op=ALU.mult,
+            )
+            nc.vector.scalar_tensor_tensor(
+                out=pull_flipped[:, WEIGHED, :],
+                in0=pull_flipped[:, WEIGHED, :],
+                scalar=-1.0,
+                in1=scale[:, 0, :],
+                op0=ALU.mult,
+                op1=ALU.mult,
+            )
+
+        def flip_pulls(s, g, first, last, psum_tile):
+            pull_flipped = pull_flipped_of[(s, g)]
+            for t in range(first, last):
+                add_flipped(psum_tile[:, t - first, :], [pull_flipped[:, t, :], pull_flipped[:, WEIGHED, :]])
 
         def flip_first_pulls(s, g):
-            passing = banks.tile([P, BANK_SLOTS, LANES], F32, tag="pulls%d" % g, offset=(4 + g) * BANK)
-            passing_of[(s, g)] = passing
-            flip_pulls(s, g, 0, BANK_SLOTS, passing)
+            flip_pulls(s, g, 0, FIRST_IN_PSUM, take_pull_bank(s, g))
 
         def copy_first_pulls(s, g):
-            pull_sbuf = arena.tile([P, 6, LANES], F32, bufs=2, offset=AT_PULL)
+            pull_sbuf = arena.tile([P, IN_SBUF, LANES], F32, bufs=2, offset=AT_PULL)
             pull_sbuf_of[(s, g)] = pull_sbuf
-            nc.scalar.copy(out=pull_sbuf[:, 0:BANK_SLOTS, :], in_=passing_of[(s, g)][:])
+            nc.scalar.copy(out=pull_sbuf[:, 0:FIRST_IN_PSUM, :], in_=pull_bank_of[(s, g)][:])
 
         def flip_second_pulls(s, g):
-            passing = banks.tile([P, BANK_SLOTS, LANES], F32, tag="pulls%d" % g, offset=(4 + g) * BANK)
-            passing_of[(s, g)] = passing
-            flip_pulls(s, g, BANK_SLOTS, IN_SBUF[s], passing)
-            for t in range(POSITIONS):
-                nc.tensor.matmul(
-                    out=passing[:, BANK_SLOTS - 1, :],
-                    lhsT=pull_flipped_of[(s, g)][:, t, :],
-                    rhs=identity[:],
-                    is_transpose=True,
-                    start=(t == 0),
-                    stop=(t == POSITIONS - 1),
-                )
+            pull_psum = take_pull_bank(s, g)
+            pull_psum_of[(s, g)] = pull_psum
+            flip_pulls(s, g, FIRST_IN_PSUM, WEIGHED, pull_psum)
 
         def copy_second_pulls(s, g):
-            n = IN_SBUF[s]
             nc.scalar.copy(
-                out=pull_sbuf_of[(s, g)][:, BANK_SLOTS:n, :],
-                in_=passing_of[(s, g)][:, 0 : n - BANK_SLOTS, :],
-            )
-            root = arena.tile([P, LANES], F32, bufs=2, offset=AT_PULL_SUM)
-            nc.scalar.activation(
-                out=root[:], in_=passing_of[(s, g)][:, BANK_SLOTS - 1, :], func=ACT.Abs_reciprocal_sqrt
-            )
-            nc.scalar.activation(out=root[:], in_=root[:], func=ACT.Square)
-            root_of[(s, g)] = root
-
-        def flip_third_pulls(s, g):
-            pull_psum = banks.tile([P, BANK_SLOTS, LANES], F32, tag="pulls%d" % g, offset=(4 + g) * BANK)
-            pull_psum_of[(s, g)] = pull_psum
-            for t in range(FIRST_IN_PSUM[s] + 1, POSITIONS):
-                nc.tensor.transpose(
-                    out=pull_psum[:, t - FIRST_IN_PSUM[s], :],
-                    in_=pull_flipped_of[(s, g)][:, t, :],
-                    identity=identity[:],
-                )
-            nc.tensor.transpose(out=pull_psum[:, 0, :], in_=root_of[(s, g)][:], identity=identity[:])
-
-        def copy_scale(s, g):
-            pull_scale = arena.tile([P, P], F32, bufs=2, offset=AT_PULL_SCALE)
-            pull_scale_of[(s, g)] = pull_scale
-            nc.scalar.copy(out=pull_scale[:], in_=pull_psum_of[(s, g)][:, 0, :])
-
-        def flip_fourth_pull(s, g):
-            nc.tensor.transpose(
-                out=pull_psum_of[(s, g)][:, 0, :],
-                in_=pull_flipped_of[(s, g)][:, FIRST_IN_PSUM[s], :],
-                identity=identity[:],
+                out=pull_sbuf_of[(s, g)][:, FIRST_IN_PSUM:IN_SBUF, :],
+                in_=pull_psum_of[(s, g)][:, 0 : IN_SBUF - FIRST_IN_PSUM, :],
             )
 
-        def flip_late_pulls(s, g):
-            late_pulls = banks.tile([P, BANK_SLOTS, LANES], F32, tag="late_pulls%d" % g, offset=g * BANK)
-            late_pulls_of[(s, g)] = late_pulls
-            flip_pulls(s, g, LAST_SHARE, FIRST_IN_PSUM[s], late_pulls)
-
-        count = len(items)
-
-        def at(i):
-            return items[i] if 0 <= i < count else (-1, -1, -1)
+        def flip_late_pull(s, g):
+            late_pull = banks.tile([P, BANK_SLOTS, LANES], F32, tag="late_pull%d" % g, offset=g * BANK)
+            late_pull_of[(s, g)] = late_pull
+            flip_pulls(s, g, LAST_SHARE, FIRST_IN_PSUM, late_pull)
 
         def phase_end(turn, lag):
             s, g, k = at(turn - lag)
@@ -523,6 +549,8 @@ def tile_capsulelayer_kernel(tc, image, weight, bias, out):
                 weigh_gpsimd(turn)
             if 0 <= at(turn - 2)[0] < PHASES - 1:
                 flip_centre(turn - 2)
+                if at(turn - 2)[0] == 0:
+                    keep_mean(turn - 2)
             if turn == 2:
                 add_and_close(*steps[-1])
             if at(turn - 1)[0] >= 1:
@@ -530,30 +558,29 @@ def tile_capsulelayer_kernel(tc, image, weight, bias, out):
             if phase_end(turn, 5):
                 pulls(*phase_end(turn, 5))
             if phase_end(turn, 6):
-                copy_first_pulls(*phase_end(turn, 6))
+                invert_sum(*phase_end(turn, 6))
+                flip_scale(*phase_end(turn, 6))
+            if at(turn - 1)[0] >= 1:
+                empty_sum(turn - 1)
+                if at(turn - 1)[0] == PHASES - 1:
+                    store(turn - 1)
             if phase_end(turn, 7):
-                copy_second_pulls(*phase_end(turn, 7))
+                normalise_pulls(*phase_end(turn, 7))
+                flip_first_pulls(*phase_end(turn, 7))
+                copy_first_pulls(*phase_end(turn, 7))
             if phase_end(turn, 8):
-                copy_scale(*phase_end(turn, 8))
+                flip_second_pulls(*phase_end(turn, 8))
+                copy_second_pulls(*phase_end(turn, 8))
+            if phase_end(turn, 6) == (PHASES - 1, 1):
+                flip_late_pull(PHASES - 1, 0)
+            if phase_end(turn, 8) == (PHASES - 1, 1):
+                flip_late_pull(PHASES - 1, 1)
             if 0 <= at(turn - 3)[0] < PHASES - 1:
-                subtract_and_square(turn - 3)
+                subtract(turn - 3)
+                square(turn - 3)
             if 0 <= at(turn - 4)[0] < PHASES - 1:
                 sum_channels(turn - 4)
             if phase_end(turn, 5):
-                flip_first_pulls(*phase_end(turn, 5))
-            if phase_end(turn, 6):
-                flip_second_pulls(*phase_end(turn, 6))
-            if phase_end(turn, 7):
-                flip_third_pulls(*phase_end(turn, 7))
-            if phase_end(turn, 8):
-                flip_fourth_pull(*phase_end(turn, 8))
-            if phase_end(turn, 5) == (PHASES - 1, 1):
-                flip_late_pulls(PHASES - 1, 0)
-            if phase_end(turn, 6) == (PHASES - 1, 1):
-                flip_late_pulls(PHASES - 1, 1)
+                sum_pulls(*phase_end(turn, 5))
             if at(turn)[0] >= 1:
                 weigh_vector(turn)
-            if at(turn - 1)[0] >= 1:
-                normalise(turn - 1)
-                if at(turn - 1)[0] == PHASES - 1:
-                    store(turn - 1)

@@ -34,15 +34,18 @@ BANK_SLOTS = 4
 BANK = 2048
 WEIGHED = POSITIONS - 1
 FIRST_IN_PSUM = 4
-MIDDLE_SHARES = (5, 6)
+MIDDLE_SHARES = (4, 6, 6, 5, 6, 5, 6, 6)
 IN_SBUF = 6
 LAST_SHARE = 3
 LATE_FROM = 6
 STILL_SUBTRACTING = 3
-GPSIMD_SUBTRACTS = 2
-GPSIMD_SQUARES = 2
+EARLY_SUBTRACTS = 6
+EARLY_SQUARES = 0
+LATE_SUBTRACTS = 2
+LATE_SQUARES = 2
 POSITION_ORDER = (1, 7, 4, 0, 6, 3, 2, 8, 5)
-EARLY_BIASES = 7
+TOP_ROWS = 18
+WHOLE_ROWS = 16
 
 FLOPS = 2 * POSITIONS * SIDE * SIDE * (P * PACK) * FEATURES
 
@@ -63,32 +66,29 @@ AT_EVEN_SCALES = AT_EVEN_CODES + KERNEL * PADDED_ROWS * SIDE * 4
 AT_ODD_SCALES = AT_EVEN_SCALES + KERNEL * PADDED_ROWS * SIDE
 AT_BIAS = AT_ODD_SCALES + KERNEL * SIDE * SIDE
 AT_WEIGHED = AT_REST
-AT_DIFFERENCE = AT_WEIGHED + 3 * WORK_BYTES
-AT_MEAN_FLIPPED = AT_DIFFERENCE + 3 * WORK_BYTES
-AT_PULL_FLIPPED = AT_MEAN_FLIPPED
-AT_CENTRE_FLIPPED = AT_PULL_FLIPPED + 2 * POSITIONS * LANES * 4
-AT_RESULT = AT_CENTRE_FLIPPED + 3 * CHUNK * P * 4
-AT_MEAN = AT_MEAN_FLIPPED + 2 * CHANNELS * P * 4
-AT_PULL = AT_MEAN + 2 * CHANNELS * LANES * 4
+AT_PULL_FLIPPED = AT_WEIGHED + 3 * WORK_BYTES
+AT_PULL = AT_PULL_FLIPPED + 2 * POSITIONS * LANES * 4
 AT_PULL_SUM = AT_PULL + 2 * IN_SBUF * LANES * 4
+AT_CENTRE_FLIPPED = AT_PULL_SUM + 2 * LANES * 4
+AT_MEAN_1 = AT_CENTRE_FLIPPED + 3 * CHUNK * P * 4
+AT_DIFFERENCE = AT_MEAN_1 + CHANNELS * P * 4
+AT_MEAN_0 = AT_DIFFERENCE + 3 * WORK_BYTES
+AT_MEAN = AT_MEAN_0 + CHANNELS * P * 4
+AT_RESULT = AT_MEAN
 
 
-def quantise_image(nc, raw_image, padded, even_codes, even_scales):
+def lay_out_image(nc, raw_image, padded, first, last):
     nc.vector.tensor_copy(
-        out=padded[:, 1 : SIDE + 1, :, :], in_=raw_image[:].rearrange("p j h w -> p h w j")
+        out=padded[:, first + 1 : last + 1, :, :],
+        in_=raw_image[:, :, first:last, :].rearrange("p j h w -> p h w j"),
     )
-    flat = padded[:].rearrange("p r w j -> p (r w j)")
-    whole = SIDE * SIDE
-    rest = (PADDED_ROWS - SIDE) * SIDE
+
+
+def quantise_image(nc, padded, codes, scales, first, last):
     nc.vector.quantize_mx(
-        out=even_codes[:, 1, 0:whole].bitcast(FP8X4),
-        scales=even_scales[:, 1, 0:whole],
-        in_=flat[:, 0 : whole * PACK],
-    )
-    nc.vector.quantize_mx(
-        out=even_codes[:, 1, whole : whole + rest].bitcast(FP8X4),
-        scales=even_scales[:, 1, whole : whole + rest],
-        in_=flat[:, whole * PACK : (whole + rest) * PACK],
+        out=codes[:, 1, first * SIDE : last * SIDE].bitcast(FP8X4),
+        scales=scales[:, 1, first * SIDE : last * SIDE],
+        in_=padded[:, first:last, :, :].rearrange("p r w j -> p (r w j)"),
     )
 
 
@@ -107,7 +107,7 @@ def finish_shift(nc, kj, codes, even_scales, odd_scales):
     pixels = PADDED_ROWS * SIDE
     to, source = (slice(1, pixels), slice(0, pixels - 1)) if kj == 0 else (slice(0, pixels - 1), slice(1, pixels))
     empty = 0 if kj == 0 else SIDE - 1
-    nc.vector.memset(
+    nc.gpsimd.memset(
         codes[:, kj, :].bitcast(I32).rearrange("p (r w) -> p r w", w=SIDE)[:, :, empty : empty + 1], 0
     )
     nc.vector.tensor_copy(out=even_scales[:, kj, to], in_=even_scales[:, 1, source])
@@ -149,12 +149,9 @@ def tile_capsulelayer_kernel(tc, image, weight, bias, out):
         priors_0 = arena.tile([P, POSITIONS, CHANNELS, LANES], F32, offset=AT_PRIORS)
         priors_1 = arena.tile([P, POSITIONS, CHANNELS, LANES], F32, offset=AT_PRIORS + PRIOR_BYTES)
         priors_of = (priors_0, priors_1)
-        mean_flipped_0 = arena.tile([P, CHANNELS, P], F32, offset=AT_MEAN_FLIPPED)
-        mean_flipped_1 = arena.tile([P, CHANNELS, P], F32, offset=AT_MEAN_FLIPPED + CHANNELS * P * 4)
+        mean_flipped_0 = arena.tile([P, CHANNELS, P], F32, offset=AT_MEAN_0)
+        mean_flipped_1 = arena.tile([P, CHANNELS, P], F32, offset=AT_MEAN_1)
         mean_flipped_of = (mean_flipped_0, mean_flipped_1)
-        mean_0 = arena.tile([P, CHANNELS, LANES], F32, offset=AT_MEAN)
-        mean_1 = arena.tile([P, CHANNELS, LANES], F32, offset=AT_MEAN + CHANNELS * LANES * 4)
-        mean_of = (mean_0, mean_1)
         weight_codes = arena.tile(
             [P, POSITIONS, FEATURES], U32, align_bytes=64, offset=AT_WEIGHT_CODES
         )
@@ -174,7 +171,7 @@ def tile_capsulelayer_kernel(tc, image, weight, bias, out):
         identity = small.tile([P, P], F32, bufs=1)
         eps = small.tile([P, 1], F32, bufs=1)
 
-        products, prior_sums = {}, {}
+        products, prior_sums = {}, []
 
         def multiply(m, t):
             ki, kj = divmod(t, KERNEL)
@@ -184,7 +181,10 @@ def tile_capsulelayer_kernel(tc, image, weight, bias, out):
                 scales = odd_scales[:, kj, P * m : P * m + P]
             else:
                 scales = even_scales[:, kj, pixels]
-            product = banks.tile([P, CAPSULES, CHANNELS], F32, bufs=4, offset=4 * BANK)
+            if m < GROUP_TILES:
+                product = banks.tile([P, CAPSULES, CHANNELS], F32, bufs=4, offset=4 * BANK)
+            else:
+                product = banks.tile([P, CAPSULES, CHANNELS], F32, tag="late_product", bufs=3, offset=5 * BANK)
             products[(m, t)] = product
             nc.tensor.matmul_mx(
                 out=product[:].rearrange("p c e -> p (c e)"),
@@ -206,29 +206,27 @@ def tile_capsulelayer_kernel(tc, image, weight, bias, out):
                 op=ALU.add,
             )
 
-        def add_to_sum(g, t):
+        def add_to_sum(t):
             if t == POSITION_ORDER[0]:
-                prior_sum_0 = banks.tile([P, BANK_SLOTS, P], F32, offset=0)
-                prior_sum_1 = banks.tile([P, BANK_SLOTS, P], F32, offset=BANK)
-                prior_sum_2 = banks.tile([P, BANK_SLOTS, P], F32, offset=2 * BANK)
-                prior_sum_3 = banks.tile([P, BANK_SLOTS, P], F32, offset=3 * BANK)
-                prior_sums[g] = (prior_sum_0, prior_sum_1, prior_sum_2, prior_sum_3)
+                for q in range(CHANNELS // BANK_SLOTS):
+                    prior_sum = banks.tile([P, BANK_SLOTS, P], F32, tag="prior_sum%d" % q, offset=q * BANK)
+                    prior_sums.append(prior_sum)
             for e in range(CHANNELS):
                 q, slot = divmod(e, BANK_SLOTS)
                 nc.tensor.matmul(
-                    out=prior_sums[g][q][:, slot, :],
-                    lhsT=priors_of[g][:, t, e, :],
+                    out=prior_sums[q][:, slot, :],
+                    lhsT=priors_of[0][:, t, e, :],
                     rhs=identity[:],
                     is_transpose=True,
                     start=(t == POSITION_ORDER[0] and slot == 0),
                     stop=(t == POSITION_ORDER[-1] and slot == BANK_SLOTS - 1),
                 )
 
-        def mean_prior(g):
+        def mean_prior():
             for q in range(CHANNELS // BANK_SLOTS):
                 nc.scalar.activation(
-                    out=mean_flipped_of[g][:, BANK_SLOTS * q : BANK_SLOTS * q + BANK_SLOTS, :],
-                    in_=prior_sums[g][q][:],
+                    out=mean_flipped_0[:, BANK_SLOTS * q : BANK_SLOTS * q + BANK_SLOTS, :],
+                    in_=prior_sums[q][:],
                     func=ACT.Copy,
                     scale=1.0 / POSITIONS,
                 )
@@ -238,9 +236,12 @@ def tile_capsulelayer_kernel(tc, image, weight, bias, out):
             out=bias_table[0:POSITIONS, :], in_=bias[0, 0, 0].rearrange("i j o n -> (i j o) n")
         )
         raw_image = arena.tile([P, PACK, SIDE, SIDE], BF16, offset=AT_RAW_IMAGE)
-        nc.sync.dma_start(out=raw_image[:], in_=image[0].rearrange("(p j) h w -> p j h w", j=PACK))
+        image_view = image[0].rearrange("(p j) h w -> p j h w", j=PACK)
+        nc.sync.dma_start(out=raw_image[:, :, 0:TOP_ROWS, :], in_=image_view[:, :, 0:TOP_ROWS, :])
         raw_weight_of = {}
-        for t in POSITION_ORDER:
+        raw_weight_of[POSITION_ORDER[0]] = load_weight(nc, arena, weight, POSITION_ORDER[0])
+        nc.sync.dma_start(out=raw_image[:, :, TOP_ROWS:SIDE, :], in_=image_view[:, :, TOP_ROWS:SIDE, :])
+        for t in POSITION_ORDER[1:]:
             raw_weight_of[t] = load_weight(nc, arena, weight, t)
         make_identity(nc, selector[:])
         make_identity(nc, identity[:])
@@ -263,16 +264,11 @@ def tile_capsulelayer_kernel(tc, image, weight, bias, out):
             )
             engine_copy(out=bias_tile[:, t, :, :], in_=product[:].rearrange("p c e -> p e c"))
 
-        for i, t in enumerate(POSITION_ORDER[0:EARLY_BIASES]):
-            spread_bias(t, nc.vector.tensor_copy if i in (0, 2) else nc.scalar.copy)
-        quantise_image(nc, raw_image, padded, even_codes, even_scales)
-        move_codes(nc, even_codes, even_scales, odd_scales)
-        for t in POSITION_ORDER[EARLY_BIASES:]:
-            spread_bias(t, nc.vector.tensor_copy)
-        def add_and_close(g, t):
-            add_to_sum(g, t)
-            if t == POSITION_ORDER[-1]:
-                mean_prior(g)
+        spread_bias(POSITION_ORDER[0], nc.scalar.copy)
+        spread_bias(POSITION_ORDER[1], nc.scalar.copy)
+        lay_out_image(nc, raw_image, padded, 0, TOP_ROWS)
+        quantise_image(nc, padded, even_codes, even_scales, 0, WHOLE_ROWS)
+        quantise_image(nc, padded, even_codes, even_scales, WHOLE_ROWS, TOP_ROWS)
 
         def prepare(i):
             if i < POSITIONS:
@@ -283,20 +279,29 @@ def tile_capsulelayer_kernel(tc, image, weight, bias, out):
                 quantise_weight(nc, arena, raw_weight_of[t], t, weight_codes, weight_scales)
 
         prepare(0)
-        steps = [(g, t) for g in range(GROUPS) for t in POSITION_ORDER]
-        for i, (g, t) in enumerate(steps):
+        for i, t in enumerate(POSITION_ORDER):
             for lane in range(GROUP_TILES):
-                if i < POSITIONS and lane == 2:
+                if lane == GROUP_TILES // 2:
                     prepare(i + 1)
-                multiply(GROUP_TILES * g + lane, t)
-                add_bias(GROUP_TILES * g + lane, t)
+                multiply(lane, t)
+                add_bias(lane, t)
+            if i == 0:
+                spread_bias(POSITION_ORDER[2], nc.scalar.copy)
+                spread_bias(POSITION_ORDER[3], nc.scalar.copy)
+            if i == 0:
+                lay_out_image(nc, raw_image, padded, TOP_ROWS, SIDE)
+                quantise_image(nc, padded, even_codes, even_scales, TOP_ROWS, PADDED_ROWS)
+                move_codes(nc, even_codes, even_scales, odd_scales)
+            if 0 < i and i + 3 < POSITIONS:
+                spread_bias(POSITION_ORDER[i + 3], nc.scalar.copy)
             if i > 0:
-                add_and_close(*steps[i - 1])
+                add_to_sum(POSITION_ORDER[i - 1])
 
         items = [(s, g, k) for s in range(PHASES) for g in range(GROUPS) for k in range(CHUNKS)]
         count = len(items)
         first_weighed = GROUPS * CHUNKS
         weighed_of, total_of, centre_flipped_of, centre_of, difference_of = {}, {}, {}, {}, {}
+        mean_of, result_of = {}, {}
         distance_banks = {}
         pull_flipped_of, root_of, pull_bank_of, pull_sbuf_of, pull_psum_of, late_pull_of = {}, {}, {}, {}, {}, {}
 
@@ -314,6 +319,16 @@ def tile_capsulelayer_kernel(tc, image, weight, bias, out):
             if g == 0 and k < STILL_SUBTRACTING:
                 return MIDDLE_SHARES[0]
             return LAST_SHARE if g == 1 or k >= LATE_FROM else FIRST_IN_PSUM
+
+        def gpsimd_subtracts(i):
+            if i + 3 < POSITIONS:
+                return EARLY_SUBTRACTS
+            return LATE_SUBTRACTS if i < CHUNKS else 0
+
+        def gpsimd_squares(i):
+            if i + 3 < POSITIONS:
+                return EARLY_SQUARES
+            return LATE_SQUARES if i + 3 < first_weighed else 0
 
         def weigh_gpsimd(i):
             s, g, k = items[i]
@@ -347,15 +362,18 @@ def tile_capsulelayer_kernel(tc, image, weight, bias, out):
 
         def sum_positions(i):
             s, g, k = items[i]
-            if s == PHASES - 1 and i % 2 == 1:
+            if s == 0:
+                weighted_sum = banks.tile([P, BANK_SLOTS, P], F32, tag="mean_sum", offset=5 * BANK)
+            elif s == PHASES - 1 and i % 2 == 1:
                 weighted_sum = banks.tile([P, BANK_SLOTS, P], F32, tag="centre", bufs=2, offset=6 * BANK)
             else:
                 weighted_sum = banks.tile([P, BANK_SLOTS, P], F32, offset=3 * BANK)
             total_of[i] = weighted_sum
             for c in range(CHUNK):
-                blocks = [weighed_of[i][:, t, c, :] for t in range(WEIGHED)]
-                if s == PHASES - 1:
-                    blocks = [mean_of[g][:, CHUNK * k + c, :]] + blocks
+                if s == 0:
+                    blocks = [chunk_priors(i)[:, t, c, :] for t in range(POSITIONS)]
+                else:
+                    blocks = [weighed_of[i][:, t, c, :] for t in range(WEIGHED)]
                 add_flipped(weighted_sum[:, c, :], blocks)
 
         def add_flipped(out_block, blocks):
@@ -370,14 +388,29 @@ def tile_capsulelayer_kernel(tc, image, weight, bias, out):
                 )
 
         def empty_sum(i):
-            if items[i][0] == PHASES - 1:
-                centre_flipped = arena.tile([P, CHUNK, P], F32, bufs=4, tag="result", offset=AT_RESULT)
-            else:
-                centre_flipped = arena.tile(
-                    [P, CHUNK, P], F32, bufs=3, tag="centre_flipped", offset=AT_CENTRE_FLIPPED
+            s, g, k = items[i]
+            if s == 0:
+                nc.scalar.activation(
+                    out=mean_flipped_of[g][:, CHUNK * k : CHUNK * k + CHUNK, :],
+                    in_=total_of[i][:, 0:CHUNK, :],
+                    func=ACT.Copy,
+                    scale=1.0 / POSITIONS,
                 )
-            centre_flipped_of[i] = centre_flipped
-            nc.scalar.copy(out=centre_flipped[:], in_=total_of[i][:, 0:CHUNK, :])
+            else:
+                centre_flipped = arena.tile([P, CHUNK, P], F32, bufs=3, offset=AT_CENTRE_FLIPPED)
+                centre_flipped_of[i] = centre_flipped
+                nc.scalar.copy(out=centre_flipped[:], in_=total_of[i][:, 0:CHUNK, :])
+
+        def finish(i):
+            s, g, k = items[i]
+            result = arena.tile([P, CHUNK, P], F32, bufs=4, offset=AT_RESULT)
+            result_of[i] = result
+            nc.vector.tensor_tensor(
+                out=result[:],
+                in0=total_of[i][:, 0:CHUNK, :],
+                in1=mean_flipped_of[g][:, CHUNK * k : CHUNK * k + CHUNK, :],
+                op=ALU.add,
+            )
 
         def store(i):
             s, g, k = items[i]
@@ -385,12 +418,15 @@ def tile_capsulelayer_kernel(tc, image, weight, bias, out):
                 m = GROUP_TILES * g + lane
                 nc.sync.dma_start(
                     out=out_view[:, CHUNK * k : CHUNK * k + CHUNK, P * m : P * m + P],
-                    in_=centre_flipped_of[i][CAPSULES * lane : CAPSULES * lane + CAPSULES, :, :],
+                    in_=result_of[i][CAPSULES * lane : CAPSULES * lane + CAPSULES, :, :],
                 )
 
         def flip_centre(i):
             s, g, k = items[i]
-            centre = banks.tile([P, BANK_SLOTS, LANES], F32, bufs=2, offset=6 * BANK)
+            if s == 0 and g == 0:
+                centre = banks.tile([P, BANK_SLOTS, LANES], F32, tag="early_centre", bufs=2, offset=3 * BANK)
+            else:
+                centre = banks.tile([P, BANK_SLOTS, LANES], F32, tag="centre", bufs=2, offset=6 * BANK)
             centre_of[i] = centre
             for c in range(CHUNK):
                 if s == 0:
@@ -400,17 +436,16 @@ def tile_capsulelayer_kernel(tc, image, weight, bias, out):
                 nc.tensor.transpose(out=centre[:, c, :], in_=flipped, identity=identity[:])
 
         def keep_mean(i):
-            s, g, k = items[i]
-            nc.scalar.copy(
-                out=mean_of[g][:, CHUNK * k : CHUNK * k + CHUNK, :], in_=centre_of[i][:, 0:CHUNK, :]
-            )
+            mean = arena.tile([P, CHUNK, LANES], F32, bufs=3, offset=AT_MEAN)
+            mean_of[i] = mean
+            nc.scalar.copy(out=mean[:], in_=centre_of[i][:, 0:CHUNK, :])
 
         def subtract(i):
             s, g, k = items[i]
             difference = arena.tile([P, POSITIONS, CHUNK, LANES], F32, bufs=3, offset=AT_DIFFERENCE)
             difference_of[i] = difference
             target = chunk_priors(i) if s == 0 else difference
-            n = POSITIONS - GPSIMD_SUBTRACTS if i + 3 < first_weighed else POSITIONS
+            n = POSITIONS - gpsimd_subtracts(i)
             nc.vector.tensor_tensor(
                 out=target[:, 0:n, :, :],
                 in0=chunk_priors(i)[:, 0:n, :, :],
@@ -421,24 +456,24 @@ def tile_capsulelayer_kernel(tc, image, weight, bias, out):
                 nc.gpsimd.tensor_tensor(
                     out=target[:, n:POSITIONS, :, :],
                     in0=chunk_priors(i)[:, n:POSITIONS, :, :],
-                    in1=mean_of[g][:, CHUNK * k : CHUNK * k + CHUNK, :]
+                    in1=mean_of[i][:]
                     .unsqueeze(1)
                     .to_broadcast([P, POSITIONS - n, CHUNK, LANES]),
                     op=ALU.subtract,
                 )
 
-        def square(i):
+        def square(i, first, last):
             s, g, k = items[i]
             source = chunk_priors(i) if s == 0 else difference_of[i]
-            n = POSITIONS - GPSIMD_SQUARES if i + 3 < first_weighed else POSITIONS
+            n = min(last, POSITIONS - gpsimd_squares(i))
             nc.scalar.activation(
-                out=difference_of[i][:, 0:n, :, :], in_=source[:, 0:n, :, :], func=ACT.Square
+                out=difference_of[i][:, first:n, :, :], in_=source[:, first:n, :, :], func=ACT.Square
             )
-            if n < POSITIONS:
+            if n < last:
                 nc.gpsimd.tensor_tensor(
-                    out=difference_of[i][:, n:POSITIONS, :, :],
-                    in0=source[:, n:POSITIONS, :, :],
-                    in1=source[:, n:POSITIONS, :, :],
+                    out=difference_of[i][:, n:last, :, :],
+                    in0=source[:, n:last, :, :],
+                    in1=source[:, n:last, :, :],
                     op=ALU.mult,
                 )
 
@@ -545,42 +580,56 @@ def tile_capsulelayer_kernel(tc, image, weight, bias, out):
             return None
 
         for turn in range(count + 9):
+            late = POSITION_ORDER[turn] if turn < POSITIONS else None
             if at(turn)[0] >= 1:
                 weigh_gpsimd(turn)
             if 0 <= at(turn - 2)[0] < PHASES - 1:
                 flip_centre(turn - 2)
-                if at(turn - 2)[0] == 0:
+                if at(turn - 2)[0] == 0 and gpsimd_subtracts(turn - 2) > 0:
                     keep_mean(turn - 2)
-            if turn == 2:
-                add_and_close(*steps[-1])
-            if at(turn - 1)[0] >= 1:
+            if late is not None:
+                for lane in range(GROUP_TILES):
+                    multiply(GROUP_TILES + lane, late)
+                    if lane < GROUP_TILES // 2:
+                        add_bias(GROUP_TILES + lane, late)
+            if turn == 0:
+                add_to_sum(POSITION_ORDER[-1])
+                mean_prior()
+            if at(turn - 1)[0:2] == (0, 1) or at(turn - 1)[0] >= 1:
                 sum_positions(turn - 1)
-            if phase_end(turn, 5):
-                pulls(*phase_end(turn, 5))
             if phase_end(turn, 6):
                 invert_sum(*phase_end(turn, 6))
                 flip_scale(*phase_end(turn, 6))
-            if at(turn - 1)[0] >= 1:
-                empty_sum(turn - 1)
-                if at(turn - 1)[0] == PHASES - 1:
-                    store(turn - 1)
-            if phase_end(turn, 7):
-                normalise_pulls(*phase_end(turn, 7))
-                flip_first_pulls(*phase_end(turn, 7))
-                copy_first_pulls(*phase_end(turn, 7))
-            if phase_end(turn, 8):
-                flip_second_pulls(*phase_end(turn, 8))
-                copy_second_pulls(*phase_end(turn, 8))
             if phase_end(turn, 6) == (PHASES - 1, 1):
                 flip_late_pull(PHASES - 1, 0)
             if phase_end(turn, 8) == (PHASES - 1, 1):
                 flip_late_pull(PHASES - 1, 1)
+            if phase_end(turn, 8):
+                flip_second_pulls(*phase_end(turn, 8))
+                copy_second_pulls(*phase_end(turn, 8))
+            if at(turn - 1)[0:2] == (0, 1) or 1 <= at(turn - 1)[0] < PHASES - 1:
+                empty_sum(turn - 1)
             if 0 <= at(turn - 3)[0] < PHASES - 1:
                 subtract(turn - 3)
-                square(turn - 3)
+                square(turn - 3, 0, 5)
+            if phase_end(turn, 7):
+                normalise_pulls(*phase_end(turn, 7))
+            if phase_end(turn, 7):
+                flip_first_pulls(*phase_end(turn, 7))
+                copy_first_pulls(*phase_end(turn, 7))
+            if late is not None:
+                for lane in range(GROUP_TILES // 2, GROUP_TILES):
+                    add_bias(GROUP_TILES + lane, late)
             if 0 <= at(turn - 4)[0] < PHASES - 1:
                 sum_channels(turn - 4)
+            if phase_end(turn, 4):
+                pulls(*phase_end(turn, 4))
+            if 0 <= at(turn - 3)[0] < PHASES - 1:
+                square(turn - 3, 5, POSITIONS)
             if phase_end(turn, 5):
                 sum_pulls(*phase_end(turn, 5))
             if at(turn)[0] >= 1:
                 weigh_vector(turn)
+            if at(turn - 1)[0] == PHASES - 1:
+                finish(turn - 1)
+                store(turn - 1)

@@ -43,6 +43,7 @@ EARLY_SUBTRACTS = 6
 EARLY_SQUARES = 0
 LATE_SUBTRACTS = 2
 LATE_SQUARES = 2
+CLOSING_PRODUCTS = 3
 POSITION_ORDER = (1, 7, 4, 0, 6, 3, 2, 8, 5)
 TOP_ROWS = 18
 WHOLE_ROWS = 16
@@ -573,6 +574,10 @@ def tile_capsulelayer_kernel(tc, image, weight, bias, out):
             late_pull_of[(s, g)] = late_pull
             flip_pulls(s, g, LAST_SHARE, FIRST_IN_PSUM, late_pull)
 
+        def keep_busy(bank, n):
+            for i in range(n):
+                nc.tensor.matmul(out=bank[:, 0, :], lhsT=identity[:], rhs=identity[:], start=True, stop=True)
+
         def phase_end(turn, lag):
             s, g, k = at(turn - lag)
             if 0 <= s < PHASES - 1 and k == CHUNKS - 1:
@@ -597,6 +602,9 @@ def tile_capsulelayer_kernel(tc, image, weight, bias, out):
                 mean_prior()
             if at(turn - 1)[0:2] == (0, 1) or at(turn - 1)[0] >= 1:
                 sum_positions(turn - 1)
+                if turn > count - GROUPS * CHUNKS + 4:
+                    idle_bank = banks.tile([P, BANK_SLOTS, P], F32, offset=2 * BANK)
+                    keep_busy(idle_bank, 1)
             if phase_end(turn, 6):
                 invert_sum(*phase_end(turn, 6))
                 flip_scale(*phase_end(turn, 6))
@@ -620,6 +628,8 @@ def tile_capsulelayer_kernel(tc, image, weight, bias, out):
             if late is not None:
                 for lane in range(GROUP_TILES // 2, GROUP_TILES):
                     add_bias(GROUP_TILES + lane, late)
+            if phase_end(turn, 5):
+                keep_busy(take_pull_bank(*phase_end(turn, 5)), CLOSING_PRODUCTS)
             if 0 <= at(turn - 4)[0] < PHASES - 1:
                 sum_channels(turn - 4)
             if phase_end(turn, 4):

@@ -41,8 +41,10 @@ LATE_FROM = 6
 STILL_SUBTRACTING = 3
 EARLY_SUBTRACTS = 6
 EARLY_SQUARES = 0
-LATE_SUBTRACTS = 2
-LATE_SQUARES = 2
+LATE_SUBTRACTS = 1
+LATE_SQUARES = 1
+PAIRS = 3
+PAIR_STEP = 4
 CLOSING_PRODUCTS = 3
 POSITION_ORDER = (1, 7, 4, 0, 6, 3, 2, 8, 5)
 TOP_ROWS = 18
@@ -67,6 +69,7 @@ AT_EVEN_SCALES = AT_EVEN_CODES + KERNEL * PADDED_ROWS * SIDE * 4
 AT_ODD_SCALES = AT_EVEN_SCALES + KERNEL * PADDED_ROWS * SIDE
 AT_BIAS = AT_ODD_SCALES + KERNEL * SIDE * SIDE
 AT_WEIGHED = AT_REST
+AT_PAIRED = AT_WEIGHED + WORK_BYTES
 AT_PULL_FLIPPED = AT_WEIGHED + 3 * WORK_BYTES
 AT_PULL = AT_PULL_FLIPPED + 2 * POSITIONS * LANES * 4
 AT_PULL_SUM = AT_PULL + 2 * IN_SBUF * LANES * 4
@@ -266,7 +269,6 @@ def tile_capsulelayer_kernel(tc, image, weight, bias, out):
             engine_copy(out=bias_tile[:, t, :, :], in_=product[:].rearrange("p c e -> p e c"))
 
         spread_bias(POSITION_ORDER[0], nc.scalar.copy)
-        spread_bias(POSITION_ORDER[1], nc.scalar.copy)
         lay_out_image(nc, raw_image, padded, 0, TOP_ROWS)
         quantise_image(nc, padded, even_codes, even_scales, 0, WHOLE_ROWS)
         quantise_image(nc, padded, even_codes, even_scales, WHOLE_ROWS, TOP_ROWS)
@@ -280,6 +282,7 @@ def tile_capsulelayer_kernel(tc, image, weight, bias, out):
                 quantise_weight(nc, arena, raw_weight_of[t], t, weight_codes, weight_scales)
 
         prepare(0)
+        spread_bias(POSITION_ORDER[1], nc.scalar.copy)
         for i, t in enumerate(POSITION_ORDER):
             for lane in range(GROUP_TILES):
                 if lane == GROUP_TILES // 2:
@@ -303,7 +306,7 @@ def tile_capsulelayer_kernel(tc, image, weight, bias, out):
         first_weighed = GROUPS * CHUNKS
         weighed_of, total_of, centre_flipped_of, centre_of, difference_of = {}, {}, {}, {}, {}
         mean_of, result_of = {}, {}
-        distance_banks = {}
+        distance_banks, paired_of = {}, {}
         pull_flipped_of, root_of, pull_bank_of, pull_sbuf_of, pull_psum_of, late_pull_of = {}, {}, {}, {}, {}, {}
 
         def at(i):
@@ -330,6 +333,21 @@ def tile_capsulelayer_kernel(tc, image, weight, bias, out):
             if i + 3 < POSITIONS:
                 return EARLY_SQUARES
             return LATE_SQUARES if i + 3 < first_weighed else 0
+
+        def gpsimd_pairs(i):
+            return PAIRS if CHUNKS < i < first_weighed else 0
+
+        def add_pairs(i):
+            n = gpsimd_pairs(i)
+            if n > 0:
+                paired = arena.tile([P, PAIRS, CHUNK, LANES], F32, bufs=2, offset=AT_PAIRED)
+                paired_of[i] = paired
+                nc.gpsimd.tensor_tensor(
+                    out=paired[:],
+                    in0=chunk_priors(i)[:, 0:n, :, :],
+                    in1=chunk_priors(i)[:, PAIR_STEP : PAIR_STEP + n, :, :],
+                    op=ALU.add,
+                )
 
         def weigh_gpsimd(i):
             s, g, k = items[i]
@@ -372,7 +390,10 @@ def tile_capsulelayer_kernel(tc, image, weight, bias, out):
             total_of[i] = weighted_sum
             for c in range(CHUNK):
                 if s == 0:
-                    blocks = [chunk_priors(i)[:, t, c, :] for t in range(POSITIONS)]
+                    n = gpsimd_pairs(i)
+                    singles = [t for t in range(POSITIONS) if t % PAIR_STEP >= n or t >= 2 * PAIR_STEP]
+                    blocks = [chunk_priors(i)[:, t, c, :] for t in singles]
+                    blocks = [paired_of[i][:, j, c, :] for j in range(n)] + blocks
                 else:
                     blocks = [weighed_of[i][:, t, c, :] for t in range(WEIGHED)]
                 add_flipped(weighted_sum[:, c, :], blocks)
@@ -478,14 +499,14 @@ def tile_capsulelayer_kernel(tc, image, weight, bias, out):
                     op=ALU.mult,
                 )
 
-        def sum_channels(i):
+        def sum_channels(i, first, last):
             s, g, k = items[i]
-            if k == 0:
+            if k == 0 and first == 0:
                 distance_0 = banks.tile([P, BANK_SLOTS, P], F32, offset=0)
                 distance_1 = banks.tile([P, BANK_SLOTS, P], F32, offset=BANK)
                 distance_2 = banks.tile([P, BANK_SLOTS, P], F32, offset=2 * BANK)
                 distance_banks[(s, g)] = (distance_0, distance_1, distance_2)
-            for t in range(POSITIONS):
+            for t in range(first, last):
                 b, slot = divmod(t, BANK_SLOTS)
                 last_slot = slot == BANK_SLOTS - 1 or t == POSITIONS - 1
                 for c in range(CHUNK):
@@ -586,6 +607,8 @@ def tile_capsulelayer_kernel(tc, image, weight, bias, out):
 
         for turn in range(count + 9):
             late = POSITION_ORDER[turn] if turn < POSITIONS else None
+            if at(turn)[0:2] == (0, 1):
+                add_pairs(turn)
             if at(turn)[0] >= 1:
                 weigh_gpsimd(turn)
             if 0 <= at(turn - 2)[0] < PHASES - 1:
@@ -628,10 +651,11 @@ def tile_capsulelayer_kernel(tc, image, weight, bias, out):
             if late is not None:
                 for lane in range(GROUP_TILES // 2, GROUP_TILES):
                     add_bias(GROUP_TILES + lane, late)
-            if phase_end(turn, 5):
-                keep_busy(take_pull_bank(*phase_end(turn, 5)), CLOSING_PRODUCTS)
             if 0 <= at(turn - 4)[0] < PHASES - 1:
-                sum_channels(turn - 4)
+                sum_channels(turn - 4, 0, 5)
+                if phase_end(turn, 5):
+                    keep_busy(take_pull_bank(*phase_end(turn, 5)), CLOSING_PRODUCTS)
+                sum_channels(turn - 4, 5, POSITIONS)
             if phase_end(turn, 4):
                 pulls(*phase_end(turn, 4))
             if 0 <= at(turn - 3)[0] < PHASES - 1:

@@ -132,7 +132,10 @@ def load_weight(nc, arena, weight, t):
 
 def quantise_weight(nc, arena, raw_weight, t, weight_codes, weight_scales):
     grouped = arena.tile([P, FEATURES, PACK], BF16, align_bytes=64, bufs=2, offset=AT_GROUPED)
-    nc.scalar.copy(out=grouped[:], in_=raw_weight[:].rearrange("p j n -> p n j"))
+    nc.scalar.copy(
+        out=grouped[:].rearrange("p (c i) j -> p c j i", i=4),
+        in_=raw_weight[:].rearrange("p j (c i) -> p c j i", i=4),
+    )
     nc.vector.quantize_mx(
         out=weight_codes[:, t, :].bitcast(FP8X4),
         scales=weight_scales[:, t, :],
@@ -625,12 +628,13 @@ def tile_capsulelayer_kernel(tc, image, weight, bias, out):
                 mean_prior()
             if at(turn - 1)[0:2] == (0, 1) or at(turn - 1)[0] >= 1:
                 sum_positions(turn - 1)
-                if turn > count - GROUPS * CHUNKS + 4:
-                    idle_bank = banks.tile([P, BANK_SLOTS, P], F32, offset=2 * BANK)
-                    keep_busy(idle_bank, 1)
             if phase_end(turn, 6):
                 invert_sum(*phase_end(turn, 6))
-                flip_scale(*phase_end(turn, 6))
+                if at(turn - 4)[0] == PHASES - 1:
+                    flip_scale(*phase_end(turn, 6))
+            if turn > count - GROUPS * CHUNKS + 4 and at(turn - 1)[0] >= 0:
+                idle_bank = banks.tile([P, BANK_SLOTS, P], F32, offset=2 * BANK)
+                keep_busy(idle_bank, 1)
             if phase_end(turn, 6) == (PHASES - 1, 1):
                 flip_late_pull(PHASES - 1, 0)
             if phase_end(turn, 8) == (PHASES - 1, 1):
@@ -655,6 +659,8 @@ def tile_capsulelayer_kernel(tc, image, weight, bias, out):
                 sum_channels(turn - 4, 0, 5)
                 if phase_end(turn, 5):
                     keep_busy(take_pull_bank(*phase_end(turn, 5)), CLOSING_PRODUCTS)
+                if phase_end(turn, 6):
+                    flip_scale(*phase_end(turn, 6))
                 sum_channels(turn - 4, 5, POSITIONS)
             if phase_end(turn, 4):
                 pulls(*phase_end(turn, 4))

@@ -43,9 +43,10 @@ EARLY_SUBTRACTS = 6
 EARLY_SQUARES = 0
 LATE_SUBTRACTS = 1
 LATE_SQUARES = 1
+WARM_UP_PRODUCTS = 5
 PAIRS = 3
 PAIR_STEP = 4
-CLOSING_PRODUCTS = 3
+CLOSING_PRODUCTS = 2
 POSITION_ORDER = (1, 7, 4, 0, 6, 3, 2, 8, 5)
 TOP_ROWS = 18
 WHOLE_ROWS = 16
@@ -285,6 +286,9 @@ def tile_capsulelayer_kernel(tc, image, weight, bias, out):
                 quantise_weight(nc, arena, raw_weight_of[t], t, weight_codes, weight_scales)
 
         prepare(0)
+        warm_up = banks.tile([P, BANK_SLOTS, P], F32, offset=0)
+        for i in range(WARM_UP_PRODUCTS):
+            nc.tensor.matmul(out=warm_up[:, 0, :], lhsT=identity[:], rhs=identity[:], start=True, stop=True)
         spread_bias(POSITION_ORDER[1], nc.scalar.copy)
         for i, t in enumerate(POSITION_ORDER):
             for lane in range(GROUP_TILES):

@@ -11,7 +11,6 @@ I32 = mybir.dt.int32
 FP8X4 = mybir.dt.float8_e4m3fn_x4
 ALU = mybir.AluOpType
 ACT = mybir.ActivationFunctionType
-X_AXIS = mybir.AxisListType.X
 
 P = 128
 PACK = 4
@@ -32,24 +31,24 @@ CHUNKS = CHANNELS // CHUNK
 PHASES = 4
 BANK_SLOTS = 4
 BANK = 2048
-WEIGHED = POSITIONS - 1
-FIRST_IN_PSUM = 4
-MIDDLE_SHARES = (4, 6, 6, 5, 6, 5, 6, 6)
-IN_SBUF = 6
-LAST_SHARE = 3
-LATE_FROM = 6
-STILL_SUBTRACTING = 3
-EARLY_SUBTRACTS = 6
-EARLY_SQUARES = 0
-LATE_SUBTRACTS = 1
-LATE_SQUARES = 1
-WARM_UP_PRODUCTS = 5
-PAIRS = 3
-PAIR_STEP = 4
-CLOSING_PRODUCTS = 2
+
 POSITION_ORDER = (1, 7, 4, 0, 6, 3, 2, 8, 5)
 TOP_ROWS = 18
 WHOLE_ROWS = 16
+
+WEIGHED = POSITIONS - 1
+FIRST_IN_PSUM = 4
+IN_SBUF = 6
+LAST_SHARE = 3
+LATE_PULL_FROM = 6
+EARLY_SUBTRACTS = 6
+LATE_SUBTRACTS = 1
+LATE_SQUARES = 1
+PAIRS = 3
+PAIR_STEP = 4
+SPLIT = 5
+WARM_UP_PRODUCTS = 5
+CLOSING_PRODUCTS = 3
 
 FLOPS = 2 * POSITIONS * SIDE * SIDE * (P * PACK) * FEATURES
 
@@ -61,25 +60,25 @@ AT_PADDED = AT_RAW_IMAGE + PACK * SIDE * SIDE * 2
 AT_RAW_WEIGHT = AT_PADDED + PADDED_ROWS * SIDE * PACK * 2
 AT_GROUPED = AT_RAW_WEIGHT + POSITIONS * PACK * FEATURES * 2
 AT_BIAS_TABLE = AT_GROUPED + 2 * PACK * FEATURES * 2
-AT_ONES = AT_BIAS_TABLE + FEATURES * 2
+AT_SELECTOR = AT_BIAS_TABLE + (FEATURES + P) * 2
 AT_REST = 2 * PRIOR_BYTES
 AT_WEIGHT_CODES = AT_REST
 AT_WEIGHT_SCALES = AT_WEIGHT_CODES + POSITIONS * FEATURES * 4
-AT_EVEN_CODES = AT_WEIGHT_SCALES + POSITIONS * FEATURES
-AT_EVEN_SCALES = AT_EVEN_CODES + KERNEL * PADDED_ROWS * SIDE * 4
+AT_CODES = AT_WEIGHT_SCALES + POSITIONS * FEATURES
+AT_EVEN_SCALES = AT_CODES + KERNEL * PADDED_ROWS * SIDE * 4
 AT_ODD_SCALES = AT_EVEN_SCALES + KERNEL * PADDED_ROWS * SIDE
 AT_BIAS = AT_ODD_SCALES + KERNEL * SIDE * SIDE
 AT_WEIGHED = AT_REST
 AT_PAIRED = AT_WEIGHED + WORK_BYTES
 AT_PULL_FLIPPED = AT_WEIGHED + 3 * WORK_BYTES
-AT_PULL = AT_PULL_FLIPPED + 2 * POSITIONS * LANES * 4
-AT_PULL_SUM = AT_PULL + 2 * IN_SBUF * LANES * 4
-AT_CENTRE_FLIPPED = AT_PULL_SUM + 2 * LANES * 4
+AT_PULL = AT_PULL_FLIPPED + 2 * POSITIONS * P * 4
+AT_ROOT = AT_PULL + 2 * IN_SBUF * LANES * 4
+AT_CENTRE_FLIPPED = AT_ROOT + 2 * LANES * 4
 AT_MEAN_1 = AT_CENTRE_FLIPPED + 3 * CHUNK * P * 4
 AT_DIFFERENCE = AT_MEAN_1 + CHANNELS * P * 4
 AT_MEAN_0 = AT_DIFFERENCE + 3 * WORK_BYTES
-AT_MEAN = AT_MEAN_0 + CHANNELS * P * 4
-AT_RESULT = AT_MEAN
+AT_MEAN_CHUNK = AT_MEAN_0 + CHANNELS * P * 4
+AT_RESULT = AT_MEAN_CHUNK
 
 
 def lay_out_image(nc, raw_image, padded, first, last):
@@ -89,10 +88,10 @@ def lay_out_image(nc, raw_image, padded, first, last):
     )
 
 
-def quantise_image(nc, padded, codes, scales, first, last):
+def quantise_image(nc, padded, codes, even_scales, first, last):
     nc.vector.quantize_mx(
         out=codes[:, 1, first * SIDE : last * SIDE].bitcast(FP8X4),
-        scales=scales[:, 1, first * SIDE : last * SIDE],
+        scales=even_scales[:, 1, first * SIDE : last * SIDE],
         in_=padded[:, first:last, :, :].rearrange("p r w j -> p (r w j)"),
     )
 
@@ -110,8 +109,10 @@ def move_codes(nc, codes, even_scales, odd_scales):
 
 def finish_shift(nc, kj, codes, even_scales, odd_scales):
     pixels = PADDED_ROWS * SIDE
-    to, source = (slice(1, pixels), slice(0, pixels - 1)) if kj == 0 else (slice(0, pixels - 1), slice(1, pixels))
-    empty = 0 if kj == 0 else SIDE - 1
+    if kj == 0:
+        to, source, empty = slice(1, pixels), slice(0, pixels - 1), 0
+    else:
+        to, source, empty = slice(0, pixels - 1), slice(1, pixels), SIDE - 1
     nc.gpsimd.memset(
         codes[:, kj, :].bitcast(I32).rearrange("p (r w) -> p r w", w=SIDE)[:, :, empty : empty + 1], 0
     )
@@ -151,7 +152,7 @@ def tile_capsulelayer_kernel(tc, image, weight, bias, out):
     with ExitStack() as stack:
         stack.enter_context(tc.manual_schedule())
         arena = stack.enter_context(tc.tile_pool(name="arena", bufs=1))
-        small = stack.enter_context(tc.tile_pool(name="small", bufs=2))
+        small = stack.enter_context(tc.tile_pool(name="small", bufs=1))
         banks = stack.enter_context(tc.psum_pool(name="banks", bufs=1))
 
         priors_0 = arena.tile([P, POSITIONS, CHANNELS, LANES], F32, offset=AT_PRIORS)
@@ -160,43 +161,34 @@ def tile_capsulelayer_kernel(tc, image, weight, bias, out):
         mean_flipped_0 = arena.tile([P, CHANNELS, P], F32, offset=AT_MEAN_0)
         mean_flipped_1 = arena.tile([P, CHANNELS, P], F32, offset=AT_MEAN_1)
         mean_flipped_of = (mean_flipped_0, mean_flipped_1)
-        weight_codes = arena.tile(
-            [P, POSITIONS, FEATURES], U32, align_bytes=64, offset=AT_WEIGHT_CODES
-        )
-        weight_scales = arena.tile(
-            [P, POSITIONS, FEATURES], U8, align_bytes=64, offset=AT_WEIGHT_SCALES
-        )
-        even_codes = arena.tile(
-            [P, KERNEL, PADDED_ROWS * SIDE], U32, align_bytes=64, offset=AT_EVEN_CODES
-        )
-        even_scales = arena.tile(
-            [P, KERNEL, PADDED_ROWS * SIDE], U8, align_bytes=64, offset=AT_EVEN_SCALES
-        )
+        weight_codes = arena.tile([P, POSITIONS, FEATURES], U32, align_bytes=64, offset=AT_WEIGHT_CODES)
+        weight_scales = arena.tile([P, POSITIONS, FEATURES], U8, align_bytes=64, offset=AT_WEIGHT_SCALES)
+        codes = arena.tile([P, KERNEL, PADDED_ROWS * SIDE], U32, align_bytes=64, offset=AT_CODES)
+        even_scales = arena.tile([P, KERNEL, PADDED_ROWS * SIDE], U8, align_bytes=64, offset=AT_EVEN_SCALES)
         odd_scales = arena.tile([P, KERNEL, SIDE * SIDE], U8, align_bytes=64, offset=AT_ODD_SCALES)
         bias_tile = arena.tile([P, POSITIONS, CHANNELS, CAPSULES], BF16, offset=AT_BIAS)
-        selector = arena.tile([P, P], BF16, offset=AT_ONES + P * 2)
+        selector = arena.tile([P, P], BF16, offset=AT_SELECTOR)
         bias_table = arena.tile([P, FEATURES], BF16, offset=AT_BIAS_TABLE)
-        identity = small.tile([P, P], F32, bufs=1)
-        eps = small.tile([P, 1], F32, bufs=1)
+        identity = small.tile([P, P], F32)
+        eps = small.tile([P, 1], F32)
 
         products, prior_sums = {}, []
 
         def multiply(m, t):
             ki, kj = divmod(t, KERNEL)
-            pixels = slice(P * m + SIDE * ki, P * m + SIDE * ki + P)
-            codes = even_codes[:, kj, pixels]
+            window = slice(P * m + SIDE * ki, P * m + SIDE * ki + P)
             if ki == 1:
                 scales = odd_scales[:, kj, P * m : P * m + P]
             else:
-                scales = even_scales[:, kj, pixels]
+                scales = even_scales[:, kj, window]
             if m < GROUP_TILES:
-                product = banks.tile([P, CAPSULES, CHANNELS], F32, bufs=4, offset=4 * BANK)
+                product = banks.tile([P, CAPSULES, CHANNELS], F32, tag="product", bufs=4, offset=4 * BANK)
             else:
                 product = banks.tile([P, CAPSULES, CHANNELS], F32, tag="late_product", bufs=3, offset=5 * BANK)
             products[(m, t)] = product
             nc.tensor.matmul_mx(
                 out=product[:].rearrange("p c e -> p (c e)"),
-                lhsT=codes.bitcast(FP8X4),
+                lhsT=codes[:, kj, window].bitcast(FP8X4),
                 lhsT_scale=scales,
                 rhs=weight_codes[:, t, :].bitcast(FP8X4),
                 rhs_scale=weight_scales[:, t, :],
@@ -205,8 +197,8 @@ def tile_capsulelayer_kernel(tc, image, weight, bias, out):
             )
 
         def add_bias(m, t):
-            g, lane = divmod(m, GROUP_TILES)
-            lanes = slice(CAPSULES * lane, CAPSULES * lane + CAPSULES)
+            g, tile = divmod(m, GROUP_TILES)
+            lanes = slice(CAPSULES * tile, CAPSULES * tile + CAPSULES)
             nc.vector.tensor_tensor(
                 out=priors_of[g][:, t, :, lanes],
                 in0=products[(m, t)][:].rearrange("p c e -> p e c"),
@@ -239,6 +231,29 @@ def tile_capsulelayer_kernel(tc, image, weight, bias, out):
                     scale=1.0 / POSITIONS,
                 )
 
+        def keep_busy(bank, n):
+            for j in range(n):
+                nc.tensor.matmul(out=bank[:, 0, :], lhsT=identity[:], rhs=identity[:], start=True, stop=True)
+
+        def spread_bias(t):
+            product = banks.tile([P, CAPSULES, CHANNELS], F32, tag="product", bufs=4, offset=4 * BANK)
+            nc.tensor.matmul(
+                out=product[:].rearrange("p c e -> p (c e)"),
+                lhsT=selector[:, t : t + 1].to_broadcast([P, P]),
+                rhs=bias_table[:],
+                start=True,
+                stop=True,
+            )
+            nc.scalar.copy(out=bias_tile[:, t, :, :], in_=product[:].rearrange("p c e -> p e c"))
+
+        def prepare(i):
+            if i < POSITIONS:
+                t = POSITION_ORDER[i]
+                ki, kj = divmod(t, KERNEL)
+                if ki == 0 and kj != 1:
+                    finish_shift(nc, kj, codes, even_scales, odd_scales)
+                quantise_weight(nc, arena, raw_weight_of[t], t, weight_codes, weight_scales)
+
         nc.vector.memset(bias_table[:], 0.0)
         nc.sync.dma_start(
             out=bias_table[0:POSITIONS, :], in_=bias[0, 0, 0].rearrange("i j o n -> (i j o) n")
@@ -254,92 +269,72 @@ def tile_capsulelayer_kernel(tc, image, weight, bias, out):
         make_identity(nc, selector[:])
         make_identity(nc, identity[:])
         nc.vector.memset(eps[:], EPS)
-        warm = small.tile([P, 1], F32, bufs=1)
-        nc.scalar.activation(out=warm[:], in_=eps[:], func=ACT.Abs_reciprocal_sqrt)
+        first_root = small.tile([P, 1], F32)
+        nc.scalar.activation(out=first_root[:], in_=eps[:], func=ACT.Abs_reciprocal_sqrt)
         padded = arena.tile([P, PADDED_ROWS, SIDE, PACK], BF16, align_bytes=64, offset=AT_PADDED)
         nc.vector.memset(padded[:, 0, :, :], 0.0)
         nc.vector.memset(padded[:, PADDED_ROWS - 1, :, :], 0.0)
         nc.vector.memset(even_scales[:].rearrange("p k x -> p (k x)").bitcast(I32), 0)
 
-        def spread_bias(t, engine_copy):
-            product = banks.tile([P, CAPSULES, CHANNELS], F32, bufs=4, offset=4 * BANK)
-            nc.tensor.matmul(
-                out=product[:].rearrange("p c e -> p (c e)"),
-                lhsT=selector[:, t : t + 1].to_broadcast([P, P]),
-                rhs=bias_table[:],
-                start=True,
-                stop=True,
-            )
-            engine_copy(out=bias_tile[:, t, :, :], in_=product[:].rearrange("p c e -> p e c"))
-
-        spread_bias(POSITION_ORDER[0], nc.scalar.copy)
+        spread_bias(POSITION_ORDER[0])
         lay_out_image(nc, raw_image, padded, 0, TOP_ROWS)
-        quantise_image(nc, padded, even_codes, even_scales, 0, WHOLE_ROWS)
-        quantise_image(nc, padded, even_codes, even_scales, WHOLE_ROWS, TOP_ROWS)
-
-        def prepare(i):
-            if i < POSITIONS:
-                t = POSITION_ORDER[i]
-                ki, kj = divmod(t, KERNEL)
-                if ki == 0 and kj != 1:
-                    finish_shift(nc, kj, even_codes, even_scales, odd_scales)
-                quantise_weight(nc, arena, raw_weight_of[t], t, weight_codes, weight_scales)
-
+        quantise_image(nc, padded, codes, even_scales, 0, WHOLE_ROWS)
+        quantise_image(nc, padded, codes, even_scales, WHOLE_ROWS, TOP_ROWS)
         prepare(0)
         warm_up = banks.tile([P, BANK_SLOTS, P], F32, offset=0)
-        for i in range(WARM_UP_PRODUCTS):
-            nc.tensor.matmul(out=warm_up[:, 0, :], lhsT=identity[:], rhs=identity[:], start=True, stop=True)
-        spread_bias(POSITION_ORDER[1], nc.scalar.copy)
+        keep_busy(warm_up, WARM_UP_PRODUCTS)
+        spread_bias(POSITION_ORDER[1])
         for i, t in enumerate(POSITION_ORDER):
-            for lane in range(GROUP_TILES):
-                if lane == GROUP_TILES // 2:
+            for m in range(GROUP_TILES):
+                if m == GROUP_TILES // 2:
                     prepare(i + 1)
-                multiply(lane, t)
-                add_bias(lane, t)
+                multiply(m, t)
+                add_bias(m, t)
             if i == 0:
-                spread_bias(POSITION_ORDER[2], nc.scalar.copy)
-                spread_bias(POSITION_ORDER[3], nc.scalar.copy)
-            if i == 0:
+                spread_bias(POSITION_ORDER[2])
+                spread_bias(POSITION_ORDER[3])
                 lay_out_image(nc, raw_image, padded, TOP_ROWS, SIDE)
-                quantise_image(nc, padded, even_codes, even_scales, TOP_ROWS, PADDED_ROWS)
-                move_codes(nc, even_codes, even_scales, odd_scales)
-            if 0 < i and i + 3 < POSITIONS:
-                spread_bias(POSITION_ORDER[i + 3], nc.scalar.copy)
-            if i > 0:
+                quantise_image(nc, padded, codes, even_scales, TOP_ROWS, PADDED_ROWS)
+                move_codes(nc, codes, even_scales, odd_scales)
+            else:
+                if i + 3 < POSITIONS:
+                    spread_bias(POSITION_ORDER[i + 3])
                 add_to_sum(POSITION_ORDER[i - 1])
 
         items = [(s, g, k) for s in range(PHASES) for g in range(GROUPS) for k in range(CHUNKS)]
         count = len(items)
         first_weighed = GROUPS * CHUNKS
         weighed_of, total_of, centre_flipped_of, centre_of, difference_of = {}, {}, {}, {}, {}
-        mean_of, result_of = {}, {}
-        distance_banks, paired_of = {}, {}
+        mean_chunk_of, result_of, distance_banks, paired_of = {}, {}, {}, {}
         pull_flipped_of, root_of, pull_bank_of, pull_sbuf_of, pull_psum_of, late_pull_of = {}, {}, {}, {}, {}, {}
 
         def at(i):
             return items[i] if 0 <= i < count else (-1, -1, -1)
 
+        def channels_of(i):
+            s, g, k = items[i]
+            return slice(CHUNK * k, CHUNK * k + CHUNK)
+
         def chunk_priors(i):
             s, g, k = items[i]
-            return priors_of[g][:, :, CHUNK * k : CHUNK * k + CHUNK, :]
+            return priors_of[g][:, :, channels_of(i), :]
+
+        def with_products(i):
+            return i + 3 < POSITIONS
 
         def gpsimd_share(i):
             s, g, k = items[i]
-            if s < PHASES - 1:
-                return MIDDLE_SHARES[k % len(MIDDLE_SHARES)]
-            if g == 0 and k < STILL_SUBTRACTING:
-                return MIDDLE_SHARES[0]
-            return LAST_SHARE if g == 1 or k >= LATE_FROM else FIRST_IN_PSUM
+            if s == PHASES - 1:
+                return LAST_SHARE if g == 1 or k >= LATE_PULL_FROM else FIRST_IN_PSUM
+            return FIRST_IN_PSUM if k == 0 else IN_SBUF - (k + 1) % 2
 
         def gpsimd_subtracts(i):
-            if i + 3 < POSITIONS:
+            if with_products(i):
                 return EARLY_SUBTRACTS
             return LATE_SUBTRACTS if i < CHUNKS else 0
 
         def gpsimd_squares(i):
-            if i + 3 < POSITIONS:
-                return EARLY_SQUARES
-            return LATE_SQUARES if i + 3 < first_weighed else 0
+            return LATE_SQUARES if not with_products(i) and i + 3 < first_weighed else 0
 
         def gpsimd_pairs(i):
             return PAIRS if CHUNKS < i < first_weighed else 0
@@ -371,39 +366,18 @@ def tile_capsulelayer_kernel(tc, image, weight, bias, out):
         def weigh_vector(i):
             s, g, k = items[i]
             n = gpsimd_share(i)
-            f = FIRST_IN_PSUM
-            for first, last, base, pulls_in_psum in (
-                (n, f, n, late_pull_of),
-                (max(n, f), WEIGHED, f, pull_psum_of),
-            ):
-                if first < last:
-                    nc.vector.tensor_tensor(
-                        out=weighed_of[i][:, first:last, :, :],
-                        in0=chunk_priors(i)[:, first:last, :, :],
-                        in1=pulls_in_psum[(s, g)][:, first - base : last - base, :]
-                        .unsqueeze(2)
-                        .to_broadcast([P, last - first, CHUNK, LANES]),
-                        op=ALU.mult,
-                    )
-
-        def sum_positions(i):
-            s, g, k = items[i]
-            if s == 0:
-                weighted_sum = banks.tile([P, BANK_SLOTS, P], F32, tag="mean_sum", offset=5 * BANK)
-            elif s == PHASES - 1 and i % 2 == 1:
-                weighted_sum = banks.tile([P, BANK_SLOTS, P], F32, tag="centre", bufs=2, offset=6 * BANK)
-            else:
-                weighted_sum = banks.tile([P, BANK_SLOTS, P], F32, offset=3 * BANK)
-            total_of[i] = weighted_sum
-            for c in range(CHUNK):
-                if s == 0:
-                    n = gpsimd_pairs(i)
-                    singles = [t for t in range(POSITIONS) if t % PAIR_STEP >= n or t >= 2 * PAIR_STEP]
-                    blocks = [chunk_priors(i)[:, t, c, :] for t in singles]
-                    blocks = [paired_of[i][:, j, c, :] for j in range(n)] + blocks
-                else:
-                    blocks = [weighed_of[i][:, t, c, :] for t in range(WEIGHED)]
-                add_flipped(weighted_sum[:, c, :], blocks)
+            shares = [(max(n, FIRST_IN_PSUM), WEIGHED, FIRST_IN_PSUM, pull_psum_of)]
+            if n < FIRST_IN_PSUM:
+                shares = [(n, FIRST_IN_PSUM, n, late_pull_of)] + shares
+            for first, last, base, pulls_in_psum in shares:
+                nc.vector.tensor_tensor(
+                    out=weighed_of[i][:, first:last, :, :],
+                    in0=chunk_priors(i)[:, first:last, :, :],
+                    in1=pulls_in_psum[(s, g)][:, first - base : last - base, :]
+                    .unsqueeze(2)
+                    .to_broadcast([P, last - first, CHUNK, LANES]),
+                    op=ALU.mult,
+                )
 
         def add_flipped(out_block, blocks):
             for j, block in enumerate(blocks):
@@ -416,11 +390,29 @@ def tile_capsulelayer_kernel(tc, image, weight, bias, out):
                     stop=(j == len(blocks) - 1),
                 )
 
-        def empty_sum(i):
+        def sum_positions(i):
             s, g, k = items[i]
             if s == 0:
+                total = banks.tile([P, BANK_SLOTS, P], F32, tag="mean_sum", offset=5 * BANK)
+            elif s == PHASES - 1 and i % 2 == 1:
+                total = banks.tile([P, BANK_SLOTS, P], F32, tag="centre", bufs=2, offset=6 * BANK)
+            else:
+                total = banks.tile([P, BANK_SLOTS, P], F32, tag="weighted_sum", offset=3 * BANK)
+            total_of[i] = total
+            for c in range(CHUNK):
+                if s == 0:
+                    n = gpsimd_pairs(i)
+                    paired = [j for j in range(n)] + [j + PAIR_STEP for j in range(n)]
+                    blocks = [paired_of[i][:, j, c, :] for j in range(n)]
+                    blocks += [chunk_priors(i)[:, t, c, :] for t in range(POSITIONS) if t not in paired]
+                else:
+                    blocks = [weighed_of[i][:, t, c, :] for t in range(WEIGHED)]
+                add_flipped(total[:, c, :], blocks)
+
+        def empty_sum(i):
+            if items[i][0] == 0:
                 nc.scalar.activation(
-                    out=mean_flipped_of[g][:, CHUNK * k : CHUNK * k + CHUNK, :],
+                    out=mean_flipped_1[:, channels_of(i), :],
                     in_=total_of[i][:, 0:CHUNK, :],
                     func=ACT.Copy,
                     scale=1.0 / POSITIONS,
@@ -437,17 +429,17 @@ def tile_capsulelayer_kernel(tc, image, weight, bias, out):
             nc.vector.tensor_tensor(
                 out=result[:],
                 in0=total_of[i][:, 0:CHUNK, :],
-                in1=mean_flipped_of[g][:, CHUNK * k : CHUNK * k + CHUNK, :],
+                in1=mean_flipped_of[g][:, channels_of(i), :],
                 op=ALU.add,
             )
 
         def store(i):
             s, g, k = items[i]
-            for lane in range(GROUP_TILES):
-                m = GROUP_TILES * g + lane
+            for tile in range(GROUP_TILES):
+                m = GROUP_TILES * g + tile
                 nc.sync.dma_start(
-                    out=out_view[:, CHUNK * k : CHUNK * k + CHUNK, P * m : P * m + P],
-                    in_=result_of[i][CAPSULES * lane : CAPSULES * lane + CAPSULES, :, :],
+                    out=out_view[:, channels_of(i), P * m : P * m + P],
+                    in_=result_of[i][CAPSULES * tile : CAPSULES * tile + CAPSULES, :, :],
                 )
 
         def flip_centre(i):
@@ -465,15 +457,14 @@ def tile_capsulelayer_kernel(tc, image, weight, bias, out):
                 nc.tensor.transpose(out=centre[:, c, :], in_=flipped, identity=identity[:])
 
         def keep_mean(i):
-            mean = arena.tile([P, CHUNK, LANES], F32, bufs=3, offset=AT_MEAN)
-            mean_of[i] = mean
-            nc.scalar.copy(out=mean[:], in_=centre_of[i][:, 0:CHUNK, :])
+            mean_chunk = arena.tile([P, CHUNK, LANES], F32, bufs=3, offset=AT_MEAN_CHUNK)
+            mean_chunk_of[i] = mean_chunk
+            nc.scalar.copy(out=mean_chunk[:], in_=centre_of[i][:, 0:CHUNK, :])
 
         def subtract(i):
-            s, g, k = items[i]
             difference = arena.tile([P, POSITIONS, CHUNK, LANES], F32, bufs=3, offset=AT_DIFFERENCE)
             difference_of[i] = difference
-            target = chunk_priors(i) if s == 0 else difference
+            target = chunk_priors(i) if items[i][0] == 0 else difference
             n = POSITIONS - gpsimd_subtracts(i)
             nc.vector.tensor_tensor(
                 out=target[:, 0:n, :, :],
@@ -485,15 +476,12 @@ def tile_capsulelayer_kernel(tc, image, weight, bias, out):
                 nc.gpsimd.tensor_tensor(
                     out=target[:, n:POSITIONS, :, :],
                     in0=chunk_priors(i)[:, n:POSITIONS, :, :],
-                    in1=mean_of[i][:]
-                    .unsqueeze(1)
-                    .to_broadcast([P, POSITIONS - n, CHUNK, LANES]),
+                    in1=mean_chunk_of[i][:].unsqueeze(1).to_broadcast([P, POSITIONS - n, CHUNK, LANES]),
                     op=ALU.subtract,
                 )
 
         def square(i, first, last):
-            s, g, k = items[i]
-            source = chunk_priors(i) if s == 0 else difference_of[i]
+            source = chunk_priors(i) if items[i][0] == 0 else difference_of[i]
             n = min(last, POSITIONS - gpsimd_squares(i))
             nc.scalar.activation(
                 out=difference_of[i][:, first:n, :, :], in_=source[:, first:n, :, :], func=ACT.Square
@@ -534,20 +522,21 @@ def tile_capsulelayer_kernel(tc, image, weight, bias, out):
         def pulls(s, g):
             pull_flipped = arena.tile([P, POSITIONS, P], F32, bufs=2, offset=AT_PULL_FLIPPED)
             pull_flipped_of[(s, g)] = pull_flipped
-            for b in range(3):
+            for b, distance in enumerate(distance_banks[(s - 1, g)]):
                 n = min(BANK_SLOTS, POSITIONS - BANK_SLOTS * b)
                 nc.scalar.activation(
                     out=pull_flipped[:, BANK_SLOTS * b : BANK_SLOTS * b + n, :],
-                    in_=distance_banks[(s - 1, g)][b][:, 0:n, :],
+                    in_=distance[:, 0:n, :],
                     func=ACT.Abs_reciprocal_sqrt,
                     bias=eps[:, 0:1],
                 )
 
         def sum_pulls(s, g):
-            add_flipped(take_pull_bank(s, g)[:, 0, :], [pull_flipped_of[(s, g)][:, t, :] for t in range(POSITIONS)])
+            pull_flipped = pull_flipped_of[(s, g)]
+            add_flipped(take_pull_bank(s, g)[:, 0, :], [pull_flipped[:, t, :] for t in range(POSITIONS)])
 
         def invert_sum(s, g):
-            root = arena.tile([P, LANES], F32, bufs=2, offset=AT_PULL_SUM)
+            root = arena.tile([P, LANES], F32, bufs=2, offset=AT_ROOT)
             root_of[(s, g)] = root
             nc.scalar.activation(out=root[:], in_=pull_bank_of[(s, g)][:, 0, :], func=ACT.Abs_reciprocal_sqrt)
             nc.scalar.activation(out=root[:], in_=root[:], func=ACT.Square)
@@ -578,102 +567,96 @@ def tile_capsulelayer_kernel(tc, image, weight, bias, out):
             for t in range(first, last):
                 add_flipped(psum_tile[:, t - first, :], [pull_flipped[:, t, :], pull_flipped[:, WEIGHED, :]])
 
-        def flip_first_pulls(s, g):
+        def first_pulls(s, g):
             flip_pulls(s, g, 0, FIRST_IN_PSUM, take_pull_bank(s, g))
-
-        def copy_first_pulls(s, g):
             pull_sbuf = arena.tile([P, IN_SBUF, LANES], F32, bufs=2, offset=AT_PULL)
             pull_sbuf_of[(s, g)] = pull_sbuf
             nc.scalar.copy(out=pull_sbuf[:, 0:FIRST_IN_PSUM, :], in_=pull_bank_of[(s, g)][:])
 
-        def flip_second_pulls(s, g):
+        def second_pulls(s, g):
             pull_psum = take_pull_bank(s, g)
             pull_psum_of[(s, g)] = pull_psum
             flip_pulls(s, g, FIRST_IN_PSUM, WEIGHED, pull_psum)
-
-        def copy_second_pulls(s, g):
             nc.scalar.copy(
                 out=pull_sbuf_of[(s, g)][:, FIRST_IN_PSUM:IN_SBUF, :],
-                in_=pull_psum_of[(s, g)][:, 0 : IN_SBUF - FIRST_IN_PSUM, :],
+                in_=pull_psum[:, 0 : IN_SBUF - FIRST_IN_PSUM, :],
             )
 
-        def flip_late_pull(s, g):
+        def flip_late_pull(g):
             late_pull = banks.tile([P, BANK_SLOTS, LANES], F32, tag="late_pull%d" % g, offset=g * BANK)
-            late_pull_of[(s, g)] = late_pull
-            flip_pulls(s, g, LAST_SHARE, FIRST_IN_PSUM, late_pull)
+            late_pull_of[(PHASES - 1, g)] = late_pull
+            flip_pulls(PHASES - 1, g, LAST_SHARE, FIRST_IN_PSUM, late_pull)
 
-        def keep_busy(bank, n):
-            for i in range(n):
-                nc.tensor.matmul(out=bank[:, 0, :], lhsT=identity[:], rhs=identity[:], start=True, stop=True)
-
-        def phase_end(turn, lag):
+        def closing(turn, lag):
             s, g, k = at(turn - lag)
             if 0 <= s < PHASES - 1 and k == CHUNKS - 1:
                 return (s + 1, g)
             return None
 
+        last_closing = (PHASES - 1, GROUPS - 1)
         for turn in range(count + 9):
+            squared, subtracted, flipped, summed = turn - 4, turn - 3, turn - 2, turn - 1
             late = POSITION_ORDER[turn] if turn < POSITIONS else None
             if at(turn)[0:2] == (0, 1):
                 add_pairs(turn)
             if at(turn)[0] >= 1:
                 weigh_gpsimd(turn)
-            if 0 <= at(turn - 2)[0] < PHASES - 1:
-                flip_centre(turn - 2)
-                if at(turn - 2)[0] == 0 and gpsimd_subtracts(turn - 2) > 0:
-                    keep_mean(turn - 2)
+            if 0 <= at(flipped)[0] < PHASES - 1:
+                flip_centre(flipped)
+                if at(flipped)[0] == 0 and gpsimd_subtracts(flipped) > 0:
+                    keep_mean(flipped)
             if late is not None:
-                for lane in range(GROUP_TILES):
-                    multiply(GROUP_TILES + lane, late)
-                    if lane < GROUP_TILES // 2:
-                        add_bias(GROUP_TILES + lane, late)
+                for tile in range(GROUP_TILES):
+                    multiply(GROUP_TILES + tile, late)
+                    if tile < GROUP_TILES // 2:
+                        add_bias(GROUP_TILES + tile, late)
             if turn == 0:
                 add_to_sum(POSITION_ORDER[-1])
                 mean_prior()
-            if at(turn - 1)[0:2] == (0, 1) or at(turn - 1)[0] >= 1:
-                sum_positions(turn - 1)
-            if phase_end(turn, 6):
-                invert_sum(*phase_end(turn, 6))
-                if at(turn - 4)[0] == PHASES - 1:
-                    flip_scale(*phase_end(turn, 6))
-            if turn > count - GROUPS * CHUNKS + 4 and at(turn - 1)[0] >= 0:
+            if at(summed)[0:2] == (0, 1) or at(summed)[0] >= 1:
+                sum_positions(summed)
+            if closing(turn, 6):
+                invert_sum(*closing(turn, 6))
+                if closing(turn, 6) == last_closing:
+                    flip_scale(*last_closing)
+            if first_weighed * (PHASES - 1) + 4 < turn <= count:
                 idle_bank = banks.tile([P, BANK_SLOTS, P], F32, offset=2 * BANK)
                 keep_busy(idle_bank, 1)
-            if phase_end(turn, 6) == (PHASES - 1, 1):
-                flip_late_pull(PHASES - 1, 0)
-            if phase_end(turn, 8) == (PHASES - 1, 1):
-                flip_late_pull(PHASES - 1, 1)
-            if phase_end(turn, 8):
-                flip_second_pulls(*phase_end(turn, 8))
-                copy_second_pulls(*phase_end(turn, 8))
-            if at(turn - 1)[0:2] == (0, 1) or 1 <= at(turn - 1)[0] < PHASES - 1:
-                empty_sum(turn - 1)
-            if 0 <= at(turn - 3)[0] < PHASES - 1:
-                subtract(turn - 3)
-                square(turn - 3, 0, 5)
-            if phase_end(turn, 7):
-                normalise_pulls(*phase_end(turn, 7))
-            if phase_end(turn, 7):
-                flip_first_pulls(*phase_end(turn, 7))
-                copy_first_pulls(*phase_end(turn, 7))
+            if closing(turn, 6) == last_closing:
+                flip_late_pull(0)
+            if closing(turn, 8) == last_closing:
+                flip_late_pull(1)
+            if closing(turn, 8):
+                second_pulls(*closing(turn, 8))
+            if at(summed)[0:2] == (0, 1) or 1 <= at(summed)[0] < PHASES - 1:
+                empty_sum(summed)
+            if 0 <= at(subtracted)[0] < PHASES - 1:
+                subtract(subtracted)
+                square(subtracted, 0, SPLIT)
+            if closing(turn, 7):
+                normalise_pulls(*closing(turn, 7))
             if late is not None:
-                for lane in range(GROUP_TILES // 2, GROUP_TILES):
-                    add_bias(GROUP_TILES + lane, late)
-            if 0 <= at(turn - 4)[0] < PHASES - 1:
-                sum_channels(turn - 4, 0, 5)
-                if phase_end(turn, 5):
-                    keep_busy(take_pull_bank(*phase_end(turn, 5)), CLOSING_PRODUCTS)
-                if phase_end(turn, 6):
-                    flip_scale(*phase_end(turn, 6))
-                sum_channels(turn - 4, 5, POSITIONS)
-            if phase_end(turn, 4):
-                pulls(*phase_end(turn, 4))
-            if 0 <= at(turn - 3)[0] < PHASES - 1:
-                square(turn - 3, 5, POSITIONS)
-            if phase_end(turn, 5):
-                sum_pulls(*phase_end(turn, 5))
+                for tile in range(GROUP_TILES // 2, GROUP_TILES):
+                    add_bias(GROUP_TILES + tile, late)
+            with_distances = 0 <= at(squared)[0] < PHASES - 1
+            if with_distances:
+                sum_channels(squared, 0, SPLIT)
+            if with_distances and closing(turn, 5):
+                keep_busy(take_pull_bank(*closing(turn, 5)), CLOSING_PRODUCTS)
+            if closing(turn, 6) and closing(turn, 6) != last_closing:
+                flip_scale(*closing(turn, 6))
+            if closing(turn, 7):
+                first_pulls(*closing(turn, 7))
+            if with_distances:
+                sum_channels(squared, SPLIT, POSITIONS)
+            if closing(turn, 4):
+                pulls(*closing(turn, 4))
+            if 0 <= at(subtracted)[0] < PHASES - 1:
+                square(subtracted, SPLIT, POSITIONS)
+            if closing(turn, 5):
+                sum_pulls(*closing(turn, 5))
             if at(turn)[0] >= 1:
                 weigh_vector(turn)
-            if at(turn - 1)[0] == PHASES - 1:
-                finish(turn - 1)
-                store(turn - 1)
+            if at(summed)[0] == PHASES - 1:
+                finish(summed)
+                store(summed)

from contextlib import ExitStack

import concourse.mybir as mybir
from concourse.masks import make_identity

F32 = mybir.dt.float32
BF16 = mybir.dt.bfloat16
U32 = mybir.dt.uint32
U8 = mybir.dt.uint8
I32 = mybir.dt.int32
FP8X4 = mybir.dt.float8_e4m3fn_x4
ALU = mybir.AluOpType
ACT = mybir.ActivationFunctionType

P = 128
PACK = 4
SIDE = 32
PADDED_ROWS = SIDE + 2
KERNEL = 3
POSITIONS = KERNEL * KERNEL
FEATURES = 512
CHANNELS = 16
CAPSULES = FEATURES // CHANNELS
EPS = 1e-4

GROUPS = 2
GROUP_TILES = 4
LANES = GROUP_TILES * CAPSULES
CHUNK = 2
CHUNKS = CHANNELS // CHUNK
PHASES = 4
BANK_SLOTS = 4
BANK = 2048

POSITION_ORDER = (1, 7, 4, 0, 6, 3, 2, 8, 5)
TOP_ROWS = 18
WHOLE_ROWS = 16

WEIGHED = POSITIONS - 1
FIRST_IN_PSUM = 4
IN_SBUF = 6
LAST_SHARE = 3
LATE_PULL_FROM = 6
EARLY_SUBTRACTS = 6
LATE_SUBTRACTS = 1
LATE_SQUARES = 1
PAIRS = 3
PAIR_STEP = 4
SPLIT = 5
WARM_UP_PRODUCTS = 5
CLOSING_PRODUCTS = 3

FLOPS = 2 * POSITIONS * SIDE * SIDE * (P * PACK) * FEATURES

PRIOR_BYTES = POSITIONS * CHANNELS * LANES * 4
WORK_BYTES = POSITIONS * CHUNK * LANES * 4
AT_PRIORS = 0
AT_RAW_IMAGE = PRIOR_BYTES
AT_PADDED = AT_RAW_IMAGE + PACK * SIDE * SIDE * 2
AT_RAW_WEIGHT = AT_PADDED + PADDED_ROWS * SIDE * PACK * 2
AT_GROUPED = AT_RAW_WEIGHT + POSITIONS * PACK * FEATURES * 2
AT_BIAS_TABLE = AT_GROUPED + 2 * PACK * FEATURES * 2
AT_SELECTOR = AT_BIAS_TABLE + (FEATURES + P) * 2
AT_REST = 2 * PRIOR_BYTES
AT_WEIGHT_CODES = AT_REST
AT_WEIGHT_SCALES = AT_WEIGHT_CODES + POSITIONS * FEATURES * 4
AT_CODES = AT_WEIGHT_SCALES + POSITIONS * FEATURES
AT_EVEN_SCALES = AT_CODES + KERNEL * PADDED_ROWS * SIDE * 4
AT_ODD_SCALES = AT_EVEN_SCALES + KERNEL * PADDED_ROWS * SIDE
AT_BIAS = AT_ODD_SCALES + KERNEL * SIDE * SIDE
AT_WEIGHED = AT_REST
AT_PAIRED = AT_WEIGHED + WORK_BYTES
AT_PULL_FLIPPED = AT_WEIGHED + 3 * WORK_BYTES
AT_PULL = AT_PULL_FLIPPED + 2 * POSITIONS * P * 4
AT_ROOT = AT_PULL + 2 * IN_SBUF * LANES * 4
AT_CENTRE_FLIPPED = AT_ROOT + 2 * LANES * 4
AT_MEAN_1 = AT_CENTRE_FLIPPED + 3 * CHUNK * P * 4
AT_DIFFERENCE = AT_MEAN_1 + CHANNELS * P * 4
AT_MEAN_0 = AT_DIFFERENCE + 3 * WORK_BYTES
AT_MEAN_CHUNK = AT_MEAN_0 + CHANNELS * P * 4
AT_RESULT = AT_MEAN_CHUNK


def lay_out_image(nc, raw_image, padded, first, last):
    nc.vector.tensor_copy(
        out=padded[:, first + 1 : last + 1, :, :],
        in_=raw_image[:, :, first:last, :].rearrange("p j h w -> p h w j"),
    )


def quantise_image(nc, padded, codes, even_scales, first, last):
    nc.vector.quantize_mx(
        out=codes[:, 1, first * SIDE : last * SIDE].bitcast(FP8X4),
        scales=even_scales[:, 1, first * SIDE : last * SIDE],
        in_=padded[:, first:last, :, :].rearrange("p r w j -> p (r w j)"),
    )


def move_codes(nc, codes, even_scales, odd_scales):
    pixels = PADDED_ROWS * SIDE
    whole = SIDE * SIDE
    middle = codes[:, 1, :].bitcast(I32)
    nc.sync.dma_start(
        out=odd_scales[:, 1, :].bitcast(I32), in_=even_scales[:, 1, SIDE : SIDE + whole].bitcast(I32)
    )
    nc.sync.dma_start(out=codes[:, 0, 1:pixels].bitcast(I32), in_=middle[:, 0 : pixels - 1])
    nc.sync.dma_start(out=codes[:, 2, 0 : pixels - 1].bitcast(I32), in_=middle[:, 1:pixels])


def finish_shift(nc, kj, codes, even_scales, odd_scales):
    pixels = PADDED_ROWS * SIDE
    if kj == 0:
        to, source, empty = slice(1, pixels), slice(0, pixels - 1), 0
    else:
        to, source, empty = slice(0, pixels - 1), slice(1, pixels), SIDE - 1
    nc.gpsimd.memset(
        codes[:, kj, :].bitcast(I32).rearrange("p (r w) -> p r w", w=SIDE)[:, :, empty : empty + 1], 0
    )
    nc.vector.tensor_copy(out=even_scales[:, kj, to], in_=even_scales[:, 1, source])
    nc.sync.dma_start(
        out=odd_scales[:, kj, :].bitcast(I32),
        in_=even_scales[:, kj, SIDE : SIDE + SIDE * SIDE].bitcast(I32),
    )


def load_weight(nc, arena, weight, t):
    raw_weight = arena.tile([P, PACK, FEATURES], BF16, bufs=POSITIONS, offset=AT_RAW_WEIGHT)
    nc.sync.dma_start(
        out=raw_weight[:],
        in_=weight[0, 0, 0, t // KERNEL, t % KERNEL].rearrange("(p j) n -> p j n", j=PACK),
    )
    return raw_weight


def quantise_weight(nc, arena, raw_weight, t, weight_codes, weight_scales):
    grouped = arena.tile([P, FEATURES, PACK], BF16, align_bytes=64, bufs=2, offset=AT_GROUPED)
    nc.scalar.copy(
        out=grouped[:].rearrange("p (c i) j -> p c j i", i=4),
        in_=raw_weight[:].rearrange("p j (c i) -> p c j i", i=4),
    )
    nc.vector.quantize_mx(
        out=weight_codes[:, t, :].bitcast(FP8X4),
        scales=weight_scales[:, t, :],
        in_=grouped[:].rearrange("p n j -> p (n j)"),
    )


def tile_capsulelayer_kernel(tc, image, weight, bias, out):
    nc = tc.nc
    out_view = out[0].rearrange("(c e) h w -> c e (h w)", e=CHANNELS)

    with ExitStack() as stack:
        stack.enter_context(tc.manual_schedule())
        arena = stack.enter_context(tc.tile_pool(name="arena", bufs=1))
        small = stack.enter_context(tc.tile_pool(name="small", bufs=1))
        banks = stack.enter_context(tc.psum_pool(name="banks", bufs=1))

        priors_0 = arena.tile([P, POSITIONS, CHANNELS, LANES], F32, offset=AT_PRIORS)
        priors_1 = arena.tile([P, POSITIONS, CHANNELS, LANES], F32, offset=AT_PRIORS + PRIOR_BYTES)
        priors_of = (priors_0, priors_1)
        mean_flipped_0 = arena.tile([P, CHANNELS, P], F32, offset=AT_MEAN_0)
        mean_flipped_1 = arena.tile([P, CHANNELS, P], F32, offset=AT_MEAN_1)
        mean_flipped_of = (mean_flipped_0, mean_flipped_1)
        weight_codes = arena.tile([P, POSITIONS, FEATURES], U32, align_bytes=64, offset=AT_WEIGHT_CODES)
        weight_scales = arena.tile([P, POSITIONS, FEATURES], U8, align_bytes=64, offset=AT_WEIGHT_SCALES)
        codes = arena.tile([P, KERNEL, PADDED_ROWS * SIDE], U32, align_bytes=64, offset=AT_CODES)
        even_scales = arena.tile([P, KERNEL, PADDED_ROWS * SIDE], U8, align_bytes=64, offset=AT_EVEN_SCALES)
        odd_scales = arena.tile([P, KERNEL, SIDE * SIDE], U8, align_bytes=64, offset=AT_ODD_SCALES)
        bias_tile = arena.tile([P, POSITIONS, CHANNELS, CAPSULES], BF16, offset=AT_BIAS)
        selector = arena.tile([P, P], BF16, offset=AT_SELECTOR)
        bias_table = arena.tile([P, FEATURES], BF16, offset=AT_BIAS_TABLE)
        identity = small.tile([P, P], F32)
        eps = small.tile([P, 1], F32)

        products, prior_sums = {}, []

        def multiply(m, t):
            ki, kj = divmod(t, KERNEL)
            window = slice(P * m + SIDE * ki, P * m + SIDE * ki + P)
            if ki == 1:
                scales = odd_scales[:, kj, P * m : P * m + P]
            else:
                scales = even_scales[:, kj, window]
            if m < GROUP_TILES:
                product = banks.tile([P, CAPSULES, CHANNELS], F32, tag="product", bufs=4, offset=4 * BANK)
            else:
                product = banks.tile([P, CAPSULES, CHANNELS], F32, tag="late_product", bufs=3, offset=5 * BANK)
            products[(m, t)] = product
            nc.tensor.matmul_mx(
                out=product[:].rearrange("p c e -> p (c e)"),
                lhsT=codes[:, kj, window].bitcast(FP8X4),
                lhsT_scale=scales,
                rhs=weight_codes[:, t, :].bitcast(FP8X4),
                rhs_scale=weight_scales[:, t, :],
                start=True,
                stop=True,
            )

        def add_bias(m, t):
            g, tile = divmod(m, GROUP_TILES)
            lanes = slice(CAPSULES * tile, CAPSULES * tile + CAPSULES)
            nc.vector.tensor_tensor(
                out=priors_of[g][:, t, :, lanes],
                in0=products[(m, t)][:].rearrange("p c e -> p e c"),
                in1=bias_tile[:, t, :, :],
                op=ALU.add,
            )

        def add_to_sum(t):
            if t == POSITION_ORDER[0]:
                for q in range(CHANNELS // BANK_SLOTS):
                    prior_sum = banks.tile([P, BANK_SLOTS, P], F32, tag="prior_sum%d" % q, offset=q * BANK)
                    prior_sums.append(prior_sum)
            for e in range(CHANNELS):
                q, slot = divmod(e, BANK_SLOTS)
                nc.tensor.matmul(
                    out=prior_sums[q][:, slot, :],
                    lhsT=priors_of[0][:, t, e, :],
                    rhs=identity[:],
                    is_transpose=True,
                    start=(t == POSITION_ORDER[0] and slot == 0),
                    stop=(t == POSITION_ORDER[-1] and slot == BANK_SLOTS - 1),
                )

        def mean_prior():
            for q in range(CHANNELS // BANK_SLOTS):
                nc.scalar.activation(
                    out=mean_flipped_0[:, BANK_SLOTS * q : BANK_SLOTS * q + BANK_SLOTS, :],
                    in_=prior_sums[q][:],
                    func=ACT.Copy,
                    scale=1.0 / POSITIONS,
                )

        def keep_busy(bank, n):
            for j in range(n):
                nc.tensor.matmul(out=bank[:, 0, :], lhsT=identity[:], rhs=identity[:], start=True, stop=True)

        def spread_bias(t):
            product = banks.tile([P, CAPSULES, CHANNELS], F32, tag="product", bufs=4, offset=4 * BANK)
            nc.tensor.matmul(
                out=product[:].rearrange("p c e -> p (c e)"),
                lhsT=selector[:, t : t + 1].to_broadcast([P, P]),
                rhs=bias_table[:],
                start=True,
                stop=True,
            )
            nc.scalar.copy(out=bias_tile[:, t, :, :], in_=product[:].rearrange("p c e -> p e c"))

        def prepare(i):
            if i < POSITIONS:
                t = POSITION_ORDER[i]
                ki, kj = divmod(t, KERNEL)
                if ki == 0 and kj != 1:
                    finish_shift(nc, kj, codes, even_scales, odd_scales)
                quantise_weight(nc, arena, raw_weight_of[t], t, weight_codes, weight_scales)

        nc.vector.memset(bias_table[:], 0.0)
        nc.sync.dma_start(
            out=bias_table[0:POSITIONS, :], in_=bias[0, 0, 0].rearrange("i j o n -> (i j o) n")
        )
        raw_image = arena.tile([P, PACK, SIDE, SIDE], BF16, offset=AT_RAW_IMAGE)
        image_view = image[0].rearrange("(p j) h w -> p j h w", j=PACK)
        nc.sync.dma_start(out=raw_image[:, :, 0:TOP_ROWS, :], in_=image_view[:, :, 0:TOP_ROWS, :])
        raw_weight_of = {}
        raw_weight_of[POSITION_ORDER[0]] = load_weight(nc, arena, weight, POSITION_ORDER[0])
        nc.sync.dma_start(out=raw_image[:, :, TOP_ROWS:SIDE, :], in_=image_view[:, :, TOP_ROWS:SIDE, :])
        for t in POSITION_ORDER[1:]:
            raw_weight_of[t] = load_weight(nc, arena, weight, t)
        make_identity(nc, selector[:])
        make_identity(nc, identity[:])
        nc.vector.memset(eps[:], EPS)
        first_root = small.tile([P, 1], F32)
        nc.scalar.activation(out=first_root[:], in_=eps[:], func=ACT.Abs_reciprocal_sqrt)
        padded = arena.tile([P, PADDED_ROWS, SIDE, PACK], BF16, align_bytes=64, offset=AT_PADDED)
        nc.vector.memset(padded[:, 0, :, :], 0.0)
        nc.vector.memset(padded[:, PADDED_ROWS - 1, :, :], 0.0)
        nc.vector.memset(even_scales[:].rearrange("p k x -> p (k x)").bitcast(I32), 0)

        spread_bias(POSITION_ORDER[0])
        lay_out_image(nc, raw_image, padded, 0, TOP_ROWS)
        quantise_image(nc, padded, codes, even_scales, 0, WHOLE_ROWS)
        quantise_image(nc, padded, codes, even_scales, WHOLE_ROWS, TOP_ROWS)
        prepare(0)
        warm_up = banks.tile([P, BANK_SLOTS, P], F32, offset=0)
        keep_busy(warm_up, WARM_UP_PRODUCTS)
        spread_bias(POSITION_ORDER[1])
        for i, t in enumerate(POSITION_ORDER):
            for m in range(GROUP_TILES):
                if m == GROUP_TILES // 2:
                    prepare(i + 1)
                multiply(m, t)
                add_bias(m, t)
            if i == 0:
                spread_bias(POSITION_ORDER[2])
                spread_bias(POSITION_ORDER[3])
                lay_out_image(nc, raw_image, padded, TOP_ROWS, SIDE)
                quantise_image(nc, padded, codes, even_scales, TOP_ROWS, PADDED_ROWS)
                move_codes(nc, codes, even_scales, odd_scales)
            else:
                if i + 3 < POSITIONS:
                    spread_bias(POSITION_ORDER[i + 3])
                add_to_sum(POSITION_ORDER[i - 1])

        items = [(s, g, k) for s in range(PHASES) for g in range(GROUPS) for k in range(CHUNKS)]
        count = len(items)
        first_weighed = GROUPS * CHUNKS
        weighed_of, total_of, centre_flipped_of, centre_of, difference_of = {}, {}, {}, {}, {}
        mean_chunk_of, result_of, distance_banks, paired_of = {}, {}, {}, {}
        pull_flipped_of, root_of, pull_bank_of, pull_sbuf_of, pull_psum_of, late_pull_of = {}, {}, {}, {}, {}, {}

        def at(i):
            return items[i] if 0 <= i < count else (-1, -1, -1)

        def channels_of(i):
            s, g, k = items[i]
            return slice(CHUNK * k, CHUNK * k + CHUNK)

        def chunk_priors(i):
            s, g, k = items[i]
            return priors_of[g][:, :, channels_of(i), :]

        def with_products(i):
            return i + 3 < POSITIONS

        def gpsimd_share(i):
            s, g, k = items[i]
            if s == PHASES - 1:
                return LAST_SHARE if g == 1 or k >= LATE_PULL_FROM else FIRST_IN_PSUM
            return FIRST_IN_PSUM if k == 0 else IN_SBUF - (k + 1) % 2

        def gpsimd_subtracts(i):
            if with_products(i):
                return EARLY_SUBTRACTS
            return LATE_SUBTRACTS if i < CHUNKS else 0

        def gpsimd_squares(i):
            return LATE_SQUARES if not with_products(i) and i + 3 < first_weighed else 0

        def gpsimd_pairs(i):
            return PAIRS if CHUNKS < i < first_weighed else 0

        def add_pairs(i):
            n = gpsimd_pairs(i)
            if n > 0:
                paired = arena.tile([P, PAIRS, CHUNK, LANES], F32, bufs=2, offset=AT_PAIRED)
                paired_of[i] = paired
                nc.gpsimd.tensor_tensor(
                    out=paired[:],
                    in0=chunk_priors(i)[:, 0:n, :, :],
                    in1=chunk_priors(i)[:, PAIR_STEP : PAIR_STEP + n, :, :],
                    op=ALU.add,
                )

        def weigh_gpsimd(i):
            s, g, k = items[i]
            n = gpsimd_share(i)
            weighed = arena.tile([P, WEIGHED, CHUNK, LANES], F32, bufs=3, offset=AT_WEIGHED)
            weighed_of[i] = weighed
            nc.gpsimd.tensor_tensor(
                out=weighed[:, 0:n, :, :],
                in0=chunk_priors(i)[:, 0:n, :, :],
                in1=pull_sbuf_of[(s, g)][:, 0:n, :].unsqueeze(2).to_broadcast([P, n, CHUNK, LANES]),
                op=ALU.mult,
            )

        def weigh_vector(i):
            s, g, k = items[i]
            n = gpsimd_share(i)
            shares = [(max(n, FIRST_IN_PSUM), WEIGHED, FIRST_IN_PSUM, pull_psum_of)]
            if n < FIRST_IN_PSUM:
                shares = [(n, FIRST_IN_PSUM, n, late_pull_of)] + shares
            for first, last, base, pulls_in_psum in shares:
                nc.vector.tensor_tensor(
                    out=weighed_of[i][:, first:last, :, :],
                    in0=chunk_priors(i)[:, first:last, :, :],
                    in1=pulls_in_psum[(s, g)][:, first - base : last - base, :]
                    .unsqueeze(2)
                    .to_broadcast([P, last - first, CHUNK, LANES]),
                    op=ALU.mult,
                )

        def add_flipped(out_block, blocks):
            for j, block in enumerate(blocks):
                nc.tensor.matmul(
                    out=out_block,
                    lhsT=block,
                    rhs=identity[:],
                    is_transpose=True,
                    start=(j == 0),
                    stop=(j == len(blocks) - 1),
                )

        def sum_positions(i):
            s, g, k = items[i]
            if s == 0:
                total = banks.tile([P, BANK_SLOTS, P], F32, tag="mean_sum", offset=5 * BANK)
            elif s == PHASES - 1 and i % 2 == 1:
                total = banks.tile([P, BANK_SLOTS, P], F32, tag="centre", bufs=2, offset=6 * BANK)
            else:
                total = banks.tile([P, BANK_SLOTS, P], F32, tag="weighted_sum", offset=3 * BANK)
            total_of[i] = total
            for c in range(CHUNK):
                if s == 0:
                    n = gpsimd_pairs(i)
                    paired = [j for j in range(n)] + [j + PAIR_STEP for j in range(n)]
                    blocks = [paired_of[i][:, j, c, :] for j in range(n)]
                    blocks += [chunk_priors(i)[:, t, c, :] for t in range(POSITIONS) if t not in paired]
                else:
                    blocks = [weighed_of[i][:, t, c, :] for t in range(WEIGHED)]
                add_flipped(total[:, c, :], blocks)

        def empty_sum(i):
            if items[i][0] == 0:
                nc.scalar.activation(
                    out=mean_flipped_1[:, channels_of(i), :],
                    in_=total_of[i][:, 0:CHUNK, :],
                    func=ACT.Copy,
                    scale=1.0 / POSITIONS,
                )
            else:
                centre_flipped = arena.tile([P, CHUNK, P], F32, bufs=3, offset=AT_CENTRE_FLIPPED)
                centre_flipped_of[i] = centre_flipped
                nc.scalar.copy(out=centre_flipped[:], in_=total_of[i][:, 0:CHUNK, :])

        def finish(i):
            s, g, k = items[i]
            result = arena.tile([P, CHUNK, P], F32, bufs=4, offset=AT_RESULT)
            result_of[i] = result
            nc.vector.tensor_tensor(
                out=result[:],
                in0=total_of[i][:, 0:CHUNK, :],
                in1=mean_flipped_of[g][:, channels_of(i), :],
                op=ALU.add,
            )

        def store(i):
            s, g, k = items[i]
            for tile in range(GROUP_TILES):
                m = GROUP_TILES * g + tile
                nc.sync.dma_start(
                    out=out_view[:, channels_of(i), P * m : P * m + P],
                    in_=result_of[i][CAPSULES * tile : CAPSULES * tile + CAPSULES, :, :],
                )

        def flip_centre(i):
            s, g, k = items[i]
            if s == 0 and g == 0:
                centre = banks.tile([P, BANK_SLOTS, LANES], F32, tag="early_centre", bufs=2, offset=3 * BANK)
            else:
                centre = banks.tile([P, BANK_SLOTS, LANES], F32, tag="centre", bufs=2, offset=6 * BANK)
            centre_of[i] = centre
            for c in range(CHUNK):
                if s == 0:
                    flipped = mean_flipped_of[g][:, CHUNK * k + c, :]
                else:
                    flipped = centre_flipped_of[i][:, c, :]
                nc.tensor.transpose(out=centre[:, c, :], in_=flipped, identity=identity[:])

        def keep_mean(i):
            mean_chunk = arena.tile([P, CHUNK, LANES], F32, bufs=3, offset=AT_MEAN_CHUNK)
            mean_chunk_of[i] = mean_chunk
            nc.scalar.copy(out=mean_chunk[:], in_=centre_of[i][:, 0:CHUNK, :])

        def subtract(i):
            difference = arena.tile([P, POSITIONS, CHUNK, LANES], F32, bufs=3, offset=AT_DIFFERENCE)
            difference_of[i] = difference
            target = chunk_priors(i) if items[i][0] == 0 else difference
            n = POSITIONS - gpsimd_subtracts(i)
            nc.vector.tensor_tensor(
                out=target[:, 0:n, :, :],
                in0=chunk_priors(i)[:, 0:n, :, :],
                in1=centre_of[i][:, 0:CHUNK, :].unsqueeze(1).to_broadcast([P, n, CHUNK, LANES]),
                op=ALU.subtract,
            )
            if n < POSITIONS:
                nc.gpsimd.tensor_tensor(
                    out=target[:, n:POSITIONS, :, :],
                    in0=chunk_priors(i)[:, n:POSITIONS, :, :],
                    in1=mean_chunk_of[i][:].unsqueeze(1).to_broadcast([P, POSITIONS - n, CHUNK, LANES]),
                    op=ALU.subtract,
                )

        def square(i, first, last):
            source = chunk_priors(i) if items[i][0] == 0 else difference_of[i]
            n = min(last, POSITIONS - gpsimd_squares(i))
            nc.scalar.activation(
                out=difference_of[i][:, first:n, :, :], in_=source[:, first:n, :, :], func=ACT.Square
            )
            if n < last:
                nc.gpsimd.tensor_tensor(
                    out=difference_of[i][:, n:last, :, :],
                    in0=source[:, n:last, :, :],
                    in1=source[:, n:last, :, :],
                    op=ALU.mult,
                )

        def sum_channels(i, first, last):
            s, g, k = items[i]
            if k == 0 and first == 0:
                distance_0 = banks.tile([P, BANK_SLOTS, P], F32, offset=0)
                distance_1 = banks.tile([P, BANK_SLOTS, P], F32, offset=BANK)
                distance_2 = banks.tile([P, BANK_SLOTS, P], F32, offset=2 * BANK)
                distance_banks[(s, g)] = (distance_0, distance_1, distance_2)
            for t in range(first, last):
                b, slot = divmod(t, BANK_SLOTS)
                last_slot = slot == BANK_SLOTS - 1 or t == POSITIONS - 1
                for c in range(CHUNK):
                    nc.tensor.matmul(
                        out=distance_banks[(s, g)][b][:, slot, :],
                        lhsT=difference_of[i][:, t, c, :],
                        rhs=identity[:],
                        is_transpose=True,
                        start=(k == 0 and slot == 0 and c == 0),
                        stop=(k == CHUNKS - 1 and last_slot and c == CHUNK - 1),
                    )

        def take_pull_bank(s, g):
            pull_bank = banks.tile([P, BANK_SLOTS, LANES], F32, tag="pulls%d" % g, offset=(4 + g) * BANK)
            pull_bank_of[(s, g)] = pull_bank
            return pull_bank

        def pulls(s, g):
            pull_flipped = arena.tile([P, POSITIONS, P], F32, bufs=2, offset=AT_PULL_FLIPPED)
            pull_flipped_of[(s, g)] = pull_flipped
            for b, distance in enumerate(distance_banks[(s - 1, g)]):
                n = min(BANK_SLOTS, POSITIONS - BANK_SLOTS * b)
                nc.scalar.activation(
                    out=pull_flipped[:, BANK_SLOTS * b : BANK_SLOTS * b + n, :],
                    in_=distance[:, 0:n, :],
                    func=ACT.Abs_reciprocal_sqrt,
                    bias=eps[:, 0:1],
                )

        def sum_pulls(s, g):
            pull_flipped = pull_flipped_of[(s, g)]
            add_flipped(take_pull_bank(s, g)[:, 0, :], [pull_flipped[:, t, :] for t in range(POSITIONS)])

        def invert_sum(s, g):
            root = arena.tile([P, LANES], F32, bufs=2, offset=AT_ROOT)
            root_of[(s, g)] = root
            nc.scalar.activation(out=root[:], in_=pull_bank_of[(s, g)][:, 0, :], func=ACT.Abs_reciprocal_sqrt)
            nc.scalar.activation(out=root[:], in_=root[:], func=ACT.Square)

        def flip_scale(s, g):
            nc.tensor.transpose(out=take_pull_bank(s, g)[:, 0, :], in_=root_of[(s, g)][:], identity=identity[:])

        def normalise_pulls(s, g):
            pull_flipped = pull_flipped_of[(s, g)]
            scale = pull_bank_of[(s, g)]
            nc.vector.tensor_tensor(
                out=pull_flipped[:, 0:WEIGHED, :],
                in0=pull_flipped[:, 0:WEIGHED, :],
                in1=scale[:, 0:1, :].to_broadcast([P, WEIGHED, P]),
                op=ALU.mult,
            )
            nc.vector.scalar_tensor_tensor(
                out=pull_flipped[:, WEIGHED, :],
                in0=pull_flipped[:, WEIGHED, :],
                scalar=-1.0,
                in1=scale[:, 0, :],
                op0=ALU.mult,
                op1=ALU.mult,
            )

        def flip_pulls(s, g, first, last, psum_tile):
            pull_flipped = pull_flipped_of[(s, g)]
            for t in range(first, last):
                add_flipped(psum_tile[:, t - first, :], [pull_flipped[:, t, :], pull_flipped[:, WEIGHED, :]])

        def first_pulls(s, g):
            flip_pulls(s, g, 0, FIRST_IN_PSUM, take_pull_bank(s, g))
            pull_sbuf = arena.tile([P, IN_SBUF, LANES], F32, bufs=2, offset=AT_PULL)
            pull_sbuf_of[(s, g)] = pull_sbuf
            nc.scalar.copy(out=pull_sbuf[:, 0:FIRST_IN_PSUM, :], in_=pull_bank_of[(s, g)][:])

        def second_pulls(s, g):
            pull_psum = take_pull_bank(s, g)
            pull_psum_of[(s, g)] = pull_psum
            flip_pulls(s, g, FIRST_IN_PSUM, WEIGHED, pull_psum)
            nc.scalar.copy(
                out=pull_sbuf_of[(s, g)][:, FIRST_IN_PSUM:IN_SBUF, :],
                in_=pull_psum[:, 0 : IN_SBUF - FIRST_IN_PSUM, :],
            )

        def flip_late_pull(g):
            late_pull = banks.tile([P, BANK_SLOTS, LANES], F32, tag="late_pull%d" % g, offset=g * BANK)
            late_pull_of[(PHASES - 1, g)] = late_pull
            flip_pulls(PHASES - 1, g, LAST_SHARE, FIRST_IN_PSUM, late_pull)

        def closing(turn, lag):
            s, g, k = at(turn - lag)
            if 0 <= s < PHASES - 1 and k == CHUNKS - 1:
                return (s + 1, g)
            return None

        last_closing = (PHASES - 1, GROUPS - 1)
        for turn in range(count + 9):
            squared, subtracted, flipped, summed = turn - 4, turn - 3, turn - 2, turn - 1
            late = POSITION_ORDER[turn] if turn < POSITIONS else None
            if at(turn)[0:2] == (0, 1):
                add_pairs(turn)
            if at(turn)[0] >= 1:
                weigh_gpsimd(turn)
            if 0 <= at(flipped)[0] < PHASES - 1:
                flip_centre(flipped)
                if at(flipped)[0] == 0 and gpsimd_subtracts(flipped) > 0:
                    keep_mean(flipped)
            if late is not None:
                for tile in range(GROUP_TILES):
                    multiply(GROUP_TILES + tile, late)
                    if tile < GROUP_TILES // 2:
                        add_bias(GROUP_TILES + tile, late)
            if turn == 0:
                add_to_sum(POSITION_ORDER[-1])
                mean_prior()
            if at(summed)[0:2] == (0, 1) or at(summed)[0] >= 1:
                sum_positions(summed)
            if closing(turn, 6):
                invert_sum(*closing(turn, 6))
                if closing(turn, 6) == last_closing:
                    flip_scale(*last_closing)
            if first_weighed * (PHASES - 1) + 4 < turn <= count:
                idle_bank = banks.tile([P, BANK_SLOTS, P], F32, offset=2 * BANK)
                keep_busy(idle_bank, 1)
            if closing(turn, 6) == last_closing:
                flip_late_pull(0)
            if closing(turn, 8) == last_closing:
                flip_late_pull(1)
            if closing(turn, 8):
                second_pulls(*closing(turn, 8))
            if at(summed)[0:2] == (0, 1) or 1 <= at(summed)[0] < PHASES - 1:
                empty_sum(summed)
            if 0 <= at(subtracted)[0] < PHASES - 1:
                subtract(subtracted)
                square(subtracted, 0, SPLIT)
            if closing(turn, 7):
                normalise_pulls(*closing(turn, 7))
            if late is not None:
                for tile in range(GROUP_TILES // 2, GROUP_TILES):
                    add_bias(GROUP_TILES + tile, late)
            with_distances = 0 <= at(squared)[0] < PHASES - 1
            if with_distances:
                sum_channels(squared, 0, SPLIT)
            if with_distances and closing(turn, 5):
                keep_busy(take_pull_bank(*closing(turn, 5)), CLOSING_PRODUCTS)
            if closing(turn, 6) and closing(turn, 6) != last_closing:
                flip_scale(*closing(turn, 6))
            if closing(turn, 7):
                first_pulls(*closing(turn, 7))
            if with_distances:
                sum_channels(squared, SPLIT, POSITIONS)
            if closing(turn, 4):
                pulls(*closing(turn, 4))
            if 0 <= at(subtracted)[0] < PHASES - 1:
                square(subtracted, SPLIT, POSITIONS)
            if closing(turn, 5):
                sum_pulls(*closing(turn, 5))
            if at(turn)[0] >= 1:
                weigh_vector(turn)
            if at(summed)[0] == PHASES - 1:
                finish(summed)
                store(summed)
